import numpy as np
import ml_dtypes


def mxq(x, axis, fmt="e4m3"):
    dtype, down = {"e4m3": (ml_dtypes.float8_e4m3fn, 7), "e5m2": (ml_dtypes.float8_e5m2, 14)}[fmt]
    v = np.moveaxis(np.asarray(x, np.float32).astype(ml_dtypes.bfloat16).astype(np.float64), axis, -1)
    blocks = v.reshape(v.shape[:-1] + (-1, 32))
    amax = np.abs(blocks).max(-1, keepdims=True)
    byte = np.maximum(np.where(amax > 0, np.frexp(amax)[1] - 1 + 127, 0) - down, 1)
    scale = np.exp2(byte - 127.0)
    codes = (blocks / scale).astype(np.float32).astype(dtype).astype(np.float64)
    return np.moveaxis((codes * scale).reshape(v.shape), -1, axis)


WIDE = False


def mx_kscale(k):
    if not WIDE:
        return np.ones(k)
    levels = np.array([10, -10, 5, -5, 0])
    a = np.random.permutation(np.resize(levels, k // 512 * 4)).reshape(k // 512, 4)
    idx = np.arange(k)
    return np.exp2(a[idx // 512, idx % 128 // 32])


BF16 = ml_dtypes.bfloat16


def bf(x):
    return np.asarray(x, np.float32).astype(BF16)


def f64(x):
    return np.asarray(x).astype(np.float64)


E2M1 = np.array([0.0, 0.5, 1.0, 1.5, 2.0, 3.0, 4.0, 6.0, -0.0, -0.5, -1.0, -1.5, -2.0, -3.0, -4.0, -6.0])


def pack_weight(w, fmt):
    k, n = w.shape
    w = f64(bf(w)).reshape(k // 32, 32, n)
    amax = np.abs(w).max(1)
    if fmt == "e4m3":
        byte = np.frexp(amax)[1] - 1 + 127 - 7
    else:
        mant, ex = np.frexp(amax / 6.0)
        byte = np.where(mant > 0.5, ex, ex - 1) + 127
    byte = np.clip(np.where(amax > 0, byte, 1), 1, 254)
    scaled = (w * np.exp2(127.0 - byte)[:, None, :]).reshape(k, n).astype(np.float32)
    by_word = np.ascontiguousarray(scaled.reshape(k // 512, 128, 4, n).transpose(0, 1, 3, 2))
    if fmt == "e4m3":
        words = by_word.astype(ml_dtypes.float8_e4m3fn).view(np.uint8)
    else:
        c = by_word.astype(ml_dtypes.float4_e2m1fn).view(np.uint8) & 0xF
        words = c[..., 0::2] | (c[..., 1::2] << 4)
    return np.ascontiguousarray(words), np.ascontiguousarray(byte.astype(np.uint8).reshape(k // 512, 16, n))


def unpack_weight(words, scales, fmt):
    g, p, n, _ = words.shape
    if fmt == "e4m3":
        vals = np.ascontiguousarray(words).view(ml_dtypes.float8_e4m3fn).astype(np.float64)
    else:
        nib = np.empty((g, p, n, 4), np.uint8)
        nib[..., 0::2] = words & 0xF
        nib[..., 1::2] = words >> 4
        vals = E2M1[nib]
    vals = vals * np.repeat(np.exp2(scales.astype(np.float64) - 127.0), 8, axis=1)[..., None]
    return vals.transpose(0, 1, 3, 2).reshape(g * 512, n)


B, C, CP, H, W, KW = 1, 512, 19, 48, 48, 7
PAD = KW // 2
BN_EPS = 1e-5
FMT = "e4m3"


def pad_hw(v):
    return np.pad(v, ((0, 0), (0, 0), (PAD, PAD), (PAD, PAD)))


def setup_inputs():
    s, t = mx_kscale(C), mx_kscale(C)
    x = bf(np.random.standard_normal((B, C, H, W)))
    coarse_probs = bf(np.random.random((B, CP, H, W)))
    sigma = bf(1.5 + 0.1 * np.random.standard_normal(1))
    w_feat = np.random.standard_normal((C, C)) * 2.0 / np.sqrt(C) * t[:, None] / s[None, :]
    w_fuse = np.random.standard_normal((C, C)) * 2.5 / np.sqrt(C) / t[None, :]
    w_feat_words, w_feat_scales = pack_weight(np.ascontiguousarray(w_feat.T), FMT)
    w_fuse_words, w_fuse_scales = pack_weight(np.ascontiguousarray(w_fuse.T), FMT)
    return {
        "x": x,
        "coarse_probs": coarse_probs,
        "sigma": sigma,
        "w_feat_words": w_feat_words,
        "w_feat_scales": w_feat_scales,
        "w_fuse_words": w_fuse_words,
        "w_fuse_scales": w_fuse_scales,
        "bn_gamma": bf((1.0 + 0.1 * np.random.standard_normal(C)) * s),
        "bn_beta": bf(0.1 * np.random.standard_normal(C) * s),
        "bn_mean": bf(0.1 * np.random.standard_normal(C)),
        "bn_var": bf(np.random.random(C) + 0.5),
    }


def reference(x, coarse_probs, sigma, w_feat_words, w_feat_scales, w_fuse_words, w_fuse_scales, bn_gamma, bn_beta, bn_mean, bn_var):
    x, p = f64(x), f64(coarse_probs)
    inv = 1.0 / np.sqrt(f64(bn_var) + BN_EPS)
    xn = (x - f64(bn_mean)[None, :, None, None]) * (inv * f64(bn_gamma))[None, :, None, None] + f64(bn_beta)[None, :, None, None]

    pp = pad_hw(p)
    dist_sq = np.stack([((pp[:, :, i:i + H, j:j + W] - p) ** 2).sum(axis=1) for i in range(KW) for j in range(KW)], axis=1)
    denom = 2.0 * np.maximum(f64(sigma)[0], 0.0) ** 2 + 1e-8
    a = np.exp(-dist_sq / denom)
    e = np.exp(a - a.max(axis=1, keepdims=True))
    affinity = e / e.sum(axis=1, keepdims=True)

    xq = mxq(xn, 1, "e4m3")
    messages = (unpack_weight(w_feat_words, w_feat_scales, FMT).T @ xq.reshape(B, C, H * W)).reshape(B, C, H, W)

    mp = pad_hw(messages)
    agg = np.zeros((B, C, H, W))
    for i in range(KW):
        for j in range(KW):
            agg = agg + mp[:, :, i:i + H, j:j + W] * affinity[:, i * KW + j][:, None]

    aq = mxq(agg, 1, "e4m3")
    refined = (unpack_weight(w_fuse_words, w_fuse_scales, FMT).T @ aq.reshape(B, C, H * W)).reshape(B, C, H, W)
    return x + refined

@@ -1,0 +1,473 @@
+from contextlib import ExitStack
+
+import concourse.mybir as mybir
+from concourse.masks import make_identity
+
+F32 = mybir.dt.float32
+BF16 = mybir.dt.bfloat16
+I32 = mybir.dt.int32
+U32 = mybir.dt.uint32
+U8 = mybir.dt.uint8
+FP8X4 = mybir.dt.float8_e4m3fn_x4
+ALU = mybir.AluOpType
+ACT = mybir.ActivationFunctionType
+AXIS = mybir.AxisListType
+
+P = 128
+PACK = 4
+C = 512
+SIDE = 48
+NPX = SIDE * SIDE
+NTILES = NPX // P
+PROBS = 19
+R = 3
+KW = 2 * R + 1
+BN_EPS = 1e-5
+
+ROUNDS = 3
+TILES_PER_ROUND = NTILES // ROUNDS
+THIRD_ROWS = SIDE // ROUNDS
+THIRD_PX = NPX // ROUNDS
+STEPS = ROUNDS * KW
+
+V_TILES = 4
+G_TILES = TILES_PER_ROUND - V_TILES
+
+MARGIN = R * SIDE
+COLS = NPX + 2 * MARGIN
+QUANT_CALLS = ((0, 1024), (1024, 1024), (2048, 512), (2560, 32))
+PLANE_COPIES = 4
+PLANE_STEP = 16
+PLANE_PITCH = 2624
+
+PADDED = SIDE + 2 * R
+ROWS = PROBS + 1
+BANDS = 6
+BAND_ROWS = SIDE // BANDS
+GROUP = 6
+ONE_SIDE = (-3, -2, -1, 1, 2, 3)
+NGROUPS = KW + 1
+ITEMS = [(g, third) for g in [KW] + list(range(KW)) for third in range(ROUNDS)]
+THIRD_RUN = (THIRD_ROWS - 1) * PADDED + SIDE
+LOAD_AHEAD = 7
+SUMS_AHEAD = 6
+EXP_AHEAD = 5
+SHIFTED_BUFS = 3
+
+FINISH_STAGES = 6
+LAST_STEPS = STEPS + TILES_PER_ROUND + FINISH_STAGES - 1
+
+FLOPS = 2 * 2 * C * C * NPX + 2 * KW * KW * C * NPX
+
+
+def group_offsets(g):
+    if g < KW:
+        return [(d, g - R) for d in ONE_SIDE]
+    return [(0, d) for d in ONE_SIDE]
+
+
+def group_and_place(di, dj):
+    if di != 0:
+        return dj + R, ONE_SIDE.index(di)
+    return KW, ONE_SIDE.index(dj)
+
+
+def last_slice_of(call, dj):
+    first_col, n = QUANT_CALLS[call]
+    return min(NTILES - 1, (first_col + n - 1 - (MARGIN - dj)) // P)
+
+
+def tile_entering(step):
+    rnd, place = divmod(step, KW)
+    if 1 <= rnd <= ROUNDS and place < TILES_PER_ROUND:
+        return TILES_PER_ROUND * (rnd - 1) + place
+    return None
+
+
+def tile_dcblock_kernel(
+    tc,
+    x,
+    coarse_probs,
+    sigma,
+    w_feat_words,
+    w_feat_scales,
+    w_fuse_words,
+    w_fuse_scales,
+    bn_gamma,
+    bn_beta,
+    bn_mean,
+    bn_var,
+    out,
+):
+    nc = tc.nc
+    with ExitStack() as ctx:
+        keep = ctx.enter_context(tc.tile_pool(name="keep", bufs=1))
+        work = ctx.enter_context(tc.tile_pool(name="work", bufs=3))
+        psum_v = ctx.enter_context(tc.psum_pool(name="psum_v", bufs=4))
+        psum_s = ctx.enter_context(tc.psum_pool(name="psum_s", bufs=2))
+        psum_one = ctx.enter_context(tc.psum_pool(name="psum_one", bufs=1))
+
+        ident_f32 = keep.tile([P, P], F32, name="ident_f32")
+        make_identity(nc, ident_f32[:])
+        ident_bf16 = keep.tile([P, P], BF16, name="ident_bf16")
+        make_identity(nc, ident_bf16[:])
+        by_offset = ident_f32[:, 0 : GROUP * ROWS].rearrange("p (j c) -> p j c", c=ROWS)
+        selector = keep.tile([P, 2 * GROUP], F32, name="selector")
+        nc.vector.tensor_reduce(out=selector[:, 0:GROUP], in_=by_offset[:, :, 1:ROWS], axis=AXIS.X, op=ALU.add)
+        nc.vector.tensor_copy(out=selector[:, GROUP : 2 * GROUP], in_=by_offset[:, :, 0])
+        minus_one = keep.tile([P, 1], F32, name="minus_one")
+        nc.vector.memset(minus_one[:], -1.0)
+
+        xn = keep.tile([P, PACK, NPX], BF16, name="xn")
+        grouped = keep.tile([P, COLS, PACK], BF16, name="grouped", align_bytes=64)
+        codes = [keep.tile([P, COLS], U32, name="codes%d" % b, align_bytes=64) for b in range(2)]
+        planes = [keep.tile([P, PLANE_COPIES, PLANE_PITCH], U8, name="planes%d" % b, align_bytes=64) for b in range(2)]
+        acc_v = {}
+        acc_g = []
+        for rnd in range(ROUNDS):
+            for place in range(V_TILES):
+                t = TILES_PER_ROUND * rnd + place
+                acc_v[t] = keep.tile([P, C], F32, name="acc_v%d" % t)
+            acc_g.append(keep.tile([P, G_TILES, C], F32, name="acc_g%d" % rnd))
+        shifted = [keep.tile([P, THIRD_ROWS * PADDED], F32, name="shifted%d" % b) for b in range(SHIFTED_BUFS)]
+        centre = keep.tile([P, SIDE * PADDED], F32, name="centre")
+        e_all = keep.tile([P, NTILES, NGROUPS * GROUP], F32, name="e_all")
+        e_inside = [keep.tile([P, NTILES, GROUP], F32, name="e_inside%d" % g) for g in range(NGROUPS)]
+        inv_sum = keep.tile([P, NTILES], F32, name="inv_sum")
+
+        def accumulator(t):
+            rnd, place = divmod(t, TILES_PER_ROUND)
+            if place < V_TILES:
+                return acc_v[t][:]
+            return acc_g[rnd][:, place - V_TILES, :]
+
+        for image in shifted + [centre]:
+            nc.gpsimd.memset(image[:], 0.0)
+
+        with tc.tile_pool(name="early", bufs=1) as first:
+            raw = first.tile([BANDS * ROWS, BAND_ROWS * SIDE], BF16, name="raw")
+            nc.vector.memset(raw[:], 1.0)
+            nc.sync.dma_start(
+                out=raw[BANDS : BANDS * ROWS, :], in_=coarse_probs[0].rearrange("c (band r) w -> (c band) (r w)", band=BANDS)
+            )
+            band_rows = first.tile([BANDS * ROWS, BAND_ROWS, PADDED], F32, name="band_rows")
+            nc.vector.memset(band_rows[:], 0.0)
+            nc.vector.tensor_copy(out=band_rows[:, :, R : R + SIDE], in_=raw[:].rearrange("p (r w) -> p r w", w=SIDE))
+            zero_rows = first.tile([ROWS, R * PADDED], F32, name="zero_rows")
+            nc.vector.memset(zero_rows[:], 0.0)
+
+            sigma_bf = first.tile([P, 1], BF16, name="sigma_bf")
+            nc.scalar.dma_start(out=sigma_bf[:], in_=sigma.partition_broadcast(P))
+            bn_in = {}
+            for label, vec in (("var", bn_var), ("gamma", bn_gamma), ("mean", bn_mean), ("beta", bn_beta)):
+                bn_in[label] = first.tile([P, PACK], BF16, name="bn_" + label)
+                nc.scalar.dma_start(out=bn_in[label][:], in_=vec.rearrange("(p j) -> p j", j=PACK))
+            x_raw = first.tile([P, PACK, NPX], BF16, name="x_raw")
+            x_by_word = x[0].rearrange("(p j) h w -> p j (h w)", j=PACK)
+            for third in range(ROUNDS):
+                px = slice(THIRD_PX * third, THIRD_PX * (third + 1))
+                nc.sync.dma_start(out=x_raw[:, :, px], in_=x_by_word[:, :, px])
+
+            def load_weight(words, scales, label):
+                w_codes = keep.tile([P, C], U32, name=label + "_codes", align_bytes=64)
+                nc.sync.dma_start(out=w_codes[:].bitcast(I32), in_=words[0].rearrange("p n t -> p (n t)").bitcast(I32))
+                w_plane = keep.tile([P, C], U8, name=label + "_plane", align_bytes=64)
+                nc.vector.memset(w_plane[:].bitcast(I32), 0)
+                scale_rows = scales[0].bitcast(I32)
+                for quadrant in range(4):
+                    nc.sync.dma_start(
+                        out=w_plane[32 * quadrant : 32 * quadrant + 4, :].bitcast(I32),
+                        in_=scale_rows[4 * quadrant : 4 * quadrant + 4, :],
+                    )
+                return w_codes, w_plane
+
+            feat_codes, feat_plane = load_weight(w_feat_words, w_feat_scales, "feat")
+
+            parked = out[0].rearrange("(c two) h w -> c (two h w)", two=2)[0:ROWS, 0 : PADDED * PADDED]
+            band_size = BAND_ROWS * PADDED
+            for band in range(BANDS):
+                start = R * PADDED + band_size * band
+                nc.sync.dma_start(
+                    out=parked[:, start : start + band_size],
+                    in_=band_rows[band : BANDS * ROWS : BANDS, :, :].rearrange("p r w -> p (r w)"),
+                )
+            nc.sync.dma_start(out=parked[:, 0 : R * PADDED], in_=zero_rows[:])
+            nc.sync.dma_start(out=parked[:, (R + SIDE) * PADDED : PADDED * PADDED], in_=zero_rows[:])
+
+            whole_run = (SIDE - 1) * PADDED + SIDE
+            for j in range(GROUP):
+                start = R * PADDED + R
+                nc.sync.dma_start(out=centre[ROWS * j : ROWS * (j + 1), 0:whole_run], in_=parked[:, start : start + whole_run])
+
+            neg_inv_denom = keep.tile([P, 1], F32, name="neg_inv_denom")
+            nc.vector.tensor_scalar_max(out=neg_inv_denom[:], in0=sigma_bf[:], scalar1=0.0)
+            nc.vector.tensor_mul(out=neg_inv_denom[:], in0=neg_inv_denom[:], in1=neg_inv_denom[:])
+            nc.vector.tensor_scalar(
+                out=neg_inv_denom[:], in0=neg_inv_denom[:], scalar1=-2.0, scalar2=-1e-8, op0=ALU.mult, op1=ALU.add
+            )
+            nc.vector.reciprocal(out=neg_inv_denom[:], in_=neg_inv_denom[:])
+            bn_scale = keep.tile([P, PACK], F32, name="bn_scale")
+            bn_shift = keep.tile([P, PACK], F32, name="bn_shift")
+            nc.vector.tensor_scalar_add(out=bn_scale[:], in0=bn_in["var"][:], scalar1=BN_EPS)
+            nc.scalar.sqrt(out=bn_scale[:], in_=bn_scale[:])
+            nc.vector.reciprocal(out=bn_scale[:], in_=bn_scale[:])
+            nc.vector.tensor_mul(out=bn_scale[:], in0=bn_scale[:], in1=bn_in["gamma"][:])
+            nc.vector.tensor_mul(out=bn_shift[:], in0=bn_scale[:], in1=bn_in["mean"][:])
+            nc.vector.tensor_sub(out=bn_shift[:], in0=bn_in["beta"][:], in1=bn_shift[:])
+
+            nc.vector.memset(grouped[:, 0 : MARGIN + R + 1, :], 0.0)
+            nc.vector.memset(grouped[:, NPX + MARGIN - R - 1 : COLS, :], 0.0)
+            for b in range(2):
+                nc.vector.memset(planes[b][:, 0, :].bitcast(I32), 0)
+
+            for third in range(ROUNDS):
+                px = slice(THIRD_PX * third, THIRD_PX * (third + 1))
+                for j in range(PACK):
+                    if j % 2 == 0:
+                        nc.scalar.activation(
+                            out=xn[:, j, px], in_=x_raw[:, j, px], func=ACT.Identity,
+                            scale=bn_scale[:, j : j + 1], bias=bn_shift[:, j : j + 1],
+                        )
+                    else:
+                        nc.vector.tensor_scalar(
+                            out=xn[:, j, px], in0=x_raw[:, j, px],
+                            scalar1=bn_scale[:, j : j + 1], scalar2=bn_shift[:, j : j + 1], op0=ALU.mult, op1=ALU.add,
+                        )
+
+        late = ctx.enter_context(tc.tile_pool(name="late", bufs=1))
+        late_work = ctx.enter_context(tc.tile_pool(name="late_work", bufs=3))
+        out_by_tile = out[0].rearrange("(m p) h w -> p m (h w)", p=P)
+
+        sq_diff = {}
+        sums = {}
+
+        def load_item(q):
+            g, third = ITEMS[q]
+            for j, (di, dj) in enumerate(group_offsets(g)):
+                start = (R + di + THIRD_ROWS * third) * PADDED + R + dj
+                nc.sync.dma_start(
+                    out=shifted[q % SHIFTED_BUFS][ROWS * j : ROWS * (j + 1), 0:THIRD_RUN], in_=parked[:, start : start + THIRD_RUN]
+                )
+
+        def subtract_item(engine, q):
+            third = ITEMS[q][1]
+            rows = "p (h w) -> p h w"
+            sq_diff[q] = work.tile([P, THIRD_PX], F32, name="sq_diff")
+            engine.tensor_tensor(
+                out=sq_diff[q][:].rearrange(rows, w=SIDE),
+                in0=shifted[q % SHIFTED_BUFS][:].rearrange(rows, w=PADDED)[:, :, 0:SIDE],
+                in1=centre[:].rearrange(rows, w=PADDED)[:, THIRD_ROWS * third : THIRD_ROWS * (third + 1), 0:SIDE],
+                op=ALU.subtract,
+            )
+
+        def square_item(q):
+            nc.scalar.activation(out=sq_diff[q][:], in_=sq_diff[q][:], func=ACT.Square)
+
+        def sum_item(q):
+            sums[q] = psum_one.tile([P, TILES_PER_ROUND, 2 * GROUP], F32, name="sums", tag="small")
+            for i in range(TILES_PER_ROUND):
+                nc.tensor.matmul(
+                    out=sums[q][:, i, :], lhsT=sq_diff[q][:, P * i : P * (i + 1)], rhs=selector[:], start=True, stop=True
+                )
+
+        def e_of_item(q):
+            g, third = ITEMS[q]
+            tiles = slice(TILES_PER_ROUND * third, TILES_PER_ROUND * (third + 1))
+            return e_all[:, tiles, GROUP * g : GROUP * (g + 1)], e_inside[g][:, tiles, :]
+
+        def exp_item(q):
+            a = work.tile([P, TILES_PER_ROUND, GROUP], F32, name="a")
+            nc.scalar.activation(out=a[:], in_=sums[q][:, :, 0:GROUP], func=ACT.Exp, scale=neg_inv_denom[:, 0:1])
+            nc.scalar.activation(out=e_of_item(q)[0], in_=a[:], func=ACT.Exp, bias=minus_one[:, 0:1])
+
+        def mask_item(q):
+            e_item, e_inside_item = e_of_item(q)
+            nc.vector.scalar_tensor_tensor(
+                out=e_inside_item, in0=sums[q][:, :, GROUP : 2 * GROUP], scalar=0.5, in1=e_item, op0=ALU.is_lt, op1=ALU.mult
+            )
+
+        def regroup(engine_copy, dj, t):
+            first_col = MARGIN - dj + P * t
+            engine_copy(
+                out=grouped[:, first_col : first_col + P, :],
+                in_=xn[:, :, P * t : P * (t + 1)].rearrange("p j w -> p w j"),
+            )
+
+        def quantise(b, call):
+            first_col, n = QUANT_CALLS[call]
+            cols = slice(first_col, first_col + n)
+            nc.vector.quantize_mx(
+                out=codes[b][:, cols].bitcast(FP8X4),
+                scales=planes[b][:, 0, cols],
+                in_=grouped[:, cols, :].rearrange("p w j -> p (w j)"),
+            )
+
+        def move_planes(b):
+            for v in range(1, PLANE_COPIES):
+                nc.vector.tensor_copy(
+                    out=planes[b][:, v, 0 : COLS - PLANE_STEP * v].bitcast(I32),
+                    in_=planes[b][:, 0, PLANE_STEP * v : COLS].bitcast(I32),
+                )
+
+        def messages_of_neighbours(bank, b, t, di):
+            col = P * t + SIDE * (di + R)
+            v = (col // PLANE_STEP) % PLANE_COPIES
+            plane_col = col - PLANE_STEP * v
+            nc.tensor.matmul_mx(
+                out=bank[:],
+                lhsT=codes[b][:, col : col + P].bitcast(FP8X4),
+                lhsT_scale=planes[b][:, v, plane_col : plane_col + P],
+                rhs=feat_codes[:].bitcast(FP8X4),
+                rhs_scale=feat_plane[:],
+                start=True,
+                stop=True,
+            )
+
+        def weight(t, di, dj):
+            if di == 0 and dj == 0:
+                return 1.0
+            g, j = group_and_place(di, dj)
+            return e_inside[g][:, t, j : j + 1]
+
+        def add_on_vector(b, t, di, dj, is_first):
+            bank = psum_v.tile([P, C], F32, name="bank_v")
+            messages_of_neighbours(bank, b, t, di)
+            if is_first:
+                nc.vector.tensor_scalar_mul(out=acc_v[t][:], in0=bank[:], scalar1=weight(t, di, dj))
+            else:
+                nc.vector.scalar_tensor_tensor(
+                    out=acc_v[t][:], in0=bank[:], scalar=weight(t, di, dj), in1=acc_v[t][:], op0=ALU.mult, op1=ALU.add
+                )
+
+        def add_on_gpsimd(b, rnd, di, dj, is_first):
+            products = acc_g[rnd] if is_first else work.tile([P, G_TILES, C], F32, name="products")
+            for i in range(G_TILES):
+                t = TILES_PER_ROUND * rnd + V_TILES + i
+                bank = psum_s.tile([P, C], F32, name="bank_s")
+                messages_of_neighbours(bank, b, t, di)
+                nc.scalar.activation(out=products[:, i, :], in_=bank[:], func=ACT.Copy, scale=weight(t, di, dj))
+            if not is_first:
+                nc.gpsimd.tensor_tensor(out=acc_g[rnd][:], in0=acc_g[rnd][:], in1=products[:], op=ALU.add)
+
+        agg = {}
+        turned = {}
+        agg_grouped = {}
+        agg_mx = {}
+        refined = {}
+
+        def normalise(t):
+            agg[t] = late_work.tile([P, PACK, P], BF16, name="agg")
+            nc.scalar.activation(
+                out=agg[t][:], in_=accumulator(t).rearrange("p (q j) -> p j q", j=PACK), func=ACT.Copy,
+                scale=inv_sum[:, t : t + 1],
+            )
+
+        def turn(t):
+            turned[t] = psum_one.tile([P, PACK, P], BF16, name="turned", tag="small")
+            for j in range(PACK):
+                nc.tensor.transpose(out=turned[t][:, j, :], in_=agg[t][:, j, :], identity=ident_bf16[:])
+
+        def regroup_agg(t):
+            agg_grouped[t] = late_work.tile([P, P, PACK], BF16, name="agg_grouped", align_bytes=64)
+            nc.scalar.copy(out=agg_grouped[t][:], in_=turned[t][:].rearrange("q j m -> q m j"))
+
+        def quantise_agg(t):
+            agg_codes = late_work.tile([P, P], U32, name="agg_codes", align_bytes=64)
+            agg_plane = late_work.tile([P, P], U8, name="agg_plane", align_bytes=64)
+            nc.vector.quantize_mx(
+                out=agg_codes[:].bitcast(FP8X4), scales=agg_plane[:], in_=agg_grouped[t][:].rearrange("q m j -> q (m j)")
+            )
+            agg_mx[t] = (agg_codes, agg_plane)
+
+        def fuse(t):
+            agg_codes, agg_plane = agg_mx[t]
+            refined[t] = psum_one.tile([P, C // P, P], F32, name="refined")
+            for m in range(C // P):
+                nc.tensor.matmul_mx(
+                    out=refined[t][:, m, :],
+                    lhsT=fuse_codes[:, P * m : P * (m + 1)].bitcast(FP8X4),
+                    lhsT_scale=fuse_plane[:, P * m : P * (m + 1)],
+                    rhs=agg_codes[:].bitcast(FP8X4),
+                    rhs_scale=agg_plane[:],
+                    start=True,
+                    stop=True,
+                )
+
+        def add_x_and_store(t):
+            result = late_work.tile([P, C // P, P], F32, name="result")
+            pixels = slice(P * t, P * (t + 1))
+            nc.vector.tensor_tensor(out=result[:], in0=refined[t][:], in1=x_res[:, :, pixels], op=ALU.add)
+            nc.sync.dma_start(out=out_by_tile[:, :, pixels], in_=result[:])
+
+        finish_stages = (normalise, turn, regroup_agg, quantise_agg, fuse, add_x_and_store)
+
+        for t in range(NTILES):
+            regroup(nc.vector.tensor_copy, -R, t)
+        for call in range(len(QUANT_CALLS)):
+            quantise(0, call)
+        move_planes(0)
+        for q in range(SHIFTED_BUFS):
+            load_item(q)
+        for q in range(SUMS_AHEAD):
+            subtract_item(nc.gpsimd if q % 2 == 0 else nc.vector, q)
+            if q + SHIFTED_BUFS < LOAD_AHEAD:
+                load_item(q + SHIFTED_BUFS)
+            square_item(q)
+            sum_item(q)
+            if q < EXP_AHEAD:
+                exp_item(q)
+                mask_item(q)
+
+        with tc.manual_schedule():
+            for phase in range(KW):
+                dj = phase - R
+                b = phase % 2
+                is_last = phase == KW - 1
+                if phase == 1:
+                    fuse_codes, fuse_plane = load_weight(w_fuse_words, w_fuse_scales, "fuse")
+                    x_res = late.tile([P, C // P, NPX], BF16, name="x_res")
+                    nc.sync.dma_start(out=x_res[:], in_=x[0].rearrange("(m p) h w -> p m (h w)", p=P))
+                for step in range(LAST_STEPS if is_last else STEPS):
+                    rnd, k = divmod(step, KW)
+                    n = ROUNDS * phase + rnd
+
+                    if step < STEPS:
+                        if k == 0 and n + LOAD_AHEAD < len(ITEMS):
+                            load_item(n + LOAD_AHEAD)
+                        if k == 0 and n + EXP_AHEAD < len(ITEMS):
+                            exp_item(n + EXP_AHEAD)
+                        if k == 1 and n + SUMS_AHEAD < len(ITEMS):
+                            subtract_item(nc.vector, n + SUMS_AHEAD)
+                        if k == 2 and n + EXP_AHEAD < len(ITEMS):
+                            mask_item(n + EXP_AHEAD)
+                        if k == 3 and n + SUMS_AHEAD < len(ITEMS):
+                            square_item(n + SUMS_AHEAD)
+                        if k == 5 and n + SUMS_AHEAD < len(ITEMS):
+                            sum_item(n + SUMS_AHEAD)
+
+                    if not is_last:
+                        if step < NTILES:
+                            regroup(nc.scalar.copy, dj + 1, step)
+                        for call in range(len(QUANT_CALLS)):
+                            if step == last_slice_of(call, dj + 1) + 2:
+                                quantise(1 - b, call)
+                        if step == STEPS - 1:
+                            move_planes(1 - b)
+
+                    if is_last:
+                        if step < STEPS and k == 4:
+                            tiles = slice(TILES_PER_ROUND * rnd, TILES_PER_ROUND * (rnd + 1))
+                            nc.vector.tensor_reduce(out=inv_sum[:, tiles], in_=e_all[:, tiles, :], axis=AXIS.X, op=ALU.add)
+                            nc.vector.tensor_scalar_add(out=inv_sum[:, tiles], in0=inv_sum[:, tiles], scalar1=1.0)
+                            nc.vector.reciprocal(out=inv_sum[:, tiles], in_=inv_sum[:, tiles])
+                        for stage in reversed(range(FINISH_STAGES)):
+                            t = tile_entering(step - stage) if step >= stage else None
+                            if t is not None:
+                                finish_stages[stage](t)
+
+                    if step < STEPS:
+                        di = k - R
+                        is_first = phase == 0 and k == 0
+                        for place in range(V_TILES):
+                            add_on_vector(b, TILES_PER_ROUND * rnd + place, di, dj, is_first)
+                        add_on_gpsimd(b, rnd, di, dj, is_first)

@@ -30,8 +30,6 @@ THIRD_ROWS = SIDE // ROUNDS
 THIRD_PX = NPX // ROUNDS
 STEPS = ROUNDS * KW
 
-V_TILES = 4
-G_TILES = TILES_PER_ROUND - V_TILES
 
 MARGIN = R * SIDE
 COLS = NPX + 2 * MARGIN
@@ -103,8 +101,7 @@ def tile_dcblock_kernel(
     with ExitStack() as ctx:
         keep = ctx.enter_context(tc.tile_pool(name="keep", bufs=1))
         work = ctx.enter_context(tc.tile_pool(name="work", bufs=3))
-        psum_v = ctx.enter_context(tc.psum_pool(name="psum_v", bufs=4))
-        psum_s = ctx.enter_context(tc.psum_pool(name="psum_s", bufs=2))
+        psum_v = ctx.enter_context(tc.psum_pool(name="psum_v", bufs=6))
         psum_one = ctx.enter_context(tc.psum_pool(name="psum_one", bufs=1))
 
         ident_f32 = keep.tile([P, P], F32, name="ident_f32")
@@ -122,24 +119,12 @@ def tile_dcblock_kernel(
         grouped = keep.tile([P, COLS, PACK], BF16, name="grouped", align_bytes=64)
         codes = [keep.tile([P, COLS], U32, name="codes%d" % b, align_bytes=64) for b in range(2)]
         planes = [keep.tile([P, PLANE_COPIES, PLANE_PITCH], U8, name="planes%d" % b, align_bytes=64) for b in range(2)]
-        acc_v = {}
-        acc_g = []
-        for rnd in range(ROUNDS):
-            for place in range(V_TILES):
-                t = TILES_PER_ROUND * rnd + place
-                acc_v[t] = keep.tile([P, C], F32, name="acc_v%d" % t)
-            acc_g.append(keep.tile([P, G_TILES, C], F32, name="acc_g%d" % rnd))
+        acc_v = [keep.tile([P, C], F32, name="acc_v%d" % t) for t in range(NTILES)]
         shifted = [keep.tile([P, THIRD_ROWS * PADDED], F32, name="shifted%d" % b) for b in range(SHIFTED_BUFS)]
         centre = keep.tile([P, SIDE * PADDED], F32, name="centre")
         e_all = keep.tile([P, NTILES, NGROUPS * GROUP], F32, name="e_all")
         e_inside = [keep.tile([P, NTILES, GROUP], F32, name="e_inside%d" % g) for g in range(NGROUPS)]
         inv_sum = keep.tile([P, NTILES], F32, name="inv_sum")
-
-        def accumulator(t):
-            rnd, place = divmod(t, TILES_PER_ROUND)
-            if place < V_TILES:
-                return acc_v[t][:]
-            return acc_g[rnd][:, place - V_TILES, :]
 
         for image in shifted + [centre]:
             nc.gpsimd.memset(image[:], 0.0)
@@ -339,16 +324,6 @@ def tile_dcblock_kernel(
                     out=acc_v[t][:], in0=bank[:], scalar=weight(t, di, dj), in1=acc_v[t][:], op0=ALU.mult, op1=ALU.add
                 )
 
-        def add_on_gpsimd(b, rnd, di, dj, is_first):
-            products = acc_g[rnd] if is_first else work.tile([P, G_TILES, C], F32, name="products")
-            for i in range(G_TILES):
-                t = TILES_PER_ROUND * rnd + V_TILES + i
-                bank = psum_s.tile([P, C], F32, name="bank_s")
-                messages_of_neighbours(bank, b, t, di)
-                nc.scalar.activation(out=products[:, i, :], in_=bank[:], func=ACT.Copy, scale=weight(t, di, dj))
-            if not is_first:
-                nc.gpsimd.tensor_tensor(out=acc_g[rnd][:], in0=acc_g[rnd][:], in1=products[:], op=ALU.add)
-
         agg = {}
         turned = {}
         agg_grouped = {}
@@ -358,7 +333,7 @@ def tile_dcblock_kernel(
         def normalise(t):
             agg[t] = late_work.tile([P, PACK, P], BF16, name="agg")
             nc.scalar.activation(
-                out=agg[t][:], in_=accumulator(t).rearrange("p (q j) -> p j q", j=PACK), func=ACT.Copy,
+                out=agg[t][:], in_=acc_v[t][:].rearrange("p (q j) -> p j q", j=PACK), func=ACT.Copy,
                 scale=inv_sum[:, t : t + 1],
             )
 
@@ -468,6 +443,5 @@ def tile_dcblock_kernel(
                     if step < STEPS:
                         di = k - R
                         is_first = phase == 0 and k == 0
-                        for place in range(V_TILES):
+                        for place in range(TILES_PER_ROUND):
                             add_on_vector(b, TILES_PER_ROUND * rnd + place, di, dj, is_first)
-                        add_on_gpsimd(b, rnd, di, dj, is_first)

@@ -30,6 +30,8 @@ THIRD_ROWS = SIDE // ROUNDS
 THIRD_PX = NPX // ROUNDS
 STEPS = ROUNDS * KW
 
+V_TILES = 4
+T_TILES = TILES_PER_ROUND - V_TILES
 
 MARGIN = R * SIDE
 COLS = NPX + 2 * MARGIN
@@ -101,7 +103,9 @@ def tile_dcblock_kernel(
     with ExitStack() as ctx:
         keep = ctx.enter_context(tc.tile_pool(name="keep", bufs=1))
         work = ctx.enter_context(tc.tile_pool(name="work", bufs=3))
-        psum_v = ctx.enter_context(tc.psum_pool(name="psum_v", bufs=6))
+        product_pool = ctx.enter_context(tc.tile_pool(name="product_pool", bufs=T_TILES * KW))
+        psum_v = ctx.enter_context(tc.psum_pool(name="psum_v", bufs=3))
+        psum_s = ctx.enter_context(tc.psum_pool(name="psum_s", bufs=2))
         psum_one = ctx.enter_context(tc.psum_pool(name="psum_one", bufs=1))
 
         ident_f32 = keep.tile([P, P], F32, name="ident_f32")
@@ -114,12 +118,20 @@ def tile_dcblock_kernel(
         nc.vector.tensor_copy(out=selector[:, GROUP : 2 * GROUP], in_=by_offset[:, :, 0])
         minus_one = keep.tile([P, 1], F32, name="minus_one")
         nc.vector.memset(minus_one[:], -1.0)
+        ones = keep.tile([P, P], F32, name="ones")
+        nc.vector.memset(ones[:], 1.0)
 
         xn = keep.tile([P, PACK, NPX], BF16, name="xn")
         grouped = keep.tile([P, COLS, PACK], BF16, name="grouped", align_bytes=64)
         codes = [keep.tile([P, COLS], U32, name="codes%d" % b, align_bytes=64) for b in range(2)]
         planes = [keep.tile([P, PLANE_COPIES, PLANE_PITCH], U8, name="planes%d" % b, align_bytes=64) for b in range(2)]
-        acc_v = [keep.tile([P, C], F32, name="acc_v%d" % t) for t in range(NTILES)]
+        acc_v = {}
+        acc_t = {}
+        for t in range(NTILES):
+            if t % TILES_PER_ROUND < V_TILES:
+                acc_v[t] = keep.tile([P, C], F32, name="acc_v%d" % t)
+            else:
+                acc_t[t] = keep.tile([P, PACK, P], F32, name="acc_t%d" % t)
         shifted = [keep.tile([P, THIRD_ROWS * PADDED], F32, name="shifted%d" % b) for b in range(SHIFTED_BUFS)]
         centre = keep.tile([P, SIDE * PADDED], F32, name="centre")
         e_all = keep.tile([P, NTILES, NGROUPS * GROUP], F32, name="e_all")
@@ -324,6 +336,40 @@ def tile_dcblock_kernel(
                     out=acc_v[t][:], in0=bank[:], scalar=weight(t, di, dj), in1=acc_v[t][:], op0=ALU.mult, op1=ALU.add
                 )
 
+        products = {}
+        sum_bank = {}
+
+        def tensor_tile(n, which):
+            return TILES_PER_ROUND * (n % ROUNDS) + V_TILES + which
+
+        def multiply_on_scalar(b, n, m, dj):
+            which, i = divmod(m, KW)
+            t = tensor_tile(n, which)
+            bank = psum_s.tile([P, C], F32, name="bank_s")
+            messages_of_neighbours(bank, b, t, i - R)
+            products[(n, m)] = product_pool.tile([P, PACK, P], F32, name="product")
+            nc.scalar.activation(
+                out=products[(n, m)][:], in_=bank[:].rearrange("p (q j) -> p j q", j=PACK), func=ACT.Copy,
+                scale=weight(t, i - R, dj),
+            )
+
+        def add_on_tensor(n, which, half):
+            if half == 0:
+                sum_bank[(n, which)] = psum_one.tile([P, PACK, P], F32, name="sum_bank")
+            for j in (2 * half, 2 * half + 1):
+                for i in range(KW):
+                    nc.tensor.matmul(
+                        out=sum_bank[(n, which)][:, j, :], lhsT=products[(n, KW * which + i)][:, j, :], rhs=ident_f32[:],
+                        is_transpose=True, start=(i == 0), stop=(i == KW - 1),
+                    )
+
+        def collect(n, which):
+            t = tensor_tile(n, which)
+            if n < ROUNDS:
+                nc.vector.tensor_copy(out=acc_t[t][:], in_=sum_bank[(n, which)][:])
+            else:
+                nc.vector.tensor_tensor(out=acc_t[t][:], in0=sum_bank[(n, which)][:], in1=acc_t[t][:], op=ALU.add)
+
         agg = {}
         turned = {}
         agg_grouped = {}
@@ -331,20 +377,34 @@ def tile_dcblock_kernel(
         refined = {}
 
         def normalise(t):
-            agg[t] = late_work.tile([P, PACK, P], BF16, name="agg")
-            nc.scalar.activation(
-                out=agg[t][:], in_=acc_v[t][:].rearrange("p (q j) -> p j q", j=PACK), func=ACT.Copy,
-                scale=inv_sum[:, t : t + 1],
-            )
+            if t in acc_v:
+                agg[t] = late_work.tile([P, PACK, P], BF16, name="agg")
+                nc.scalar.activation(
+                    out=agg[t][:], in_=acc_v[t][:].rearrange("p (q j) -> p j q", j=PACK), func=ACT.Copy,
+                    scale=inv_sum[:, t : t + 1],
+                )
+            else:
+                agg[t] = late_work.tile([P, P], F32, name="inv_sum_repeated")
+                nc.scalar.activation(out=agg[t][:], in_=ones[:], func=ACT.Copy, scale=inv_sum[:, t : t + 1])
 
         def turn(t):
-            turned[t] = psum_one.tile([P, PACK, P], BF16, name="turned", tag="small")
-            for j in range(PACK):
-                nc.tensor.transpose(out=turned[t][:, j, :], in_=agg[t][:, j, :], identity=ident_bf16[:])
+            if t in acc_v:
+                turned[t] = psum_one.tile([P, PACK, P], BF16, name="turned", tag="small")
+                for j in range(PACK):
+                    nc.tensor.transpose(out=turned[t][:, j, :], in_=agg[t][:, j, :], identity=ident_bf16[:])
+            else:
+                turned[t] = psum_one.tile([P, P], F32, name="inv_sum_spread", tag="small")
+                nc.tensor.transpose(out=turned[t][:], in_=agg[t][:], identity=ident_f32[:])
 
         def regroup_agg(t):
             agg_grouped[t] = late_work.tile([P, P, PACK], BF16, name="agg_grouped", align_bytes=64)
-            nc.scalar.copy(out=agg_grouped[t][:], in_=turned[t][:].rearrange("q j m -> q m j"))
+            if t in acc_v:
+                nc.scalar.copy(out=agg_grouped[t][:], in_=turned[t][:].rearrange("q j m -> q m j"))
+            else:
+                nc.vector.tensor_tensor(
+                    out=agg_grouped[t][:], in0=acc_t[t][:].rearrange("q j m -> q m j"),
+                    in1=turned[t][:].unsqueeze(2).to_broadcast([P, P, PACK]), op=ALU.mult,
+                )
 
         def quantise_agg(t):
             agg_codes = late_work.tile([P, P], U32, name="agg_codes", align_bytes=64)
@@ -409,16 +469,27 @@ def tile_dcblock_kernel(
                     if step < STEPS:
                         if k == 0 and n + LOAD_AHEAD < len(ITEMS):
                             load_item(n + LOAD_AHEAD)
-                        if k == 0 and n + EXP_AHEAD < len(ITEMS):
+                        if k == 1 and n + EXP_AHEAD < len(ITEMS):
                             exp_item(n + EXP_AHEAD)
                         if k == 1 and n + SUMS_AHEAD < len(ITEMS):
-                            subtract_item(nc.vector, n + SUMS_AHEAD)
-                        if k == 2 and n + EXP_AHEAD < len(ITEMS):
+                            subtract_item(nc.gpsimd, n + SUMS_AHEAD)
+                        if k == 3 and n + EXP_AHEAD < len(ITEMS):
                             mask_item(n + EXP_AHEAD)
                         if k == 3 and n + SUMS_AHEAD < len(ITEMS):
                             square_item(n + SUMS_AHEAD)
-                        if k == 5 and n + SUMS_AHEAD < len(ITEMS):
+                        if k == 6 and n + SUMS_AHEAD < len(ITEMS):
                             sum_item(n + SUMS_AHEAD)
+
+                    if n >= 1 and rnd <= ROUNDS:
+                        if k in (1, 2):
+                            add_on_tensor(n - 1, 1, k - 1)
+                        if k == 3:
+                            collect(n - 1, 1)
+                    if step < STEPS:
+                        if k in (4, 5):
+                            add_on_tensor(n, 0, k - 4)
+                        if k == 6:
+                            collect(n, 0)
 
                     if not is_last:
                         if step < NTILES:
@@ -443,5 +514,7 @@ def tile_dcblock_kernel(
                     if step < STEPS:
                         di = k - R
                         is_first = phase == 0 and k == 0
-                        for place in range(TILES_PER_ROUND):
+                        for place in range(V_TILES):
                             add_on_vector(b, TILES_PER_ROUND * rnd + place, di, dj, is_first)
+                        for m in range(T_TILES * k, T_TILES * (k + 1)):
+                            multiply_on_scalar(b, n, m, dj)

@@ -31,7 +31,9 @@ THIRD_PX = NPX // ROUNDS
 STEPS = ROUNDS * KW
 
 V_TILES = 4
-T_TILES = TILES_PER_ROUND - V_TILES
+G_PLACE = 4
+T_PLACE = 5
+PRODUCT_BUFS = KW + 5
 
 MARGIN = R * SIDE
 COLS = NPX + 2 * MARGIN
@@ -103,10 +105,10 @@ def tile_dcblock_kernel(
     with ExitStack() as ctx:
         keep = ctx.enter_context(tc.tile_pool(name="keep", bufs=1))
         work = ctx.enter_context(tc.tile_pool(name="work", bufs=3))
-        product_pool = ctx.enter_context(tc.tile_pool(name="product_pool", bufs=T_TILES * KW))
-        psum_v = ctx.enter_context(tc.psum_pool(name="psum_v", bufs=3))
+        product_pool = ctx.enter_context(tc.tile_pool(name="product_pool", bufs=PRODUCT_BUFS))
+        psum_turns = ctx.enter_context(tc.psum_pool(name="psum_turns", bufs=5))
         psum_s = ctx.enter_context(tc.psum_pool(name="psum_s", bufs=2))
-        psum_one = ctx.enter_context(tc.psum_pool(name="psum_one", bufs=1))
+        psum_sum = ctx.enter_context(tc.psum_pool(name="psum_sum", bufs=1))
 
         ident_f32 = keep.tile([P, P], F32, name="ident_f32")
         make_identity(nc, ident_f32[:])
@@ -125,13 +127,13 @@ def tile_dcblock_kernel(
         grouped = keep.tile([P, COLS, PACK], BF16, name="grouped", align_bytes=64)
         codes = [keep.tile([P, COLS], U32, name="codes%d" % b, align_bytes=64) for b in range(2)]
         planes = [keep.tile([P, PLANE_COPIES, PLANE_PITCH], U8, name="planes%d" % b, align_bytes=64) for b in range(2)]
-        acc_v = {}
+        acc = {}
         acc_t = {}
         for t in range(NTILES):
-            if t % TILES_PER_ROUND < V_TILES:
-                acc_v[t] = keep.tile([P, C], F32, name="acc_v%d" % t)
-            else:
+            if t % TILES_PER_ROUND == T_PLACE:
                 acc_t[t] = keep.tile([P, PACK, P], F32, name="acc_t%d" % t)
+            else:
+                acc[t] = keep.tile([P, C], F32, name="acc%d" % t)
         shifted = [keep.tile([P, THIRD_ROWS * PADDED], F32, name="shifted%d" % b) for b in range(SHIFTED_BUFS)]
         centre = keep.tile([P, SIDE * PADDED], F32, name="centre")
         e_all = keep.tile([P, NTILES, NGROUPS * GROUP], F32, name="e_all")
@@ -237,6 +239,7 @@ def tile_dcblock_kernel(
 
         sq_diff = {}
         sums = {}
+        outside = {}
 
         def load_item(q):
             g, third = ITEMS[q]
@@ -261,7 +264,7 @@ def tile_dcblock_kernel(
             nc.scalar.activation(out=sq_diff[q][:], in_=sq_diff[q][:], func=ACT.Square)
 
         def sum_item(q):
-            sums[q] = psum_one.tile([P, TILES_PER_ROUND, 2 * GROUP], F32, name="sums", tag="small")
+            sums[q] = psum_turns.tile([P, TILES_PER_ROUND, 2 * GROUP], F32, name="sums", tag="bank")
             for i in range(TILES_PER_ROUND):
                 nc.tensor.matmul(
                     out=sums[q][:, i, :], lhsT=sq_diff[q][:, P * i : P * (i + 1)], rhs=selector[:], start=True, stop=True
@@ -276,11 +279,13 @@ def tile_dcblock_kernel(
             a = work.tile([P, TILES_PER_ROUND, GROUP], F32, name="a")
             nc.scalar.activation(out=a[:], in_=sums[q][:, :, 0:GROUP], func=ACT.Exp, scale=neg_inv_denom[:, 0:1])
             nc.scalar.activation(out=e_of_item(q)[0], in_=a[:], func=ACT.Exp, bias=minus_one[:, 0:1])
+            outside[q] = work.tile([P, TILES_PER_ROUND, GROUP], F32, name="outside")
+            nc.scalar.copy(out=outside[q][:], in_=sums[q][:, :, GROUP : 2 * GROUP])
 
         def mask_item(q):
             e_item, e_inside_item = e_of_item(q)
             nc.vector.scalar_tensor_tensor(
-                out=e_inside_item, in0=sums[q][:, :, GROUP : 2 * GROUP], scalar=0.5, in1=e_item, op0=ALU.is_lt, op1=ALU.mult
+                out=e_inside_item, in0=outside[q][:], scalar=0.5, in1=e_item, op0=ALU.is_lt, op1=ALU.mult
             )
 
         def regroup(engine_copy, dj, t):
@@ -327,48 +332,52 @@ def tile_dcblock_kernel(
             return e_inside[g][:, t, j : j + 1]
 
         def add_on_vector(b, t, di, dj, is_first):
-            bank = psum_v.tile([P, C], F32, name="bank_v")
+            bank = psum_turns.tile([P, C], F32, name="bank_v", tag="bank")
             messages_of_neighbours(bank, b, t, di)
             if is_first:
-                nc.vector.tensor_scalar_mul(out=acc_v[t][:], in0=bank[:], scalar1=weight(t, di, dj))
+                nc.vector.tensor_scalar_mul(out=acc[t][:], in0=bank[:], scalar1=weight(t, di, dj))
             else:
                 nc.vector.scalar_tensor_tensor(
-                    out=acc_v[t][:], in0=bank[:], scalar=weight(t, di, dj), in1=acc_v[t][:], op0=ALU.mult, op1=ALU.add
+                    out=acc[t][:], in0=bank[:], scalar=weight(t, di, dj), in1=acc[t][:], op0=ALU.mult, op1=ALU.add
                 )
 
         products = {}
         sum_bank = {}
 
-        def tensor_tile(n, which):
-            return TILES_PER_ROUND * (n % ROUNDS) + V_TILES + which
-
-        def multiply_on_scalar(b, n, m, dj):
-            which, i = divmod(m, KW)
-            t = tensor_tile(n, which)
+        def add_on_gpsimd(b, t, di, dj, is_first):
             bank = psum_s.tile([P, C], F32, name="bank_s")
-            messages_of_neighbours(bank, b, t, i - R)
-            products[(n, m)] = product_pool.tile([P, PACK, P], F32, name="product")
+            messages_of_neighbours(bank, b, t, di)
+            if is_first:
+                nc.scalar.activation(out=acc[t][:], in_=bank[:], func=ACT.Copy, scale=weight(t, di, dj))
+            else:
+                product = work.tile([P, C], F32, name="product_g")
+                nc.scalar.activation(out=product[:], in_=bank[:], func=ACT.Copy, scale=weight(t, di, dj))
+                nc.gpsimd.tensor_tensor(out=acc[t][:], in0=acc[t][:], in1=product[:], op=ALU.add)
+
+        def multiply_for_tensor(b, n, t, di, dj):
+            bank = psum_s.tile([P, C], F32, name="bank_s")
+            messages_of_neighbours(bank, b, t, di)
+            products[(n, di)] = product_pool.tile([P, PACK, P], F32, name="product_t")
             nc.scalar.activation(
-                out=products[(n, m)][:], in_=bank[:].rearrange("p (q j) -> p j q", j=PACK), func=ACT.Copy,
-                scale=weight(t, i - R, dj),
+                out=products[(n, di)][:], in_=bank[:].rearrange("p (q j) -> p j q", j=PACK), func=ACT.Copy,
+                scale=weight(t, di, dj),
             )
 
-        def add_on_tensor(n, which, half):
-            if half == 0:
-                sum_bank[(n, which)] = psum_one.tile([P, PACK, P], F32, name="sum_bank")
-            for j in (2 * half, 2 * half + 1):
-                for i in range(KW):
-                    nc.tensor.matmul(
-                        out=sum_bank[(n, which)][:, j, :], lhsT=products[(n, KW * which + i)][:, j, :], rhs=ident_f32[:],
-                        is_transpose=True, start=(i == 0), stop=(i == KW - 1),
-                    )
+        def add_on_tensor(n, j):
+            if j == 0:
+                sum_bank[n] = psum_sum.tile([P, PACK, P], F32, name="sum_bank")
+            for di in range(-R, R + 1):
+                nc.tensor.matmul(
+                    out=sum_bank[n][:, j, :], lhsT=products[(n, di)][:, j, :], rhs=ident_f32[:],
+                    is_transpose=True, start=(di == -R), stop=(di == R),
+                )
 
-        def collect(n, which):
-            t = tensor_tile(n, which)
+        def collect(n):
+            t = TILES_PER_ROUND * (n % ROUNDS) + T_PLACE
             if n < ROUNDS:
-                nc.vector.tensor_copy(out=acc_t[t][:], in_=sum_bank[(n, which)][:])
+                nc.vector.tensor_copy(out=acc_t[t][:], in_=sum_bank[n][:])
             else:
-                nc.vector.tensor_tensor(out=acc_t[t][:], in0=sum_bank[(n, which)][:], in1=acc_t[t][:], op=ALU.add)
+                nc.vector.tensor_tensor(out=acc_t[t][:], in0=sum_bank[n][:], in1=acc_t[t][:], op=ALU.add)
 
         agg = {}
         turned = {}
@@ -377,10 +386,10 @@ def tile_dcblock_kernel(
         refined = {}
 
         def normalise(t):
-            if t in acc_v:
+            if t in acc:
                 agg[t] = late_work.tile([P, PACK, P], BF16, name="agg")
                 nc.scalar.activation(
-                    out=agg[t][:], in_=acc_v[t][:].rearrange("p (q j) -> p j q", j=PACK), func=ACT.Copy,
+                    out=agg[t][:], in_=acc[t][:].rearrange("p (q j) -> p j q", j=PACK), func=ACT.Copy,
                     scale=inv_sum[:, t : t + 1],
                 )
             else:
@@ -388,17 +397,17 @@ def tile_dcblock_kernel(
                 nc.scalar.activation(out=agg[t][:], in_=ones[:], func=ACT.Copy, scale=inv_sum[:, t : t + 1])
 
         def turn(t):
-            if t in acc_v:
-                turned[t] = psum_one.tile([P, PACK, P], BF16, name="turned", tag="small")
+            if t in acc:
+                turned[t] = psum_turns.tile([P, PACK, P], BF16, name="turned", tag="bank")
                 for j in range(PACK):
                     nc.tensor.transpose(out=turned[t][:, j, :], in_=agg[t][:, j, :], identity=ident_bf16[:])
             else:
-                turned[t] = psum_one.tile([P, P], F32, name="inv_sum_spread", tag="small")
+                turned[t] = psum_turns.tile([P, P], F32, name="inv_sum_spread", tag="bank")
                 nc.tensor.transpose(out=turned[t][:], in_=agg[t][:], identity=ident_f32[:])
 
         def regroup_agg(t):
             agg_grouped[t] = late_work.tile([P, P, PACK], BF16, name="agg_grouped", align_bytes=64)
-            if t in acc_v:
+            if t in acc:
                 nc.scalar.copy(out=agg_grouped[t][:], in_=turned[t][:].rearrange("q j m -> q m j"))
             else:
                 nc.vector.tensor_tensor(
@@ -416,7 +425,7 @@ def tile_dcblock_kernel(
 
         def fuse(t):
             agg_codes, agg_plane = agg_mx[t]
-            refined[t] = psum_one.tile([P, C // P, P], F32, name="refined")
+            refined[t] = psum_turns.tile([P, C // P, P], F32, name="refined", tag="bank")
             for m in range(C // P):
                 nc.tensor.matmul_mx(
                     out=refined[t][:, m, :],
@@ -433,8 +442,6 @@ def tile_dcblock_kernel(
             pixels = slice(P * t, P * (t + 1))
             nc.vector.tensor_tensor(out=result[:], in0=refined[t][:], in1=x_res[:, :, pixels], op=ALU.add)
             nc.sync.dma_start(out=out_by_tile[:, :, pixels], in_=result[:])
-
-        finish_stages = (normalise, turn, regroup_agg, quantise_agg, fuse, add_x_and_store)
 
         for t in range(NTILES):
             regroup(nc.vector.tensor_copy, -R, t)
@@ -465,31 +472,22 @@ def tile_dcblock_kernel(
                 for step in range(LAST_STEPS if is_last else STEPS):
                     rnd, k = divmod(step, KW)
                     n = ROUNDS * phase + rnd
+                    adding = step < STEPS
+                    sums_left = n >= 1 and rnd <= ROUNDS
 
-                    if step < STEPS:
-                        if k == 0 and n + LOAD_AHEAD < len(ITEMS):
-                            load_item(n + LOAD_AHEAD)
-                        if k == 1 and n + EXP_AHEAD < len(ITEMS):
-                            exp_item(n + EXP_AHEAD)
-                        if k == 1 and n + SUMS_AHEAD < len(ITEMS):
-                            subtract_item(nc.gpsimd, n + SUMS_AHEAD)
-                        if k == 3 and n + EXP_AHEAD < len(ITEMS):
-                            mask_item(n + EXP_AHEAD)
-                        if k == 3 and n + SUMS_AHEAD < len(ITEMS):
-                            square_item(n + SUMS_AHEAD)
-                        if k == 6 and n + SUMS_AHEAD < len(ITEMS):
-                            sum_item(n + SUMS_AHEAD)
+                    if adding and k == 0 and n + LOAD_AHEAD < len(ITEMS):
+                        load_item(n + LOAD_AHEAD)
+                    if adding and k == 1 and n + EXP_AHEAD < len(ITEMS):
+                        exp_item(n + EXP_AHEAD)
+                    if adding and k == 1 and n + SUMS_AHEAD < len(ITEMS):
+                        subtract_item(nc.gpsimd, n + SUMS_AHEAD)
+                    if adding and k == 3 and n + EXP_AHEAD < len(ITEMS):
+                        mask_item(n + EXP_AHEAD)
+                    if adding and k == 3 and n + SUMS_AHEAD < len(ITEMS):
+                        square_item(n + SUMS_AHEAD)
 
-                    if n >= 1 and rnd <= ROUNDS:
-                        if k in (1, 2):
-                            add_on_tensor(n - 1, 1, k - 1)
-                        if k == 3:
-                            collect(n - 1, 1)
-                    if step < STEPS:
-                        if k in (4, 5):
-                            add_on_tensor(n, 0, k - 4)
-                        if k == 6:
-                            collect(n, 0)
+                    if sums_left and k == 6:
+                        collect(n - 1)
 
                     if not is_last:
                         if step < NTILES:
@@ -500,21 +498,30 @@ def tile_dcblock_kernel(
                         if step == STEPS - 1:
                             move_planes(1 - b)
 
+                    if is_last and adding and k == 4:
+                        tiles = slice(TILES_PER_ROUND * rnd, TILES_PER_ROUND * (rnd + 1))
+                        nc.vector.tensor_reduce(out=inv_sum[:, tiles], in_=e_all[:, tiles, :], axis=AXIS.X, op=ALU.add)
+                        nc.vector.tensor_scalar_add(out=inv_sum[:, tiles], in0=inv_sum[:, tiles], scalar1=1.0)
+                        nc.vector.reciprocal(out=inv_sum[:, tiles], in_=inv_sum[:, tiles])
                     if is_last:
-                        if step < STEPS and k == 4:
-                            tiles = slice(TILES_PER_ROUND * rnd, TILES_PER_ROUND * (rnd + 1))
-                            nc.vector.tensor_reduce(out=inv_sum[:, tiles], in_=e_all[:, tiles, :], axis=AXIS.X, op=ALU.add)
-                            nc.vector.tensor_scalar_add(out=inv_sum[:, tiles], in0=inv_sum[:, tiles], scalar1=1.0)
-                            nc.vector.reciprocal(out=inv_sum[:, tiles], in_=inv_sum[:, tiles])
-                        for stage in reversed(range(FINISH_STAGES)):
-                            t = tile_entering(step - stage) if step >= stage else None
-                            if t is not None:
-                                finish_stages[stage](t)
+                        for steps_ago, stage in ((5, add_x_and_store), (3, quantise_agg), (2, regroup_agg), (0, normalise)):
+                            if tile_entering(step - steps_ago) is not None:
+                                stage(tile_entering(step - steps_ago))
 
-                    if step < STEPS:
+                    if adding:
                         di = k - R
                         is_first = phase == 0 and k == 0
+                        first_tile = TILES_PER_ROUND * rnd
                         for place in range(V_TILES):
-                            add_on_vector(b, TILES_PER_ROUND * rnd + place, di, dj, is_first)
-                        for m in range(T_TILES * k, T_TILES * (k + 1)):
-                            multiply_on_scalar(b, n, m, dj)
+                            add_on_vector(b, first_tile + place, di, dj, is_first)
+                        add_on_gpsimd(b, first_tile + G_PLACE, di, dj, is_first)
+                        multiply_for_tensor(b, n, first_tile + T_PLACE, di, dj)
+
+                    if sums_left and 1 <= k <= PACK:
+                        add_on_tensor(n - 1, k - 1)
+                    if adding and k == 6 and n + SUMS_AHEAD < len(ITEMS):
+                        sum_item(n + SUMS_AHEAD)
+                    if is_last:
+                        for steps_ago, stage in ((4, fuse), (1, turn)):
+                            if tile_entering(step - steps_ago) is not None:
+                                stage(tile_entering(step - steps_ago))

@@ -375,9 +375,11 @@ def tile_dcblock_kernel(
         def collect(n):
             t = TILES_PER_ROUND * (n % ROUNDS) + T_PLACE
             if n < ROUNDS:
-                nc.vector.tensor_copy(out=acc_t[t][:], in_=sum_bank[n][:])
+                nc.scalar.copy(out=acc_t[t][:], in_=sum_bank[n][:])
             else:
-                nc.vector.tensor_tensor(out=acc_t[t][:], in0=sum_bank[n][:], in1=acc_t[t][:], op=ALU.add)
+                round_sum = work.tile([P, PACK, P], F32, name="round_sum")
+                nc.scalar.copy(out=round_sum[:], in_=sum_bank[n][:])
+                nc.gpsimd.tensor_tensor(out=acc_t[t][:], in0=acc_t[t][:], in1=round_sum[:], op=ALU.add)
 
         agg = {}
         turned = {}

@@ -34,6 +34,7 @@ V_TILES = 4
 G_PLACE = 4
 T_PLACE = 5
 PRODUCT_BUFS = KW + 5
+GPSIMD_BUFS = 6
 
 MARGIN = R * SIDE
 COLS = NPX + 2 * MARGIN
@@ -106,6 +107,7 @@ def tile_dcblock_kernel(
         keep = ctx.enter_context(tc.tile_pool(name="keep", bufs=1))
         work = ctx.enter_context(tc.tile_pool(name="work", bufs=3))
         product_pool = ctx.enter_context(tc.tile_pool(name="product_pool", bufs=PRODUCT_BUFS))
+        gpsimd_pool = ctx.enter_context(tc.tile_pool(name="gpsimd_pool", bufs=GPSIMD_BUFS))
         psum_turns = ctx.enter_context(tc.psum_pool(name="psum_turns", bufs=5))
         psum_s = ctx.enter_context(tc.psum_pool(name="psum_s", bufs=2))
         psum_sum = ctx.enter_context(tc.psum_pool(name="psum_sum", bufs=1))
@@ -291,8 +293,8 @@ def tile_dcblock_kernel(
         def regroup(engine_copy, dj, t):
             first_col = MARGIN - dj + P * t
             engine_copy(
-                out=grouped[:, first_col : first_col + P, :],
-                in_=xn[:, :, P * t : P * (t + 1)].rearrange("p j w -> p w j"),
+                out=grouped[:, first_col : first_col + P, :].rearrange("p (w i) j -> p w j i", i=4),
+                in_=xn[:, :, P * t : P * (t + 1)].rearrange("p j (w i) -> p w j i", i=4),
             )
 
         def quantise(b, call):
@@ -350,7 +352,7 @@ def tile_dcblock_kernel(
             if is_first:
                 nc.scalar.activation(out=acc[t][:], in_=bank[:], func=ACT.Copy, scale=weight(t, di, dj))
             else:
-                product = work.tile([P, C], F32, name="product_g")
+                product = gpsimd_pool.tile([P, C], F32, name="product_g")
                 nc.scalar.activation(out=product[:], in_=bank[:], func=ACT.Copy, scale=weight(t, di, dj))
                 nc.gpsimd.tensor_tensor(out=acc[t][:], in0=acc[t][:], in1=product[:], op=ALU.add)
 
@@ -375,11 +377,9 @@ def tile_dcblock_kernel(
         def collect(n):
             t = TILES_PER_ROUND * (n % ROUNDS) + T_PLACE
             if n < ROUNDS:
-                nc.scalar.copy(out=acc_t[t][:], in_=sum_bank[n][:])
+                nc.vector.tensor_copy(out=acc_t[t][:], in_=sum_bank[n][:])
             else:
-                round_sum = work.tile([P, PACK, P], F32, name="round_sum")
-                nc.scalar.copy(out=round_sum[:], in_=sum_bank[n][:])
-                nc.gpsimd.tensor_tensor(out=acc_t[t][:], in0=acc_t[t][:], in1=round_sum[:], op=ALU.add)
+                nc.vector.tensor_tensor(out=acc_t[t][:], in0=sum_bank[n][:], in1=acc_t[t][:], op=ALU.add)
 
         agg = {}
         turned = {}
@@ -453,7 +453,7 @@ def tile_dcblock_kernel(
         for q in range(SHIFTED_BUFS):
             load_item(q)
         for q in range(SUMS_AHEAD):
-            subtract_item(nc.gpsimd if q % 2 == 0 else nc.vector, q)
+            subtract_item(nc.gpsimd, q)
             if q + SHIFTED_BUFS < LOAD_AHEAD:
                 load_item(q + SHIFTED_BUFS)
             square_item(q)

@@ -18,47 +18,50 @@ PACK = 4
 C = 512
 SIDE = 48
 NPX = SIDE * SIDE
-NTILES = NPX // P
 PROBS = 19
 R = 3
 KW = 2 * R + 1
 BN_EPS = 1e-5
 
-ROUNDS = 3
-TILES_PER_ROUND = NTILES // ROUNDS
-THIRD_ROWS = SIDE // ROUNDS
-THIRD_PX = NPX // ROUNDS
-STEPS = ROUNDS * KW
+THIRD_ROWS = SIDE // 3
+THIRD_PX = THIRD_ROWS * SIDE
+TILES = THIRD_PX // P
+STEPS = KW * KW
 
-V_TILES = 4
-G_PLACE = 4
-T_PLACE = 5
-PRODUCT_BUFS = KW + 5
-GPSIMD_BUFS = 6
+PITCH = SIDE + 2 * R
+WORDS = 2944
+QUANT_CALLS = ((0, 1024), (1024, 1024), (2048, 512), (2560, 256), (2816, 128))
+CHUNK_ROWS = 8
 
-MARGIN = R * SIDE
-COLS = NPX + 2 * MARGIN
-QUANT_CALLS = ((0, 1024), (1024, 1024), (2048, 512), (2560, 32))
+MID_ROWS = THIRD_ROWS + 2 * R
+MID_COLS = MID_ROWS * SIDE
 PLANE_COPIES = 4
 PLANE_STEP = 16
-PLANE_PITCH = 2624
+PLANE_PITCH = 1088
 
-PADDED = SIDE + 2 * R
-ROWS = PROBS + 1
-BANDS = 6
-BAND_ROWS = SIDE // BANDS
+B_ROWS, B_COLS = 4, 6
+B_PX = B_ROWS * B_COLS
+Q_ROWS, Q_COLS = B_ROWS + 2 * R, B_COLS + 2 * R
+Q_PX = Q_ROWS * Q_COLS
+STRIPS = 2 * THIRD_ROWS // B_ROWS
+B_PER_STRIP = SIDE // B_COLS
+BLOCKS = STRIPS * B_PER_STRIP
+HALF_ROWS = B_ROWS // 2
+CLASSES = HALF_ROWS * B_COLS
+
 GROUP = 6
+OFFSET_ROWS = PROBS + 1
+ROWS_USED = GROUP * OFFSET_ROWS
+PAD_LEFT = 4
+PAD_PITCH = PAD_LEFT + SIDE + 4
+PAD_ROWS = SIDE + 2 * R
+RUN = (SIDE - 1) * PAD_PITCH + SIDE
 ONE_SIDE = (-3, -2, -1, 1, 2, 3)
-NGROUPS = KW + 1
-ITEMS = [(g, third) for g in [KW] + list(range(KW)) for third in range(ROUNDS)]
-THIRD_RUN = (THIRD_ROWS - 1) * PADDED + SIDE
-LOAD_AHEAD = 7
-SUMS_AHEAD = 6
-EXP_AHEAD = 5
-SHIFTED_BUFS = 3
+GROUPS = [KW] + list(range(KW))
+EARLY_GROUPS = 4
+SHIFTED_BUFS = 4
 
-FINISH_STAGES = 6
-LAST_STEPS = STEPS + TILES_PER_ROUND + FINISH_STAGES - 1
+V_TILES = 4
 
 FLOPS = 2 * 2 * C * C * NPX + 2 * KW * KW * C * NPX
 
@@ -73,18 +76,6 @@ def group_and_place(di, dj):
     if di != 0:
         return dj + R, ONE_SIDE.index(di)
     return KW, ONE_SIDE.index(dj)
-
-
-def last_slice_of(call, dj):
-    first_col, n = QUANT_CALLS[call]
-    return min(NTILES - 1, (first_col + n - 1 - (MARGIN - dj)) // P)
-
-
-def tile_entering(step):
-    rnd, place = divmod(step, KW)
-    if 1 <= rnd <= ROUNDS and place < TILES_PER_ROUND:
-        return TILES_PER_ROUND * (rnd - 1) + place
-    return None
 
 
 def tile_dcblock_kernel(
@@ -105,57 +96,44 @@ def tile_dcblock_kernel(
     nc = tc.nc
     with ExitStack() as ctx:
         keep = ctx.enter_context(tc.tile_pool(name="keep", bufs=1))
-        work = ctx.enter_context(tc.tile_pool(name="work", bufs=3))
-        product_pool = ctx.enter_context(tc.tile_pool(name="product_pool", bufs=PRODUCT_BUFS))
-        gpsimd_pool = ctx.enter_context(tc.tile_pool(name="gpsimd_pool", bufs=GPSIMD_BUFS))
-        psum_turns = ctx.enter_context(tc.psum_pool(name="psum_turns", bufs=5))
+        work = ctx.enter_context(tc.tile_pool(name="work", bufs=2))
+        psum_turns = ctx.enter_context(tc.psum_pool(name="psum_turns", bufs=4))
         psum_s = ctx.enter_context(tc.psum_pool(name="psum_s", bufs=2))
-        psum_sum = ctx.enter_context(tc.psum_pool(name="psum_sum", bufs=1))
+        psum_main = ctx.enter_context(tc.psum_pool(name="psum_main", bufs=2))
 
         ident_f32 = keep.tile([P, P], F32, name="ident_f32")
         make_identity(nc, ident_f32[:])
         ident_bf16 = keep.tile([P, P], BF16, name="ident_bf16")
         make_identity(nc, ident_bf16[:])
-        by_offset = ident_f32[:, 0 : GROUP * ROWS].rearrange("p (j c) -> p j c", c=ROWS)
-        selector = keep.tile([P, 2 * GROUP], F32, name="selector")
-        nc.vector.tensor_reduce(out=selector[:, 0:GROUP], in_=by_offset[:, :, 1:ROWS], axis=AXIS.X, op=ALU.add)
-        nc.vector.tensor_copy(out=selector[:, GROUP : 2 * GROUP], in_=by_offset[:, :, 0])
+        selector = keep.tile([P, GROUP], F32, name="selector")
+        by_offset = ident_f32[:, 0:ROWS_USED].rearrange("p (j c) -> p j c", c=OFFSET_ROWS)
+        nc.vector.tensor_reduce(out=selector[:], in_=by_offset[:, :, 0:PROBS], axis=AXIS.X, op=ALU.add)
         minus_one = keep.tile([P, 1], F32, name="minus_one")
         nc.vector.memset(minus_one[:], -1.0)
-        ones = keep.tile([P, P], F32, name="ones")
-        nc.vector.memset(ones[:], 1.0)
 
-        xn = keep.tile([P, PACK, NPX], BF16, name="xn")
-        grouped = keep.tile([P, COLS, PACK], BF16, name="grouped", align_bytes=64)
-        codes = [keep.tile([P, COLS], U32, name="codes%d" % b, align_bytes=64) for b in range(2)]
+        codes_img = keep.tile([P, WORDS], U32, name="codes_img", align_bytes=64)
+        plane_img = keep.tile([P, WORDS], U8, name="plane_img", align_bytes=64)
+        codes = [keep.tile([P, MID_COLS], U32, name="codes%d" % b, align_bytes=64) for b in range(2)]
         planes = [keep.tile([P, PLANE_COPIES, PLANE_PITCH], U8, name="planes%d" % b, align_bytes=64) for b in range(2)]
-        acc = {}
-        acc_t = {}
-        for t in range(NTILES):
-            if t % TILES_PER_ROUND == T_PLACE:
-                acc_t[t] = keep.tile([P, PACK, P], F32, name="acc_t%d" % t)
-            else:
-                acc[t] = keep.tile([P, C], F32, name="acc%d" % t)
-        shifted = [keep.tile([P, THIRD_ROWS * PADDED], F32, name="shifted%d" % b) for b in range(SHIFTED_BUFS)]
-        centre = keep.tile([P, SIDE * PADDED], F32, name="centre")
-        e_all = keep.tile([P, NTILES, NGROUPS * GROUP], F32, name="e_all")
-        e_inside = [keep.tile([P, NTILES, GROUP], F32, name="e_inside%d" % g) for g in range(NGROUPS)]
-        inv_sum = keep.tile([P, NTILES], F32, name="inv_sum")
+        q_codes = [keep.tile([P, B_PER_STRIP, P], U32, name="q_codes%d" % b, align_bytes=64) for b in range(2)]
+        q_plane = [keep.tile([P, B_PER_STRIP, P], U8, name="q_plane%d" % b, align_bytes=64) for b in range(2)]
+        acc = [keep.tile([P, C], F32, name="acc%d" % t) for t in range(TILES)]
+        shifted = [keep.tile([P, SIDE * PAD_PITCH], BF16, name="shifted%d" % b) for b in range(SHIFTED_BUFS)]
+        centre = keep.tile([P, SIDE * PAD_PITCH], BF16, name="centre")
+        e_mid = keep.tile([P, TILES, (KW + 1) * GROUP], F32, name="e_mid")
+        inv_sum = keep.tile([P, TILES], F32, name="inv_sum")
+        e_out = keep.tile([P, CLASSES, KW, KW], F32, name="e_out")
+        out_sum = keep.tile([P, CLASSES], F32, name="out_sum")
 
-        for image in shifted + [centre]:
-            nc.gpsimd.memset(image[:], 0.0)
+        nc.vector.memset(e_out[:, :, R, R], 1.0)
 
         with tc.tile_pool(name="early", bufs=1) as first:
-            raw = first.tile([BANDS * ROWS, BAND_ROWS * SIDE], BF16, name="raw")
-            nc.vector.memset(raw[:], 1.0)
-            nc.sync.dma_start(
-                out=raw[BANDS : BANDS * ROWS, :], in_=coarse_probs[0].rearrange("c (band r) w -> (c band) (r w)", band=BANDS)
-            )
-            band_rows = first.tile([BANDS * ROWS, BAND_ROWS, PADDED], F32, name="band_rows")
-            nc.vector.memset(band_rows[:], 0.0)
-            nc.vector.tensor_copy(out=band_rows[:, :, R : R + SIDE], in_=raw[:].rearrange("p (r w) -> p r w", w=SIDE))
-            zero_rows = first.tile([ROWS, R * PADDED], F32, name="zero_rows")
-            nc.vector.memset(zero_rows[:], 0.0)
+            padded = first.tile([OFFSET_ROWS, PAD_ROWS, PAD_PITCH], BF16, name="padded")
+            nc.vector.memset(padded[:], 0.0)
+            for channels in (slice(0, 16), slice(16, PROBS)):
+                nc.sync.dma_start(
+                    out=padded[channels, R : R + SIDE, PAD_LEFT : PAD_LEFT + SIDE], in_=coarse_probs[0, channels]
+                )
 
             sigma_bf = first.tile([P, 1], BF16, name="sigma_bf")
             nc.scalar.dma_start(out=sigma_bf[:], in_=sigma.partition_broadcast(P))
@@ -164,10 +142,23 @@ def tile_dcblock_kernel(
                 bn_in[label] = first.tile([P, PACK], BF16, name="bn_" + label)
                 nc.scalar.dma_start(out=bn_in[label][:], in_=vec.rearrange("(p j) -> p j", j=PACK))
             x_raw = first.tile([P, PACK, NPX], BF16, name="x_raw")
+            xn = first.tile([P, PACK, NPX], BF16, name="xn")
+            grouped = first.tile([P, WORDS, PACK], BF16, name="grouped", align_bytes=64)
             x_by_word = x[0].rearrange("(p j) h w -> p j (h w)", j=PACK)
-            for third in range(ROUNDS):
+            for third in range(3):
                 px = slice(THIRD_PX * third, THIRD_PX * (third + 1))
                 nc.sync.dma_start(out=x_raw[:, :, px], in_=x_by_word[:, :, px])
+
+            parked = out[0].rearrange("c h w -> c (h w)").bitcast(BF16)[0:OFFSET_ROWS, 0 : PAD_ROWS * PAD_PITCH]
+            nc.sync.dma_start(out=parked, in_=padded[:].rearrange("c h w -> c (h w)"))
+
+            def load_shifted(tile, j, di, dj):
+                start = (R + di) * PAD_PITCH + PAD_LEFT + dj
+                nc.sync.dma_start(out=tile[OFFSET_ROWS * j : OFFSET_ROWS * (j + 1), 0:RUN], in_=parked[:, start : start + RUN])
+
+            def load_group(i):
+                for j, (di, dj) in enumerate(group_offsets(GROUPS[i])):
+                    load_shifted(shifted[i % SHIFTED_BUFS], j, di, dj)
 
             def load_weight(words, scales, label):
                 w_codes = keep.tile([P, C], U32, name=label + "_codes", align_bytes=64)
@@ -182,23 +173,17 @@ def tile_dcblock_kernel(
                     )
                 return w_codes, w_plane
 
-            feat_codes, feat_plane = load_weight(w_feat_words, w_feat_scales, "feat")
+            def fill_unused(tile):
+                nc.sync.dma_start(out=tile[ROWS_USED:P, 0:RUN], in_=parked[0 : P - ROWS_USED, 0:RUN])
 
-            parked = out[0].rearrange("(c two) h w -> c (two h w)", two=2)[0:ROWS, 0 : PADDED * PADDED]
-            band_size = BAND_ROWS * PADDED
-            for band in range(BANDS):
-                start = R * PADDED + band_size * band
-                nc.sync.dma_start(
-                    out=parked[:, start : start + band_size],
-                    in_=band_rows[band : BANDS * ROWS : BANDS, :, :].rearrange("p r w -> p (r w)"),
-                )
-            nc.sync.dma_start(out=parked[:, 0 : R * PADDED], in_=zero_rows[:])
-            nc.sync.dma_start(out=parked[:, (R + SIDE) * PADDED : PADDED * PADDED], in_=zero_rows[:])
-
-            whole_run = (SIDE - 1) * PADDED + SIDE
             for j in range(GROUP):
-                start = R * PADDED + R
-                nc.sync.dma_start(out=centre[ROWS * j : ROWS * (j + 1), 0:whole_run], in_=parked[:, start : start + whole_run])
+                load_shifted(centre, j, 0, 0)
+            fill_unused(centre)
+            for i in range(EARLY_GROUPS):
+                fill_unused(shifted[i])
+                load_group(i)
+                if i == 1:
+                    feat_codes, feat_plane = load_weight(w_feat_words, w_feat_scales, "feat")
 
             neg_inv_denom = keep.tile([P, 1], F32, name="neg_inv_denom")
             nc.vector.tensor_scalar_max(out=neg_inv_denom[:], in0=sigma_bf[:], scalar1=0.0)
@@ -216,12 +201,17 @@ def tile_dcblock_kernel(
             nc.vector.tensor_mul(out=bn_shift[:], in0=bn_scale[:], in1=bn_in["mean"][:])
             nc.vector.tensor_sub(out=bn_shift[:], in0=bn_in["beta"][:], in1=bn_shift[:])
 
-            nc.vector.memset(grouped[:, 0 : MARGIN + R + 1, :], 0.0)
-            nc.vector.memset(grouped[:, NPX + MARGIN - R - 1 : COLS, :], 0.0)
+            top = R * PITCH + R
+            nc.vector.memset(grouped[:, 0:top, :], 0.0)
+            nc.vector.memset(grouped[:, (R + SIDE) * PITCH - R : WORDS, :], 0.0)
+            between = grouped[:, top + SIDE : top + SIDE + (SIDE - 1) * PITCH, :].rearrange("p (r w) j -> p r w j", w=PITCH)
+            nc.vector.memset(between[:, :, 0 : 2 * R, :], 0.0)
+            nc.vector.memset(plane_img[:].bitcast(I32), 0)
             for b in range(2):
-                nc.vector.memset(planes[b][:, 0, :].bitcast(I32), 0)
+                nc.vector.memset(q_codes[b][:, :, Q_PX:P], 0)
+                nc.vector.memset(q_plane[b][:].bitcast(I32), 0)
 
-            for third in range(ROUNDS):
+            for third in range(3):
                 px = slice(THIRD_PX * third, THIRD_PX * (third + 1))
                 for j in range(PACK):
                     if j % 2 == 0:
@@ -234,84 +224,192 @@ def tile_dcblock_kernel(
                             out=xn[:, j, px], in0=x_raw[:, j, px],
                             scalar1=bn_scale[:, j : j + 1], scalar2=bn_shift[:, j : j + 1], op0=ALU.mult, op1=ALU.add,
                         )
+            image = grouped[:, top : top + SIDE * PITCH, :].rearrange("p (r w) j -> p r w j", w=PITCH)
+            for chunk in range(SIDE // CHUNK_ROWS):
+                rows = slice(CHUNK_ROWS * chunk, CHUNK_ROWS * (chunk + 1))
+                engine_copy = nc.scalar.copy if chunk in (0, 5) else nc.vector.tensor_copy
+                engine_copy(
+                    out=image[:, rows, 0:SIDE, :],
+                    in_=xn[:, :, SIDE * rows.start : SIDE * rows.stop].rearrange("p j (r w) -> p r w j", w=SIDE),
+                )
+            for first_word, n in QUANT_CALLS:
+                words = slice(first_word, first_word + n)
+                nc.vector.quantize_mx(
+                    out=codes_img[:, words].bitcast(FP8X4), scales=plane_img[:, words],
+                    in_=grouped[:, words, :].rearrange("p w j -> p (w j)"),
+                )
+
+            diff = {}
+            square = {}
+            sums = {}
+
+            def subtract(engine, i):
+                diff[i] = work.tile([P, NPX], F32, name="diff")
+                thirds = "p (t h w) -> p t h w"
+                a = shifted[i % SHIFTED_BUFS][:].rearrange(thirds, t=3, w=PAD_PITCH)[:, :, :, 0:SIDE]
+                c = centre[:].rearrange(thirds, t=3, w=PAD_PITCH)[:, :, :, 0:SIDE]
+                for place, third in ((0, 1), (1, 0), (2, 2)):
+                    engine.tensor_tensor(
+                        out=diff[i][:, THIRD_PX * place : THIRD_PX * (place + 1)].rearrange("p (h w) -> p h w", w=SIDE),
+                        in0=a[:, third], in1=c[:, third], op=ALU.subtract,
+                    )
+
+            def square_diff(i):
+                square[i] = work.tile([P, NPX], F32, name="square")
+                nc.scalar.activation(out=square[i][:, 0:THIRD_PX], in_=diff[i][:, 0:THIRD_PX], func=ACT.Square)
+                by_class = square[i][:, THIRD_PX:NPX].rearrange("p (i j m) -> p i j m", i=HALF_ROWS, j=B_COLS)
+                source = diff[i][:, THIRD_PX:NPX].rearrange(
+                    "p (b h i c j) -> p h i j b c", b=STRIPS, h=2, i=HALF_ROWS, j=B_COLS
+                )
+                for h in range(2):
+                    for half_row in range(HALF_ROWS):
+                        nc.scalar.activation(
+                            out=by_class[:, half_row, :, 64 * h : 64 * (h + 1)].rearrange("p j (b c) -> p j b c", b=STRIPS),
+                            in_=source[:, h, half_row], func=ACT.Square,
+                        )
+
+            def sum_channels(i):
+                sums[i] = psum_turns.tile([P, NPX // P, GROUP], F32, name="sums", tag="bank")
+                for m in range(NPX // P):
+                    nc.tensor.matmul(
+                        out=sums[i][:, m, :], lhsT=square[i][:, P * m : P * (m + 1)], rhs=selector[:], start=True, stop=True
+                    )
+
+            def exps(i):
+                g = GROUPS[i]
+                a = work.tile([P, NPX // P, GROUP], F32, name="a")
+                nc.scalar.activation(out=a[:], in_=sums[i][:], func=ACT.Exp, scale=neg_inv_denom[:, 0:1])
+                nc.scalar.activation(
+                    out=e_mid[:, :, GROUP * g : GROUP * (g + 1)], in_=a[:, 0:TILES, :], func=ACT.Exp, bias=minus_one[:, 0:1]
+                )
+                if g < KW:
+                    places = e_out[:, :, :, g]
+                else:
+                    places = e_out[:, :, R, :]
+                for side in range(2):
+                    nc.scalar.activation(
+                        out=places[:, :, (R + 1) * side : (R + 1) * side + R],
+                        in_=a[:, TILES : NPX // P, R * side : R * (side + 1)], func=ACT.Exp, bias=minus_one[:, 0:1],
+                    )
+
+            for i in range(EARLY_GROUPS):
+                subtract(nc.gpsimd, i)
+                if i + SHIFTED_BUFS < len(GROUPS):
+                    load_group(i + SHIFTED_BUFS)
+                square_diff(i)
+                sum_channels(i)
+                exps(i)
+
+            def move_codes(dj, b):
+                row0 = THIRD_ROWS * PITCH
+                rows = slice(row0, row0 + MID_ROWS * PITCH)
+                cols = slice(R + dj, R + dj + SIDE)
+                nc.vector.tensor_copy(
+                    out=codes[b][:].bitcast(I32).rearrange("p (r w) -> p r w", w=SIDE),
+                    in_=codes_img[:, rows].bitcast(I32).rearrange("p (r w) -> p r w", w=PITCH)[:, :, cols],
+                )
+                nc.vector.tensor_copy(
+                    out=planes[b][:, 0, 0:MID_COLS].rearrange("p (r w) -> p r w", w=SIDE),
+                    in_=plane_img[:, rows].rearrange("p (r w) -> p r w", w=PITCH)[:, :, cols],
+                )
+
+            def move_planes(b):
+                for v in range(1, PLANE_COPIES):
+                    nc.vector.tensor_copy(
+                        out=planes[b][:, v, 0 : MID_COLS - PLANE_STEP * v].bitcast(I32),
+                        in_=planes[b][:, 0, PLANE_STEP * v : MID_COLS].bitcast(I32),
+                    )
+
+            move_codes(-R, 0)
+            move_planes(0)
 
         late = ctx.enter_context(tc.tile_pool(name="late", bufs=1))
         late_work = ctx.enter_context(tc.tile_pool(name="late_work", bufs=3))
+        product_pool = ctx.enter_context(tc.tile_pool(name="product_pool", bufs=6))
+        message_pool = ctx.enter_context(tc.tile_pool(name="message_pool", bufs=4))
         out_by_tile = out[0].rearrange("(m p) h w -> p m (h w)", p=P)
+        spread = late.tile([P, CLASSES, P], F32, name="spread")
+        weights = late.tile([P, BLOCKS, B_PX], F32, name="weights")
+        agg_out = late.tile([P, 2, THIRD_PX, PACK], BF16, name="agg_out", align_bytes=64)
 
-        sq_diff = {}
-        sums = {}
-        outside = {}
+        def strip_row(strip):
+            return (strip // 4) * 2 * THIRD_ROWS + (strip % 4) * B_ROWS
 
-        def load_item(q):
-            g, third = ITEMS[q]
-            for j, (di, dj) in enumerate(group_offsets(g)):
-                start = (R + di + THIRD_ROWS * third) * PADDED + R + dj
-                nc.sync.dma_start(
-                    out=shifted[q % SHIFTED_BUFS][ROWS * j : ROWS * (j + 1), 0:THIRD_RUN], in_=parked[:, start : start + THIRD_RUN]
+        def gather_strip(strip):
+            b = strip % 2
+            start = strip_row(strip) * PITCH
+            rows = slice(start, start + Q_ROWS * PITCH)
+            for half in range(2):
+                cols = slice(B_COLS * half, B_COLS * half + SIDE)
+                for dst, source, dtype in ((q_codes[b], codes_img, I32), (q_plane[b], plane_img, U8)):
+                    nc.vector.tensor_copy(
+                        out=dst[:, :, 0:Q_PX].bitcast(dtype).rearrange("p b (r c) -> p b r c", c=Q_COLS)[
+                            :, :, :, B_COLS * half : B_COLS * (half + 1)
+                        ],
+                        in_=source[:, rows].bitcast(dtype).rearrange("p (r w) -> p r w", w=PITCH)[:, :, cols].rearrange(
+                            "p r (b c) -> p b r c", c=B_COLS
+                        ),
+                    )
+
+        def softmax_out():
+            nc.vector.tensor_reduce(
+                out=out_sum[:], in_=e_out[:].rearrange("p k a b -> p k (a b)"), axis=AXIS.X, op=ALU.add
+            )
+            nc.vector.reciprocal(out=out_sum[:], in_=out_sum[:])
+
+        def spread_out(h, half_row):
+            half = slice(64 * h, 64 * (h + 1))
+            ks = slice(B_COLS * half_row, B_COLS * (half_row + 1))
+            row = 2 * h + half_row
+            for j in range(B_COLS):
+                k = B_COLS * half_row + j
+                nc.vector.tensor_scalar_mul(
+                    out=spread[half, k, 0:Q_PX].rearrange("p (r c) -> p r c", c=Q_COLS)[:, row : row + KW, j : j + KW],
+                    in0=e_out[half, k], scalar1=out_sum[half, k : k + 1],
                 )
 
-        def subtract_item(engine, q):
-            third = ITEMS[q][1]
-            rows = "p (h w) -> p h w"
-            sq_diff[q] = work.tile([P, THIRD_PX], F32, name="sq_diff")
-            engine.tensor_tensor(
-                out=sq_diff[q][:].rearrange(rows, w=SIDE),
-                in0=shifted[q % SHIFTED_BUFS][:].rearrange(rows, w=PADDED)[:, :, 0:SIDE],
-                in1=centre[:].rearrange(rows, w=PADDED)[:, THIRD_ROWS * third : THIRD_ROWS * (third + 1), 0:SIDE],
-                op=ALU.subtract,
+        def turn_out(bank_no):
+            bank = psum_turns.tile([P, 4, P], F32, name="spread_turned", tag="bank")
+            for m in range(4):
+                nc.tensor.transpose(out=bank[:, m, :], in_=spread[:, 4 * bank_no + m, :], identity=ident_f32[:])
+            nc.scalar.copy(
+                out=weights[:].rearrange("q b (h k) -> q b h k", h=2)[:, :, :, 4 * bank_no : 4 * bank_no + 4],
+                in_=bank[:].rearrange("q m (h b) -> q b h m", h=2),
             )
 
-        def square_item(q):
-            nc.scalar.activation(out=sq_diff[q][:], in_=sq_diff[q][:], func=ACT.Square)
+        messages = {}
+        main_bank = {}
 
-        def sum_item(q):
-            sums[q] = psum_turns.tile([P, TILES_PER_ROUND, 2 * GROUP], F32, name="sums", tag="bank")
-            for i in range(TILES_PER_ROUND):
+        def make_messages(n):
+            bank = psum_s.tile([P, C], F32, name="bank_s")
+            strip, place = divmod(n, B_PER_STRIP)
+            nc.tensor.matmul_mx(
+                out=bank[:],
+                lhsT=q_codes[strip % 2][:, place, :].bitcast(FP8X4), lhsT_scale=q_plane[strip % 2][:, place, :],
+                rhs=feat_codes[:].bitcast(FP8X4), rhs_scale=feat_plane[:], start=True, stop=True,
+            )
+            messages[n] = message_pool.tile([P, PACK, P], F32, name="messages")
+            nc.scalar.copy(out=messages[n][:], in_=bank[:].rearrange("p (q j) -> p j q", j=PACK))
+
+        def aggregate(n):
+            if n % 4 == 0:
+                main_bank[n // 4] = psum_main.tile([P, PACK, B_ROWS, 4 * B_COLS], F32, name="main_bank")
+            bank = main_bank[n // 4]
+            cols = slice(B_COLS * (n % 4), B_COLS * (n % 4 + 1))
+            for j in range(PACK):
                 nc.tensor.matmul(
-                    out=sums[q][:, i, :], lhsT=sq_diff[q][:, P * i : P * (i + 1)], rhs=selector[:], start=True, stop=True
+                    out=bank[:, j, :, cols], lhsT=messages[n][:, j, :], rhs=weights[:, n, :].rearrange("q (i j) -> q i j", j=B_COLS),
+                    start=True, stop=True,
                 )
 
-        def e_of_item(q):
-            g, third = ITEMS[q]
-            tiles = slice(TILES_PER_ROUND * third, TILES_PER_ROUND * (third + 1))
-            return e_all[:, tiles, GROUP * g : GROUP * (g + 1)], e_inside[g][:, tiles, :]
-
-        def exp_item(q):
-            a = work.tile([P, TILES_PER_ROUND, GROUP], F32, name="a")
-            nc.scalar.activation(out=a[:], in_=sums[q][:, :, 0:GROUP], func=ACT.Exp, scale=neg_inv_denom[:, 0:1])
-            nc.scalar.activation(out=e_of_item(q)[0], in_=a[:], func=ACT.Exp, bias=minus_one[:, 0:1])
-            outside[q] = work.tile([P, TILES_PER_ROUND, GROUP], F32, name="outside")
-            nc.scalar.copy(out=outside[q][:], in_=sums[q][:, :, GROUP : 2 * GROUP])
-
-        def mask_item(q):
-            e_item, e_inside_item = e_of_item(q)
-            nc.vector.scalar_tensor_tensor(
-                out=e_inside_item, in0=outside[q][:], scalar=0.5, in1=e_item, op0=ALU.is_lt, op1=ALU.mult
+        def collect_quad(m):
+            strip, half = divmod(m, 2)
+            rows = slice(B_ROWS * (strip % 4), B_ROWS * (strip % 4 + 1))
+            cols = slice(24 * half, 24 * (half + 1))
+            nc.scalar.copy(
+                out=agg_out[:, strip // 4].rearrange("p (r w) j -> p r w j", w=SIDE)[:, rows, cols, :],
+                in_=main_bank[m][:].rearrange("p j r w -> p r w j"),
             )
-
-        def regroup(engine_copy, dj, t):
-            first_col = MARGIN - dj + P * t
-            engine_copy(
-                out=grouped[:, first_col : first_col + P, :].rearrange("p (w i) j -> p w j i", i=4),
-                in_=xn[:, :, P * t : P * (t + 1)].rearrange("p j (w i) -> p w j i", i=4),
-            )
-
-        def quantise(b, call):
-            first_col, n = QUANT_CALLS[call]
-            cols = slice(first_col, first_col + n)
-            nc.vector.quantize_mx(
-                out=codes[b][:, cols].bitcast(FP8X4),
-                scales=planes[b][:, 0, cols],
-                in_=grouped[:, cols, :].rearrange("p w j -> p (w j)"),
-            )
-
-        def move_planes(b):
-            for v in range(1, PLANE_COPIES):
-                nc.vector.tensor_copy(
-                    out=planes[b][:, v, 0 : COLS - PLANE_STEP * v].bitcast(I32),
-                    in_=planes[b][:, 0, PLANE_STEP * v : COLS].bitcast(I32),
-                )
 
         def messages_of_neighbours(bank, b, t, di):
             col = P * t + SIDE * (di + R)
@@ -319,19 +417,15 @@ def tile_dcblock_kernel(
             plane_col = col - PLANE_STEP * v
             nc.tensor.matmul_mx(
                 out=bank[:],
-                lhsT=codes[b][:, col : col + P].bitcast(FP8X4),
-                lhsT_scale=planes[b][:, v, plane_col : plane_col + P],
-                rhs=feat_codes[:].bitcast(FP8X4),
-                rhs_scale=feat_plane[:],
-                start=True,
-                stop=True,
+                lhsT=codes[b][:, col : col + P].bitcast(FP8X4), lhsT_scale=planes[b][:, v, plane_col : plane_col + P],
+                rhs=feat_codes[:].bitcast(FP8X4), rhs_scale=feat_plane[:], start=True, stop=True,
             )
 
         def weight(t, di, dj):
             if di == 0 and dj == 0:
                 return 1.0
             g, j = group_and_place(di, dj)
-            return e_inside[g][:, t, j : j + 1]
+            return e_mid[:, t, GROUP * g + j : GROUP * g + j + 1]
 
         def add_on_vector(b, t, di, dj, is_first):
             bank = psum_turns.tile([P, C], F32, name="bank_v", tag="bank")
@@ -343,85 +437,48 @@ def tile_dcblock_kernel(
                     out=acc[t][:], in0=bank[:], scalar=weight(t, di, dj), in1=acc[t][:], op0=ALU.mult, op1=ALU.add
                 )
 
-        products = {}
-        sum_bank = {}
-
         def add_on_gpsimd(b, t, di, dj, is_first):
             bank = psum_s.tile([P, C], F32, name="bank_s")
             messages_of_neighbours(bank, b, t, di)
             if is_first:
                 nc.scalar.activation(out=acc[t][:], in_=bank[:], func=ACT.Copy, scale=weight(t, di, dj))
             else:
-                product = gpsimd_pool.tile([P, C], F32, name="product_g")
+                product = product_pool.tile([P, C], F32, name="product")
                 nc.scalar.activation(out=product[:], in_=bank[:], func=ACT.Copy, scale=weight(t, di, dj))
                 nc.gpsimd.tensor_tensor(out=acc[t][:], in0=acc[t][:], in1=product[:], op=ALU.add)
 
-        def multiply_for_tensor(b, n, t, di, dj):
-            bank = psum_s.tile([P, C], F32, name="bank_s")
-            messages_of_neighbours(bank, b, t, di)
-            products[(n, di)] = product_pool.tile([P, PACK, P], F32, name="product_t")
-            nc.scalar.activation(
-                out=products[(n, di)][:], in_=bank[:].rearrange("p (q j) -> p j q", j=PACK), func=ACT.Copy,
-                scale=weight(t, di, dj),
-            )
-
-        def add_on_tensor(n, j):
-            if j == 0:
-                sum_bank[n] = psum_sum.tile([P, PACK, P], F32, name="sum_bank")
-            for di in range(-R, R + 1):
-                nc.tensor.matmul(
-                    out=sum_bank[n][:, j, :], lhsT=products[(n, di)][:, j, :], rhs=ident_f32[:],
-                    is_transpose=True, start=(di == -R), stop=(di == R),
-                )
-
-        def collect(n):
-            t = TILES_PER_ROUND * (n % ROUNDS) + T_PLACE
-            if n < ROUNDS:
-                nc.vector.tensor_copy(out=acc_t[t][:], in_=sum_bank[n][:])
-            else:
-                nc.vector.tensor_tensor(out=acc_t[t][:], in0=sum_bank[n][:], in1=acc_t[t][:], op=ALU.add)
-
         agg = {}
         turned = {}
-        agg_grouped = {}
+        grouped_agg = {}
         agg_mx = {}
         refined = {}
 
         def normalise(t):
-            if t in acc:
-                agg[t] = late_work.tile([P, PACK, P], BF16, name="agg")
-                nc.scalar.activation(
-                    out=agg[t][:], in_=acc[t][:].rearrange("p (q j) -> p j q", j=PACK), func=ACT.Copy,
-                    scale=inv_sum[:, t : t + 1],
-                )
-            else:
-                agg[t] = late_work.tile([P, P], F32, name="inv_sum_repeated")
-                nc.scalar.activation(out=agg[t][:], in_=ones[:], func=ACT.Copy, scale=inv_sum[:, t : t + 1])
+            agg[t] = late_work.tile([P, PACK, P], BF16, name="agg")
+            nc.scalar.activation(
+                out=agg[t][:], in_=acc[t][:].rearrange("p (q j) -> p j q", j=PACK), func=ACT.Copy, scale=inv_sum[:, t : t + 1]
+            )
 
         def turn(t):
-            if t in acc:
-                turned[t] = psum_turns.tile([P, PACK, P], BF16, name="turned", tag="bank")
-                for j in range(PACK):
-                    nc.tensor.transpose(out=turned[t][:, j, :], in_=agg[t][:, j, :], identity=ident_bf16[:])
-            else:
-                turned[t] = psum_turns.tile([P, P], F32, name="inv_sum_spread", tag="bank")
-                nc.tensor.transpose(out=turned[t][:], in_=agg[t][:], identity=ident_f32[:])
+            turned[t] = psum_turns.tile([P, PACK, P], BF16, name="turned", tag="bank")
+            for j in range(PACK):
+                nc.tensor.transpose(out=turned[t][:, j, :], in_=agg[t][:, j, :], identity=ident_bf16[:])
 
         def regroup_agg(t):
-            agg_grouped[t] = late_work.tile([P, P, PACK], BF16, name="agg_grouped", align_bytes=64)
-            if t in acc:
-                nc.scalar.copy(out=agg_grouped[t][:], in_=turned[t][:].rearrange("q j m -> q m j"))
-            else:
-                nc.vector.tensor_tensor(
-                    out=agg_grouped[t][:], in0=acc_t[t][:].rearrange("q j m -> q m j"),
-                    in1=turned[t][:].unsqueeze(2).to_broadcast([P, P, PACK]), op=ALU.mult,
-                )
+            tile = late_work.tile([P, P, PACK], BF16, name="agg_grouped", align_bytes=64)
+            nc.scalar.copy(out=tile[:], in_=turned[t][:].rearrange("q j m -> q m j"))
+            grouped_agg[TILES + t] = tile[:]
 
         def quantise_agg(t):
             agg_codes = late_work.tile([P, P], U32, name="agg_codes", align_bytes=64)
             agg_plane = late_work.tile([P, P], U8, name="agg_plane", align_bytes=64)
+            if TILES <= t < 2 * TILES:
+                source = grouped_agg[t]
+            else:
+                m = t % TILES
+                source = agg_out[:, t // (2 * TILES), P * m : P * (m + 1), :]
             nc.vector.quantize_mx(
-                out=agg_codes[:].bitcast(FP8X4), scales=agg_plane[:], in_=agg_grouped[t][:].rearrange("q m j -> q (m j)")
+                out=agg_codes[:].bitcast(FP8X4), scales=agg_plane[:], in_=source.rearrange("q m j -> q (m j)")
             )
             agg_mx[t] = (agg_codes, agg_plane)
 
@@ -431,12 +488,8 @@ def tile_dcblock_kernel(
             for m in range(C // P):
                 nc.tensor.matmul_mx(
                     out=refined[t][:, m, :],
-                    lhsT=fuse_codes[:, P * m : P * (m + 1)].bitcast(FP8X4),
-                    lhsT_scale=fuse_plane[:, P * m : P * (m + 1)],
-                    rhs=agg_codes[:].bitcast(FP8X4),
-                    rhs_scale=agg_plane[:],
-                    start=True,
-                    stop=True,
+                    lhsT=fuse_codes[:, P * m : P * (m + 1)].bitcast(FP8X4), lhsT_scale=fuse_plane[:, P * m : P * (m + 1)],
+                    rhs=agg_codes[:].bitcast(FP8X4), rhs_scale=agg_plane[:], start=True, stop=True,
                 )
 
         def add_x_and_store(t):
@@ -445,85 +498,103 @@ def tile_dcblock_kernel(
             nc.vector.tensor_tensor(out=result[:], in0=refined[t][:], in1=x_res[:, :, pixels], op=ALU.add)
             nc.sync.dma_start(out=out_by_tile[:, :, pixels], in_=result[:])
 
-        for t in range(NTILES):
-            regroup(nc.vector.tensor_copy, -R, t)
-        for call in range(len(QUANT_CALLS)):
-            quantise(0, call)
-        move_planes(0)
-        for q in range(SHIFTED_BUFS):
-            load_item(q)
-        for q in range(SUMS_AHEAD):
-            subtract_item(nc.gpsimd, q)
-            if q + SHIFTED_BUFS < LOAD_AHEAD:
-                load_item(q + SHIFTED_BUFS)
-            square_item(q)
-            sum_item(q)
-            if q < EXP_AHEAD:
-                exp_item(q)
-                mask_item(q)
+        later_groups = {0: (4, nc.gpsimd), 2: (5, nc.vector), 4: (6, nc.gpsimd), 6: (7, nc.vector)}
+        spread_step = 11
+        first_block_step = 13
+        blocks_per_step = 2
+        n_block = 0
+        n_aggregated = 0
+        quads_to_collect = []
+        stage_queue = {}
 
+        def plan(step, stage, t):
+            stage_queue.setdefault(step, []).append((stage, t))
+
+        tail = 3 + 5 + TILES
         with tc.manual_schedule():
-            for phase in range(KW):
-                dj = phase - R
+            nc.gpsimd.memset(spread[:], 0.0)
+            for step in range(STEPS + tail):
+                adding = step < STEPS
+                phase, k = divmod(step, KW)
+                dj, di = phase - R, k - R
                 b = phase % 2
-                is_last = phase == KW - 1
-                if phase == 1:
+
+                if step == 1:
                     fuse_codes, fuse_plane = load_weight(w_fuse_words, w_fuse_scales, "fuse")
                     x_res = late.tile([P, C // P, NPX], BF16, name="x_res")
                     nc.sync.dma_start(out=x_res[:], in_=x[0].rearrange("(m p) h w -> p m (h w)", p=P))
-                for step in range(LAST_STEPS if is_last else STEPS):
-                    rnd, k = divmod(step, KW)
-                    n = ROUNDS * phase + rnd
-                    adding = step < STEPS
-                    sums_left = n >= 1 and rnd <= ROUNDS
+                if step in later_groups:
+                    i, engine = later_groups[step]
+                    subtract(engine, i)
+                if step - 2 in later_groups:
+                    i = later_groups[step - 2][0]
+                    square_diff(i)
+                if step - 3 in later_groups:
+                    exps(later_groups[step - 3][0])
+                if step == spread_step - 1:
+                    softmax_out()
+                    nc.vector.tensor_reduce(out=inv_sum[:], in_=e_mid[:], axis=AXIS.X, op=ALU.add)
+                    nc.vector.tensor_scalar_add(out=inv_sum[:], in0=inv_sum[:], scalar1=1.0)
+                    nc.vector.reciprocal(out=inv_sum[:], in_=inv_sum[:])
+                if step == spread_step:
+                    for h in range(2):
+                        for half_row in range(HALF_ROWS):
+                            spread_out(h, half_row)
 
-                    if adding and k == 0 and n + LOAD_AHEAD < len(ITEMS):
-                        load_item(n + LOAD_AHEAD)
-                    if adding and k == 1 and n + EXP_AHEAD < len(ITEMS):
-                        exp_item(n + EXP_AHEAD)
-                    if adding and k == 1 and n + SUMS_AHEAD < len(ITEMS):
-                        subtract_item(nc.gpsimd, n + SUMS_AHEAD)
-                    if adding and k == 3 and n + EXP_AHEAD < len(ITEMS):
-                        mask_item(n + EXP_AHEAD)
-                    if adding and k == 3 and n + SUMS_AHEAD < len(ITEMS):
-                        square_item(n + SUMS_AHEAD)
+                if adding and phase < KW - 1 and k == 4:
+                    move_codes(dj + 1, 1 - b)
+                if adding and phase < KW - 1 and k == 5:
+                    move_planes(1 - b)
+                for strip in range(STRIPS):
+                    if step == first_block_step - 2 + strip * B_PER_STRIP // blocks_per_step:
+                        gather_strip(strip)
 
-                    if sums_left and k == 6:
-                        collect(n - 1)
+                for stage, t in stage_queue.get(step, []):
+                    if stage in (add_x_and_store, quantise_agg, regroup_agg, normalise):
+                        stage(t)
 
-                    if not is_last:
-                        if step < NTILES:
-                            regroup(nc.scalar.copy, dj + 1, step)
-                        for call in range(len(QUANT_CALLS)):
-                            if step == last_slice_of(call, dj + 1) + 2:
-                                quantise(1 - b, call)
-                        if step == STEPS - 1:
-                            move_planes(1 - b)
+                if adding:
+                    is_first = step == 0
+                    for place in range(V_TILES):
+                        add_on_vector(b, place, di, dj, is_first)
+                        if V_TILES + place < TILES:
+                            add_on_gpsimd(b, V_TILES + place, di, dj, is_first)
 
-                    if is_last and adding and k == 4:
-                        tiles = slice(TILES_PER_ROUND * rnd, TILES_PER_ROUND * (rnd + 1))
-                        nc.vector.tensor_reduce(out=inv_sum[:, tiles], in_=e_all[:, tiles, :], axis=AXIS.X, op=ALU.add)
-                        nc.vector.tensor_scalar_add(out=inv_sum[:, tiles], in0=inv_sum[:, tiles], scalar1=1.0)
-                        nc.vector.reciprocal(out=inv_sum[:, tiles], in_=inv_sum[:, tiles])
-                    if is_last:
-                        for steps_ago, stage in ((5, add_x_and_store), (3, quantise_agg), (2, regroup_agg), (0, normalise)):
-                            if tile_entering(step - steps_ago) is not None:
-                                stage(tile_entering(step - steps_ago))
+                for m in quads_to_collect:
+                    collect_quad(m)
+                    strip, half = divmod(m, 2)
+                    if half == 1:
+                        base = 2 * TILES * (strip // 4) + 3 * (strip % 4 // 2)
+                        for place, tile in enumerate((base,) if strip % 2 == 0 else (base + 1, base + 2)):
+                            plan(step + 1 + place, quantise_agg, tile)
+                            plan(step + 2 + place, fuse, tile)
+                            plan(step + 3 + place, add_x_and_store, tile)
+                quads_to_collect = []
+                done = n_block
+                if step >= first_block_step:
+                    for i in range(blocks_per_step):
+                        if n_block < BLOCKS:
+                            make_messages(n_block)
+                            n_block += 1
+                while n_aggregated < done:
+                    aggregate(n_aggregated)
+                    n_aggregated += 1
+                    if n_aggregated % 4 == 0:
+                        quads_to_collect.append(n_aggregated // 4 - 1)
 
-                    if adding:
-                        di = k - R
-                        is_first = phase == 0 and k == 0
-                        first_tile = TILES_PER_ROUND * rnd
-                        for place in range(V_TILES):
-                            add_on_vector(b, first_tile + place, di, dj, is_first)
-                        add_on_gpsimd(b, first_tile + G_PLACE, di, dj, is_first)
-                        multiply_for_tensor(b, n, first_tile + T_PLACE, di, dj)
-
-                    if sums_left and 1 <= k <= PACK:
-                        add_on_tensor(n - 1, k - 1)
-                    if adding and k == 6 and n + SUMS_AHEAD < len(ITEMS):
-                        sum_item(n + SUMS_AHEAD)
-                    if is_last:
-                        for steps_ago, stage in ((4, fuse), (1, turn)):
-                            if tile_entering(step - steps_ago) is not None:
-                                stage(tile_entering(step - steps_ago))
+                if step - 2 in later_groups:
+                    sum_channels(later_groups[step - 2][0])
+                if step == spread_step:
+                    for bank_no in range(3):
+                        turn_out(bank_no)
+                for stage, t in stage_queue.get(step, []):
+                    if stage in (fuse, turn):
+                        stage(t)
+                if step == STEPS - 1:
+                    for t in range(TILES):
+                        plan(STEPS + t, normalise, t)
+                        plan(STEPS + t + 1, turn, t)
+                        plan(STEPS + t + 2, regroup_agg, t)
+                        plan(STEPS + t + 3, quantise_agg, TILES + t)
+                        plan(STEPS + t + 4, fuse, TILES + t)
+                        plan(STEPS + t + 5, add_x_and_store, TILES + t)

@@ -22,60 +22,63 @@ PROBS = 19
 R = 3
 KW = 2 * R + 1
 BN_EPS = 1e-5
-
-THIRD_ROWS = SIDE // 3
-THIRD_PX = THIRD_ROWS * SIDE
-TILES = THIRD_PX // P
 STEPS = KW * KW
 
 PITCH = SIDE + 2 * R
 WORDS = 2944
 QUANT_CALLS = ((0, 1024), (1024, 1024), (2048, 512), (2560, 256), (2816, 128))
 CHUNK_ROWS = 8
+THIRD_PX = NPX // 3
 
-MID_ROWS = THIRD_ROWS + 2 * R
-MID_COLS = MID_ROWS * SIDE
-PLANE_COPIES = 4
-PLANE_STEP = 16
-PLANE_PITCH = 1088
+CORE_ROW, CORE_COL = 16, 6
+CORE_ROWS, CORE_COLS = 16, 32
+CORE_USED = 30
+CORE_PX = CORE_ROWS * CORE_COLS
+CORE_TILES = CORE_PX // P
+TILE_ROWS = P // CORE_COLS
+MID_ROWS = CORE_ROWS + 2 * R
+MID_COLS = MID_ROWS * CORE_COLS
 
 B_ROWS, B_COLS = 4, 6
 B_PX = B_ROWS * B_COLS
 Q_ROWS, Q_COLS = B_ROWS + 2 * R, B_COLS + 2 * R
 Q_PX = Q_ROWS * Q_COLS
-STRIPS = 2 * THIRD_ROWS // B_ROWS
-B_PER_STRIP = SIDE // B_COLS
-BLOCKS = STRIPS * B_PER_STRIP
-HALF_ROWS = B_ROWS // 2
-CLASSES = HALF_ROWS * B_COLS
+STRIPS = SIDE // B_ROWS
+PER_STRIP = SIDE // B_COLS
+LANES = STRIPS * PER_STRIP
 
-GROUP = 6
-OFFSET_ROWS = PROBS + 1
-ROWS_USED = GROUP * OFFSET_ROWS
+SETS = 4
+D = 6
+CH = 5
+SLICES = 4
+SET_ROWS = 32
 PAD_LEFT = 4
 PAD_PITCH = PAD_LEFT + SIDE + 4
 PAD_ROWS = SIDE + 2 * R
+ROW_LEN = SIDE * PAD_PITCH
 RUN = (SIDE - 1) * PAD_PITCH + SIDE
 ONE_SIDE = (-3, -2, -1, 1, 2, 3)
-GROUPS = [KW] + list(range(KW))
-EARLY_GROUPS = 4
+SET_ORDER = [KW] + list(range(KW))
+CLASS_PX = LANES * B_PX
+SQ_COLS = CORE_PX + CLASS_PX + P - LANES
 SHIFTED_BUFS = 4
 
-V_TILES = 4
+STORE_ROWS = 32
+BLOCK_ROWS = STORE_ROWS * D
+PARK_PITCH = 3072
+
+PART_ONE = 10
+FIRST_BLOCK_STEP = 10
+FIRST_SUM_STEP = 12
+FIRST_GPSIMD_STEP = 6
 
 FLOPS = 2 * 2 * C * C * NPX + 2 * KW * KW * C * NPX
 
 
-def group_offsets(g):
-    if g < KW:
-        return [(d, g - R) for d in ONE_SIDE]
-    return [(0, d) for d in ONE_SIDE]
-
-
-def group_and_place(di, dj):
+def place_of(di, dj):
     if di != 0:
-        return dj + R, ONE_SIDE.index(di)
-    return KW, ONE_SIDE.index(dj)
+        return D * SET_ORDER.index(dj + R) + ONE_SIDE.index(di)
+    return D * SET_ORDER.index(KW) + ONE_SIDE.index(dj)
 
 
 def tile_dcblock_kernel(
@@ -96,7 +99,6 @@ def tile_dcblock_kernel(
     nc = tc.nc
     with ExitStack() as ctx:
         keep = ctx.enter_context(tc.tile_pool(name="keep", bufs=1))
-        work = ctx.enter_context(tc.tile_pool(name="work", bufs=2))
         psum_turns = ctx.enter_context(tc.psum_pool(name="psum_turns", bufs=4))
         psum_s = ctx.enter_context(tc.psum_pool(name="psum_s", bufs=2))
         psum_main = ctx.enter_context(tc.psum_pool(name="psum_main", bufs=2))
@@ -105,239 +107,398 @@ def tile_dcblock_kernel(
         make_identity(nc, ident_f32[:])
         ident_bf16 = keep.tile([P, P], BF16, name="ident_bf16")
         make_identity(nc, ident_bf16[:])
-        selector = keep.tile([P, GROUP], F32, name="selector")
-        by_offset = ident_f32[:, 0:ROWS_USED].rearrange("p (j c) -> p j c", c=OFFSET_ROWS)
-        nc.vector.tensor_reduce(out=selector[:], in_=by_offset[:, :, 0:PROBS], axis=AXIS.X, op=ALU.add)
         minus_one = keep.tile([P, 1], F32, name="minus_one")
         nc.vector.memset(minus_one[:], -1.0)
 
         codes_img = keep.tile([P, WORDS], U32, name="codes_img", align_bytes=64)
         plane_img = keep.tile([P, WORDS], U8, name="plane_img", align_bytes=64)
         codes = [keep.tile([P, MID_COLS], U32, name="codes%d" % b, align_bytes=64) for b in range(2)]
-        planes = [keep.tile([P, PLANE_COPIES, PLANE_PITCH], U8, name="planes%d" % b, align_bytes=64) for b in range(2)]
-        q_codes = [keep.tile([P, B_PER_STRIP, P], U32, name="q_codes%d" % b, align_bytes=64) for b in range(2)]
-        q_plane = [keep.tile([P, B_PER_STRIP, P], U8, name="q_plane%d" % b, align_bytes=64) for b in range(2)]
-        acc = [keep.tile([P, C], F32, name="acc%d" % t) for t in range(TILES)]
-        shifted = [keep.tile([P, SIDE * PAD_PITCH], BF16, name="shifted%d" % b) for b in range(SHIFTED_BUFS)]
-        centre = keep.tile([P, SIDE * PAD_PITCH], BF16, name="centre")
-        e_mid = keep.tile([P, TILES, (KW + 1) * GROUP], F32, name="e_mid")
-        inv_sum = keep.tile([P, TILES], F32, name="inv_sum")
-        e_out = keep.tile([P, CLASSES, KW, KW], F32, name="e_out")
-        out_sum = keep.tile([P, CLASSES], F32, name="out_sum")
+        planes = [keep.tile([P, 2, MID_COLS], U8, name="planes%d" % b, align_bytes=64) for b in range(2)]
+        q_codes = [keep.tile([P, PER_STRIP, P], U32, name="q_codes%d" % b, align_bytes=64) for b in range(2)]
+        q_plane = [keep.tile([P, PER_STRIP, P], U8, name="q_plane%d" % b, align_bytes=64) for b in range(2)]
+        acc = [keep.tile([P, C], F32, name="acc%d" % t) for t in range(CORE_TILES)]
+        dist_core = keep.tile([P, CORE_TILES, 2 * SETS * D], F32, name="dist_core")
+        e_core = keep.tile([P, CORE_TILES, 2 * SETS * D], F32, name="e_core")
+        inv_sum = keep.tile([P, CORE_TILES], F32, name="inv_sum")
+        dist_class = keep.tile([P, B_PX, 2 * SETS * D], F32, name="dist_class")
+        e_class = keep.tile([P, B_PX, 8, 8], F32, name="e_class")
+        inv_class = keep.tile([P, B_PX], F32, name="inv_class")
+        spread = keep.tile([P, B_PX, P], F32, name="spread")
+        nc.vector.memset(e_class[:, :, R, R], 1.0)
+        nc.gpsimd.memset(spread[:], 0.0)
 
-        nc.vector.memset(e_out[:, :, R, R], 1.0)
-
-        with tc.tile_pool(name="early", bufs=1) as first:
-            padded = first.tile([OFFSET_ROWS, PAD_ROWS, PAD_PITCH], BF16, name="padded")
-            nc.vector.memset(padded[:], 0.0)
-            for channels in (slice(0, 16), slice(16, PROBS)):
+        def load_weight(words, scales, label):
+            w_codes = keep.tile([P, C], U32, name=label + "_codes", align_bytes=64)
+            nc.sync.dma_start(out=w_codes[:].bitcast(I32), in_=words[0].rearrange("p n t -> p (n t)").bitcast(I32))
+            w_plane = keep.tile([P, C], U8, name=label + "_plane", align_bytes=64)
+            nc.vector.memset(w_plane[:].bitcast(I32), 0)
+            scale_rows = scales[0].bitcast(I32)
+            for quadrant in range(4):
                 nc.sync.dma_start(
-                    out=padded[channels, R : R + SIDE, PAD_LEFT : PAD_LEFT + SIDE], in_=coarse_probs[0, channels]
+                    out=w_plane[32 * quadrant : 32 * quadrant + 4, :].bitcast(I32),
+                    in_=scale_rows[4 * quadrant : 4 * quadrant + 4, :],
+                )
+            return w_codes, w_plane
+
+        def messages_of_neighbours(bank, b, t, di):
+            col = P * t + CORE_COLS * (di + R)
+            v = (di + R) % 2
+            plane_col = col - CORE_COLS * v
+            nc.tensor.matmul_mx(
+                out=bank[:],
+                lhsT=codes[b][:, col : col + P].bitcast(FP8X4), lhsT_scale=planes[b][:, v, plane_col : plane_col + P],
+                rhs=feat_codes[:].bitcast(FP8X4), rhs_scale=feat_plane[:], start=True, stop=True,
+            )
+
+        def weight(t, di, dj):
+            if di == 0 and dj == 0:
+                return 1.0
+            j = place_of(di, dj)
+            return e_core[:, t, j : j + 1]
+
+        def add_on_vector(b, t, di, dj, is_first):
+            bank = psum_turns.tile([P, C], F32, name="bank_v", tag="bank")
+            messages_of_neighbours(bank, b, t, di)
+            if is_first:
+                nc.vector.tensor_scalar_mul(out=acc[t][:], in0=bank[:], scalar1=weight(t, di, dj))
+            else:
+                nc.vector.scalar_tensor_tensor(
+                    out=acc[t][:], in0=bank[:], scalar=weight(t, di, dj), in1=acc[t][:], op0=ALU.mult, op1=ALU.add
                 )
 
-            sigma_bf = first.tile([P, 1], BF16, name="sigma_bf")
-            nc.scalar.dma_start(out=sigma_bf[:], in_=sigma.partition_broadcast(P))
-            bn_in = {}
-            for label, vec in (("var", bn_var), ("gamma", bn_gamma), ("mean", bn_mean), ("beta", bn_beta)):
-                bn_in[label] = first.tile([P, PACK], BF16, name="bn_" + label)
-                nc.scalar.dma_start(out=bn_in[label][:], in_=vec.rearrange("(p j) -> p j", j=PACK))
-            x_raw = first.tile([P, PACK, NPX], BF16, name="x_raw")
-            xn = first.tile([P, PACK, NPX], BF16, name="xn")
-            grouped = first.tile([P, WORDS, PACK], BF16, name="grouped", align_bytes=64)
-            x_by_word = x[0].rearrange("(p j) h w -> p j (h w)", j=PACK)
-            for third in range(3):
-                px = slice(THIRD_PX * third, THIRD_PX * (third + 1))
-                nc.sync.dma_start(out=x_raw[:, :, px], in_=x_by_word[:, :, px])
-
-            parked = out[0].rearrange("c h w -> c (h w)").bitcast(BF16)[0:OFFSET_ROWS, 0 : PAD_ROWS * PAD_PITCH]
-            nc.sync.dma_start(out=parked, in_=padded[:].rearrange("c h w -> c (h w)"))
-
-            def load_shifted(tile, j, di, dj):
-                start = (R + di) * PAD_PITCH + PAD_LEFT + dj
-                nc.sync.dma_start(out=tile[OFFSET_ROWS * j : OFFSET_ROWS * (j + 1), 0:RUN], in_=parked[:, start : start + RUN])
-
-            def load_group(i):
-                for j, (di, dj) in enumerate(group_offsets(GROUPS[i])):
-                    load_shifted(shifted[i % SHIFTED_BUFS], j, di, dj)
-
-            def load_weight(words, scales, label):
-                w_codes = keep.tile([P, C], U32, name=label + "_codes", align_bytes=64)
-                nc.sync.dma_start(out=w_codes[:].bitcast(I32), in_=words[0].rearrange("p n t -> p (n t)").bitcast(I32))
-                w_plane = keep.tile([P, C], U8, name=label + "_plane", align_bytes=64)
-                nc.vector.memset(w_plane[:].bitcast(I32), 0)
-                scale_rows = scales[0].bitcast(I32)
-                for quadrant in range(4):
-                    nc.sync.dma_start(
-                        out=w_plane[32 * quadrant : 32 * quadrant + 4, :].bitcast(I32),
-                        in_=scale_rows[4 * quadrant : 4 * quadrant + 4, :],
-                    )
-                return w_codes, w_plane
-
-            def fill_unused(tile):
-                nc.sync.dma_start(out=tile[ROWS_USED:P, 0:RUN], in_=parked[0 : P - ROWS_USED, 0:RUN])
-
-            for j in range(GROUP):
-                load_shifted(centre, j, 0, 0)
-            fill_unused(centre)
-            for i in range(EARLY_GROUPS):
-                fill_unused(shifted[i])
-                load_group(i)
-                if i == 1:
-                    feat_codes, feat_plane = load_weight(w_feat_words, w_feat_scales, "feat")
-
-            neg_inv_denom = keep.tile([P, 1], F32, name="neg_inv_denom")
-            nc.vector.tensor_scalar_max(out=neg_inv_denom[:], in0=sigma_bf[:], scalar1=0.0)
-            nc.vector.tensor_mul(out=neg_inv_denom[:], in0=neg_inv_denom[:], in1=neg_inv_denom[:])
-            nc.vector.tensor_scalar(
-                out=neg_inv_denom[:], in0=neg_inv_denom[:], scalar1=-2.0, scalar2=-1e-8, op0=ALU.mult, op1=ALU.add
+        def move_codes(dj, b):
+            rows = slice(CORE_ROW * PITCH, (CORE_ROW + MID_ROWS) * PITCH)
+            cols = slice(CORE_COL + R + dj, CORE_COL + R + dj + CORE_COLS)
+            nc.vector.tensor_copy(
+                out=codes[b][:].bitcast(I32).rearrange("p (r w) -> p r w", w=CORE_COLS),
+                in_=codes_img[:, rows].bitcast(I32).rearrange("p (r w) -> p r w", w=PITCH)[:, :, cols],
             )
-            nc.vector.reciprocal(out=neg_inv_denom[:], in_=neg_inv_denom[:])
-            bn_scale = keep.tile([P, PACK], F32, name="bn_scale")
-            bn_shift = keep.tile([P, PACK], F32, name="bn_shift")
-            nc.vector.tensor_scalar_add(out=bn_scale[:], in0=bn_in["var"][:], scalar1=BN_EPS)
-            nc.scalar.sqrt(out=bn_scale[:], in_=bn_scale[:])
-            nc.vector.reciprocal(out=bn_scale[:], in_=bn_scale[:])
-            nc.vector.tensor_mul(out=bn_scale[:], in0=bn_scale[:], in1=bn_in["gamma"][:])
-            nc.vector.tensor_mul(out=bn_shift[:], in0=bn_scale[:], in1=bn_in["mean"][:])
-            nc.vector.tensor_sub(out=bn_shift[:], in0=bn_in["beta"][:], in1=bn_shift[:])
+            nc.vector.tensor_copy(
+                out=planes[b][:, 0, :].rearrange("p (r w) -> p r w", w=CORE_COLS),
+                in_=plane_img[:, rows].rearrange("p (r w) -> p r w", w=PITCH)[:, :, cols],
+            )
 
-            top = R * PITCH + R
-            nc.vector.memset(grouped[:, 0:top, :], 0.0)
-            nc.vector.memset(grouped[:, (R + SIDE) * PITCH - R : WORDS, :], 0.0)
-            between = grouped[:, top + SIDE : top + SIDE + (SIDE - 1) * PITCH, :].rearrange("p (r w) j -> p r w j", w=PITCH)
-            nc.vector.memset(between[:, :, 0 : 2 * R, :], 0.0)
-            nc.vector.memset(plane_img[:].bitcast(I32), 0)
-            for b in range(2):
-                nc.vector.memset(q_codes[b][:, :, Q_PX:P], 0)
-                nc.vector.memset(q_plane[b][:].bitcast(I32), 0)
+        def move_plane(b):
+            nc.vector.tensor_copy(
+                out=planes[b][:, 1, 0 : MID_COLS - CORE_COLS].bitcast(I32), in_=planes[b][:, 0, CORE_COLS:MID_COLS].bitcast(I32)
+            )
 
-            for third in range(3):
-                px = slice(THIRD_PX * third, THIRD_PX * (third + 1))
-                for j in range(PACK):
-                    if j % 2 == 0:
-                        nc.scalar.activation(
-                            out=xn[:, j, px], in_=x_raw[:, j, px], func=ACT.Identity,
-                            scale=bn_scale[:, j : j + 1], bias=bn_shift[:, j : j + 1],
+        def next_codes(step):
+            phase, k = divmod(step, KW)
+            if phase < KW - 1 and k == 4:
+                move_codes(phase + 1 - R, (phase + 1) % 2)
+            if phase < KW - 1 and k == 5:
+                move_plane((phase + 1) % 2)
+
+        def add_on_gpsimd(b, t, di, dj):
+            bank = psum_s.tile([P, C], F32, name="bank_s")
+            messages_of_neighbours(bank, b, t, di)
+            product = pools["product"].tile([P, C], F32, name="product")
+            nc.scalar.activation(out=product[:], in_=bank[:], func=ACT.Copy, scale=weight(t, di, dj))
+            nc.gpsimd.tensor_tensor(out=acc[t][:], in0=acc[t][:], in1=product[:], op=ALU.add)
+
+        def add_products(step, between=None):
+            phase, k = divmod(step, KW)
+            for t in range(CORE_TILES):
+                if t == CORE_TILES - 1 and step >= FIRST_GPSIMD_STEP:
+                    add_on_gpsimd(phase % 2, t, k - R, phase - R)
+                else:
+                    add_on_vector(phase % 2, t, k - R, phase - R, step == 0)
+                if between is not None:
+                    between(1)
+
+        pools = {}
+        with ExitStack() as ctx_one:
+            dist = ctx_one.enter_context(tc.tile_pool(name="dist", bufs=1))
+            centre = [dist.tile([P, ROW_LEN], BF16, name="centre%d" % s) for s in range(SLICES)]
+            shifted = [dist.tile([P, ROW_LEN], BF16, name="shifted%d" % b) for b in range(SHIFTED_BUFS)]
+            sq = []
+
+            def more_squares(pool, n):
+                for b in range(len(sq), len(sq) + n):
+                    tile = pool.tile([P, SQ_COLS], F32, name="sq%d" % b)
+                    nc.vector.memset(tile[:, CORE_PX + CLASS_PX : SQ_COLS], 0.0)
+                    sq.append(tile)
+
+            more_squares(dist, SLICES + 1)
+
+            def load_shifted(u):
+                half, s = divmod(u, SLICES)
+                for pos in range(SETS):
+                    g = SET_ORDER[SETS * half + pos]
+                    start = PAD_LEFT + g - R if g < KW else 2 * R + 1
+                    rows = parked_of(2 if g < KW else 0, s)
+                    nc.sync.dma_start(
+                        out=shifted[u % SHIFTED_BUFS][SET_ROWS * pos : SET_ROWS * (pos + 1), 0:RUN], in_=rows[:, start : start + RUN]
+                    )
+
+            def subtract_core(engine, u):
+                def core(t):
+                    rows = t[:].rearrange("p (h w) -> p h w", w=PAD_PITCH)
+                    return rows[:, CORE_ROW : CORE_ROW + CORE_ROWS, CORE_COL : CORE_COL + CORE_COLS]
+
+                engine.tensor_tensor(
+                    out=sq[u][:, 0:CORE_PX].rearrange("p (h w) -> p h w", w=CORE_COLS),
+                    in0=core(shifted[u % SHIFTED_BUFS]), in1=core(centre[u % SLICES]), op=ALU.subtract,
+                )
+
+            def subtract_class(engine, u):
+                a, c, d = shifted[u % SHIFTED_BUFS], centre[u % SLICES], sq[u]
+
+                def class_row(t, i):
+                    rows = t[:].rearrange("p (b i w) -> p b i w", i=B_ROWS, w=PAD_PITCH)
+                    return rows[:, :, i, 0:SIDE].rearrange("p b (c j) -> p j b c", j=B_COLS)
+
+                for i in range(B_ROWS):
+                    first_col = CORE_PX + LANES * B_COLS * i
+                    engine.tensor_tensor(
+                        out=d[:, first_col : first_col + LANES * B_COLS].rearrange("p (j b c) -> p j b c", j=B_COLS, c=PER_STRIP),
+                        in0=class_row(a, i), in1=class_row(c, i), op=ALU.subtract,
+                    )
+
+            def square_core(u):
+                d = sq[u]
+                nc.scalar.activation(out=d[:, 0:CORE_PX], in_=d[:, 0:CORE_PX], func=ACT.Square)
+
+            def square_class(u):
+                d = sq[u]
+                nc.scalar.activation(out=d[:, CORE_PX:SQ_COLS], in_=d[:, CORE_PX:SQ_COLS], func=ACT.Square)
+
+            banks = {}
+
+            def turn_squares(half, q):
+                banks[half, q] = psum_turns.tile([P, 4, P], F32, name="turned_squares", tag="bank")
+                for m in range(4):
+                    first_col = P * m if q == 0 else CORE_PX + LANES * (4 * (q - 1) + m)
+                    for s in range(SLICES):
+                        nc.tensor.matmul(
+                            out=banks[half, q][:, m, :], lhsT=sq[SLICES * half + s][:, first_col : first_col + P],
+                            rhs=ident_f32[:], is_transpose=True, start=(s == 0), stop=(s == SLICES - 1),
                         )
+
+            def sum_channels(half, q):
+                dst = dist_core[:] if q == 0 else dist_class[:, 4 * (q - 1) : 4 * q, :]
+                nc.vector.tensor_reduce(
+                    out=dst[:, :, SETS * D * half : SETS * D * (half + 1)].rearrange("p m (g d) -> p m g d", d=D),
+                    in_=banks[half, q][:].rearrange("p m (g r) -> p m g r", r=SET_ROWS)[:, :, :, 0 : CH * D].rearrange(
+                        "p m g (c d) -> p m g d c", d=D
+                    ),
+                    axis=AXIS.X, op=ALU.add,
+                )
+
+            def exp_core(half):
+                cols = slice(SETS * D * half, SETS * D * (half + 1))
+                nc.scalar.activation(out=dist_core[:, :, cols], in_=dist_core[:, :, cols], func=ACT.Exp, scale=neg_inv_denom[:, 0:1])
+                nc.scalar.activation(out=e_core[:, :, cols], in_=dist_core[:, :, cols], func=ACT.Exp, bias=minus_one[:, 0:1])
+
+            def exp_class(half):
+                cols = slice(SETS * D * half, SETS * D * (half + 1))
+                nc.scalar.activation(out=dist_class[:, :, cols], in_=dist_class[:, :, cols], func=ACT.Exp, scale=neg_inv_denom[:, 0:1])
+                for pos in range(SETS):
+                    g = SET_ORDER[SETS * half + pos]
+                    first_col = D * (SETS * half + pos)
+                    if g < KW:
+                        places = e_class[:, :, :, g]
                     else:
+                        places = e_class[:, :, R, :]
+                    nc.scalar.activation(
+                        out=places.rearrange("p k (s r) -> p k s r", s=2)[:, :, :, 0:R],
+                        in_=dist_class[:, :, first_col : first_col + D].rearrange("p k (s r) -> p k s r", s=2),
+                        func=ACT.Exp, bias=minus_one[:, 0:1],
+                    )
+
+            with tc.tile_pool(name="early", bufs=1) as first:
+                padded = first.tile([P, PAD_ROWS, PAD_PITCH], BF16, name="padded")
+                nc.vector.memset(padded[:].rearrange("c h w -> c (h w)").bitcast(I32), 0)
+                for channels in (slice(0, 16), slice(16, PROBS)):
+                    nc.sync.dma_start(
+                        out=padded[4 * channels.start : 4 * channels.stop : 4, R : R + SIDE, PAD_LEFT : PAD_LEFT + SIDE],
+                        in_=coarse_probs[0, channels],
+                    )
+                sigma_bf = first.tile([P, 1], BF16, name="sigma_bf")
+                nc.scalar.dma_start(out=sigma_bf[:], in_=sigma.partition_broadcast(P))
+                bn_in = {}
+                for label, vec in (("var", bn_var), ("gamma", bn_gamma), ("mean", bn_mean), ("beta", bn_beta)):
+                    bn_in[label] = first.tile([P, PACK], BF16, name="bn_" + label)
+                    nc.scalar.dma_start(out=bn_in[label][:], in_=vec.rearrange("(p j) -> p j", j=PACK))
+                xn = first.tile([P, PACK, NPX], BF16, name="xn")
+                grouped = first.tile([P, WORDS, PACK], BF16, name="grouped", align_bytes=64)
+                x_by_word = x[0].rearrange("(p j) h w -> p j (h w)", j=PACK)
+                for third in range(3):
+                    px = slice(THIRD_PX * third, THIRD_PX * (third + 1))
+                    nc.sync.dma_start(out=xn[:, :, px], in_=x_by_word[:, :, px])
+
+                parked = out[0].rearrange("c h w -> (c h w)").bitcast(BF16).rearrange("(r n) -> r n", n=PARK_PITCH)
+
+                def parked_of(block, s):
+                    first_row = BLOCK_ROWS * block + CH * D * s
+                    return parked[first_row : first_row + SET_ROWS, :]
+
+                flat = padded[0:P:4].rearrange("c h w -> c (h w)")
+                for block in (0, 1, 2):
+                    rows = parked[BLOCK_ROWS * block : BLOCK_ROWS * (block + 1), :].rearrange("(c d) n -> c d n", d=D)
+                    for d in range(D):
+                        row0 = R + ONE_SIDE[d] if block == 2 else R
+                        at = R - ONE_SIDE[d] if block == 0 else 0
+                        nc.sync.dma_start(
+                            out=rows[:, d, at : at + ROW_LEN], in_=flat[:, PAD_PITCH * row0 : PAD_PITCH * row0 + ROW_LEN]
+                        )
+
+                def load_centre(s):
+                    for pos in range(SETS):
+                        nc.sync.dma_start(
+                            out=centre[s][SET_ROWS * pos : SET_ROWS * (pos + 1), 0:RUN],
+                            in_=parked_of(1, s)[:, PAD_LEFT : PAD_LEFT + RUN],
+                        )
+
+                for s in range(SLICES):
+                    load_centre(s)
+                    load_shifted(s)
+                feat_codes, feat_plane = load_weight(w_feat_words, w_feat_scales, "feat")
+
+                neg_inv_denom = keep.tile([P, 1], F32, name="neg_inv_denom")
+                nc.vector.tensor_scalar_max(out=neg_inv_denom[:], in0=sigma_bf[:], scalar1=0.0)
+                nc.vector.tensor_mul(out=neg_inv_denom[:], in0=neg_inv_denom[:], in1=neg_inv_denom[:])
+                nc.vector.tensor_scalar(
+                    out=neg_inv_denom[:], in0=neg_inv_denom[:], scalar1=-2.0, scalar2=-1e-8, op0=ALU.mult, op1=ALU.add
+                )
+                nc.vector.reciprocal(out=neg_inv_denom[:], in_=neg_inv_denom[:])
+                bn_scale = keep.tile([P, PACK], F32, name="bn_scale")
+                bn_shift = keep.tile([P, PACK], F32, name="bn_shift")
+                nc.vector.tensor_scalar_add(out=bn_scale[:], in0=bn_in["var"][:], scalar1=BN_EPS)
+                nc.scalar.sqrt(out=bn_scale[:], in_=bn_scale[:])
+                nc.vector.reciprocal(out=bn_scale[:], in_=bn_scale[:])
+                nc.vector.tensor_mul(out=bn_scale[:], in0=bn_scale[:], in1=bn_in["gamma"][:])
+                nc.vector.tensor_mul(out=bn_shift[:], in0=bn_scale[:], in1=bn_in["mean"][:])
+                nc.vector.tensor_sub(out=bn_shift[:], in0=bn_in["beta"][:], in1=bn_shift[:])
+
+                top = R * PITCH + R
+                nc.vector.memset(grouped[:, 0:top, :], 0.0)
+                nc.vector.memset(grouped[:, (R + SIDE) * PITCH - R : WORDS, :], 0.0)
+                between = grouped[:, top + SIDE : top + SIDE + (SIDE - 1) * PITCH, :].rearrange("p (r w) j -> p r w j", w=PITCH)
+                nc.vector.memset(between[:, :, 0 : 2 * R, :], 0.0)
+                nc.vector.memset(plane_img[:].bitcast(I32), 0)
+                for b in range(2):
+                    nc.vector.memset(q_codes[b][:, :, Q_PX:P], 0)
+                    nc.vector.memset(q_plane[b][:].bitcast(I32), 0)
+
+                for third in range(3):
+                    px = slice(THIRD_PX * third, THIRD_PX * (third + 1))
+                    for j in range(PACK):
                         nc.vector.tensor_scalar(
-                            out=xn[:, j, px], in0=x_raw[:, j, px],
+                            out=xn[:, j, px], in0=xn[:, j, px],
                             scalar1=bn_scale[:, j : j + 1], scalar2=bn_shift[:, j : j + 1], op0=ALU.mult, op1=ALU.add,
                         )
-            image = grouped[:, top : top + SIDE * PITCH, :].rearrange("p (r w) j -> p r w j", w=PITCH)
-            for chunk in range(SIDE // CHUNK_ROWS):
-                rows = slice(CHUNK_ROWS * chunk, CHUNK_ROWS * (chunk + 1))
-                engine_copy = nc.scalar.copy if chunk in (0, 5) else nc.vector.tensor_copy
-                engine_copy(
-                    out=image[:, rows, 0:SIDE, :],
-                    in_=xn[:, :, SIDE * rows.start : SIDE * rows.stop].rearrange("p j (r w) -> p r w j", w=SIDE),
-                )
-            for first_word, n in QUANT_CALLS:
-                words = slice(first_word, first_word + n)
-                nc.vector.quantize_mx(
-                    out=codes_img[:, words].bitcast(FP8X4), scales=plane_img[:, words],
-                    in_=grouped[:, words, :].rearrange("p w j -> p (w j)"),
-                )
-
-            diff = {}
-            square = {}
-            sums = {}
-
-            def subtract(engine, i):
-                diff[i] = work.tile([P, NPX], F32, name="diff")
-                thirds = "p (t h w) -> p t h w"
-                a = shifted[i % SHIFTED_BUFS][:].rearrange(thirds, t=3, w=PAD_PITCH)[:, :, :, 0:SIDE]
-                c = centre[:].rearrange(thirds, t=3, w=PAD_PITCH)[:, :, :, 0:SIDE]
-                for place, third in ((0, 1), (1, 0), (2, 2)):
-                    engine.tensor_tensor(
-                        out=diff[i][:, THIRD_PX * place : THIRD_PX * (place + 1)].rearrange("p (h w) -> p h w", w=SIDE),
-                        in0=a[:, third], in1=c[:, third], op=ALU.subtract,
+                image = grouped[:, top : top + SIDE * PITCH, :].rearrange("p (r w) j -> p r w j", w=PITCH)
+                for chunk in range(SIDE // CHUNK_ROWS):
+                    rows = slice(CHUNK_ROWS * chunk, CHUNK_ROWS * (chunk + 1))
+                    engine_copy = nc.scalar.copy if chunk in (0, 5) else nc.vector.tensor_copy
+                    engine_copy(
+                        out=image[:, rows, 0:SIDE, :],
+                        in_=xn[:, :, SIDE * rows.start : SIDE * rows.stop].rearrange("p j (r w) -> p r w j", w=SIDE),
                     )
-
-            def square_diff(i):
-                square[i] = work.tile([P, NPX], F32, name="square")
-                nc.scalar.activation(out=square[i][:, 0:THIRD_PX], in_=diff[i][:, 0:THIRD_PX], func=ACT.Square)
-                by_class = square[i][:, THIRD_PX:NPX].rearrange("p (i j m) -> p i j m", i=HALF_ROWS, j=B_COLS)
-                source = diff[i][:, THIRD_PX:NPX].rearrange(
-                    "p (b h i c j) -> p h i j b c", b=STRIPS, h=2, i=HALF_ROWS, j=B_COLS
-                )
-                for h in range(2):
-                    for half_row in range(HALF_ROWS):
-                        nc.scalar.activation(
-                            out=by_class[:, half_row, :, 64 * h : 64 * (h + 1)].rearrange("p j (b c) -> p j b c", b=STRIPS),
-                            in_=source[:, h, half_row], func=ACT.Square,
-                        )
-
-            def sum_channels(i):
-                sums[i] = psum_turns.tile([P, NPX // P, GROUP], F32, name="sums", tag="bank")
-                for m in range(NPX // P):
-                    nc.tensor.matmul(
-                        out=sums[i][:, m, :], lhsT=square[i][:, P * m : P * (m + 1)], rhs=selector[:], start=True, stop=True
+                for first_word, n in QUANT_CALLS:
+                    words = slice(first_word, first_word + n)
+                    nc.vector.quantize_mx(
+                        out=codes_img[:, words].bitcast(FP8X4), scales=plane_img[:, words],
+                        in_=grouped[:, words, :].rearrange("p w j -> p (w j)"),
                     )
+                move_codes(-R, 0)
+                move_plane(0)
 
-            def exps(i):
-                g = GROUPS[i]
-                a = work.tile([P, NPX // P, GROUP], F32, name="a")
-                nc.scalar.activation(out=a[:], in_=sums[i][:], func=ACT.Exp, scale=neg_inv_denom[:, 0:1])
-                nc.scalar.activation(
-                    out=e_mid[:, :, GROUP * g : GROUP * (g + 1)], in_=a[:, 0:TILES, :], func=ACT.Exp, bias=minus_one[:, 0:1]
-                )
-                if g < KW:
-                    places = e_out[:, :, :, g]
-                else:
-                    places = e_out[:, :, R, :]
-                for side in range(2):
-                    nc.scalar.activation(
-                        out=places[:, :, (R + 1) * side : (R + 1) * side + R],
-                        in_=a[:, TILES : NPX // P, R * side : R * (side + 1)], func=ACT.Exp, bias=minus_one[:, 0:1],
-                    )
-
-            for i in range(EARLY_GROUPS):
-                subtract(nc.gpsimd, i)
-                if i + SHIFTED_BUFS < len(GROUPS):
-                    load_group(i + SHIFTED_BUFS)
-                square_diff(i)
-                sum_channels(i)
-                exps(i)
-
-            def move_codes(dj, b):
-                row0 = THIRD_ROWS * PITCH
-                rows = slice(row0, row0 + MID_ROWS * PITCH)
-                cols = slice(R + dj, R + dj + SIDE)
-                nc.vector.tensor_copy(
-                    out=codes[b][:].bitcast(I32).rearrange("p (r w) -> p r w", w=SIDE),
-                    in_=codes_img[:, rows].bitcast(I32).rearrange("p (r w) -> p r w", w=PITCH)[:, :, cols],
-                )
-                nc.vector.tensor_copy(
-                    out=planes[b][:, 0, 0:MID_COLS].rearrange("p (r w) -> p r w", w=SIDE),
-                    in_=plane_img[:, rows].rearrange("p (r w) -> p r w", w=PITCH)[:, :, cols],
-                )
-
-            def move_planes(b):
-                for v in range(1, PLANE_COPIES):
-                    nc.vector.tensor_copy(
-                        out=planes[b][:, v, 0 : MID_COLS - PLANE_STEP * v].bitcast(I32),
-                        in_=planes[b][:, 0, PLANE_STEP * v : MID_COLS].bitcast(I32),
-                    )
-
-            move_codes(-R, 0)
-            move_planes(0)
+            pools["product"] = ctx_one.enter_context(tc.tile_pool(name="product_one", bufs=4))
+            more_squares(ctx_one.enter_context(tc.tile_pool(name="dist_two", bufs=1)), SLICES - 1)
+            with tc.manual_schedule():
+                for u in range(SLICES):
+                    subtract_core(nc.vector, u)
+                    if u % 2 == 0:
+                        subtract_class(nc.gpsimd, u)
+                    else:
+                        subtract_class(nc.vector, u)
+                    load_shifted(u + SLICES)
+                square_core(0)
+                square_core(1)
+                square_class(0)
+                square_core(2)
+                square_class(1)
+                square_core(3)
+                turn_squares(0, 0)
+                sum_channels(0, 0)
+                square_class(2)
+                exp_core(0)
+                square_class(3)
+                for step in range(PART_ONE):
+                    phase, k = divmod(step, KW)
+                    for u, at, engine in ((4, 0, nc.gpsimd), (5, 0, nc.gpsimd), (6, 1, nc.vector), (7, 3, nc.vector)):
+                        if step == at:
+                            subtract_core(engine, u)
+                            subtract_class(engine, u)
+                    for q in range(B_PX // 4 + 1):
+                        if q > 0 and step == q:
+                            sum_channels(0, q)
+                        if step == 6 + q // 2:
+                            sum_channels(1, q)
+                    if step == 7:
+                        exp_core(1)
+                        exp_class(0)
+                    if step == 9:
+                        exp_class(1)
+                    for u, at in ((4, 2), (6, 2), (7, 4), (5, 4)):
+                        if step == at:
+                            square_core(u)
+                            square_class(u)
+                    next_codes(step)
+                    add_products(step)
+                    for q in range(B_PX // 4 + 1):
+                        if q > 0 and step == q - 1:
+                            turn_squares(0, q)
+                        if step == 5 + q // 2:
+                            turn_squares(1, q)
+            fuse_codes, fuse_plane = load_weight(w_fuse_words, w_fuse_scales, "fuse")
 
         late = ctx.enter_context(tc.tile_pool(name="late", bufs=1))
         late_work = ctx.enter_context(tc.tile_pool(name="late_work", bufs=3))
-        product_pool = ctx.enter_context(tc.tile_pool(name="product_pool", bufs=6))
-        message_pool = ctx.enter_context(tc.tile_pool(name="message_pool", bufs=4))
+        pools["product"] = ctx.enter_context(tc.tile_pool(name="product_two", bufs=6))
+        message_pool = ctx.enter_context(tc.tile_pool(name="message_pool", bufs=8))
         out_by_tile = out[0].rearrange("(m p) h w -> p m (h w)", p=P)
-        spread = late.tile([P, CLASSES, P], F32, name="spread")
-        weights = late.tile([P, BLOCKS, B_PX], F32, name="weights")
-        agg_out = late.tile([P, 2, THIRD_PX, PACK], BF16, name="agg_out", align_bytes=64)
+        weights = late.tile([P, LANES, B_PX], F32, name="weights")
+        agg_img = late.tile([P, NPX, PACK], BF16, name="agg_img", align_bytes=64)
+        x_res = late.tile([P, C // P, NPX], BF16, name="x_res")
 
-        def strip_row(strip):
-            return (strip // 4) * 2 * THIRD_ROWS + (strip % 4) * B_ROWS
+        def spread_class():
+            seven = e_class[:, :, 0:KW, 0:KW]
+            nc.vector.tensor_reduce(out=inv_class[:], in_=seven, axis=AXIS.XY, op=ALU.add)
+            nc.vector.reciprocal(out=inv_class[:], in_=inv_class[:])
+            for k in range(B_PX):
+                i, j = divmod(k, B_COLS)
+                window = spread[:, k, 0:Q_PX].rearrange("p (r c) -> p r c", c=Q_COLS)
+                nc.vector.tensor_scalar_mul(
+                    out=window[:, i : i + KW, j : j + KW], in0=seven[:, k], scalar1=inv_class[:, k : k + 1]
+                )
+
+        turned_class = {}
+
+        def turn_class(q):
+            turned_class[q] = psum_turns.tile([P, 4, P], F32, name="turned_class", tag="bank")
+            for m in range(4):
+                nc.tensor.transpose(out=turned_class[q][:, m, :], in_=spread[:, 4 * q + m, :], identity=ident_f32[:])
+
+        def collect_class(engine_copy, q):
+            engine_copy(
+                out=weights[:, :, 4 * q : 4 * q + 4], in_=turned_class[q][:].rearrange("q m b -> q b m")[:, 0:LANES, :]
+            )
+
+        strips = []
+        for strip in range(STRIPS):
+            row = B_ROWS * strip
+            in_core = CORE_ROW <= row < CORE_ROW + CORE_ROWS
+            taken = range(CORE_COL // B_COLS, (CORE_COL + CORE_USED) // B_COLS) if in_core else ()
+            strips.append([bc for bc in range(PER_STRIP) if bc not in taken])
+        blocks = [(strip, bc) for strip in range(STRIPS) for bc in strips[strip]]
 
         def gather_strip(strip):
             b = strip % 2
-            start = strip_row(strip) * PITCH
+            start = B_ROWS * strip * PITCH
             rows = slice(start, start + Q_ROWS * PITCH)
             for half in range(2):
                 cols = slice(B_COLS * half, B_COLS * half + SIDE)
@@ -351,105 +512,54 @@ def tile_dcblock_kernel(
                         ),
                     )
 
-        def softmax_out():
-            nc.vector.tensor_reduce(
-                out=out_sum[:], in_=e_out[:].rearrange("p k a b -> p k (a b)"), axis=AXIS.X, op=ALU.add
-            )
-            nc.vector.reciprocal(out=out_sum[:], in_=out_sum[:])
-
-        def spread_out(h, half_row):
-            half = slice(64 * h, 64 * (h + 1))
-            ks = slice(B_COLS * half_row, B_COLS * (half_row + 1))
-            row = 2 * h + half_row
-            for j in range(B_COLS):
-                k = B_COLS * half_row + j
-                nc.vector.tensor_scalar_mul(
-                    out=spread[half, k, 0:Q_PX].rearrange("p (r c) -> p r c", c=Q_COLS)[:, row : row + KW, j : j + KW],
-                    in0=e_out[half, k], scalar1=out_sum[half, k : k + 1],
-                )
-
-        def turn_out(bank_no):
-            bank = psum_turns.tile([P, 4, P], F32, name="spread_turned", tag="bank")
-            for m in range(4):
-                nc.tensor.transpose(out=bank[:, m, :], in_=spread[:, 4 * bank_no + m, :], identity=ident_f32[:])
-            nc.scalar.copy(
-                out=weights[:].rearrange("q b (h k) -> q b h k", h=2)[:, :, :, 4 * bank_no : 4 * bank_no + 4],
-                in_=bank[:].rearrange("q m (h b) -> q b h m", h=2),
-            )
-
         messages = {}
         main_bank = {}
 
         def make_messages(n):
+            strip, bc = blocks[n]
             bank = psum_s.tile([P, C], F32, name="bank_s")
-            strip, place = divmod(n, B_PER_STRIP)
             nc.tensor.matmul_mx(
                 out=bank[:],
-                lhsT=q_codes[strip % 2][:, place, :].bitcast(FP8X4), lhsT_scale=q_plane[strip % 2][:, place, :],
+                lhsT=q_codes[strip % 2][:, bc, :].bitcast(FP8X4), lhsT_scale=q_plane[strip % 2][:, bc, :],
                 rhs=feat_codes[:].bitcast(FP8X4), rhs_scale=feat_plane[:], start=True, stop=True,
             )
             messages[n] = message_pool.tile([P, PACK, P], F32, name="messages")
             nc.scalar.copy(out=messages[n][:], in_=bank[:].rearrange("p (q j) -> p j q", j=PACK))
 
-        def aggregate(n):
-            if n % 4 == 0:
-                main_bank[n // 4] = psum_main.tile([P, PACK, B_ROWS, 4 * B_COLS], F32, name="main_bank")
-            bank = main_bank[n // 4]
-            cols = slice(B_COLS * (n % 4), B_COLS * (n % 4 + 1))
-            for j in range(PACK):
-                nc.tensor.matmul(
-                    out=bank[:, j, :, cols], lhsT=messages[n][:, j, :], rhs=weights[:, n, :].rearrange("q (i j) -> q i j", j=B_COLS),
-                    start=True, stop=True,
-                )
+        def bank_of(n):
+            strip, bc = blocks[n]
+            i = strips[strip].index(bc)
+            mates = strips[strip][4 * (i // 4) : 4 * (i // 4) + 4]
+            return (strip, i // 4), i % 4, mates
 
-        def collect_quad(m):
-            strip, half = divmod(m, 2)
-            rows = slice(B_ROWS * (strip % 4), B_ROWS * (strip % 4 + 1))
-            cols = slice(24 * half, 24 * (half + 1))
-            nc.scalar.copy(
-                out=agg_out[:, strip // 4].rearrange("p (r w) j -> p r w j", w=SIDE)[:, rows, cols, :],
-                in_=main_bank[m][:].rearrange("p j r w -> p r w j"),
+        def aggregate_part(n, j):
+            key, place, mates = bank_of(n)
+            if place == 0 and j == 0:
+                main_bank[key] = psum_main.tile([P, PACK, B_ROWS, 4 * B_COLS], F32, name="main_bank")
+            strip, bc = blocks[n]
+            nc.tensor.matmul(
+                out=main_bank[key][:, j, :, B_COLS * place : B_COLS * (place + 1)], lhsT=messages[n][:, j, :],
+                rhs=weights[:, PER_STRIP * strip + bc, :].rearrange("q (i j) -> q i j", j=B_COLS), start=True, stop=True,
             )
 
-        def messages_of_neighbours(bank, b, t, di):
-            col = P * t + SIDE * (di + R)
-            v = (col // PLANE_STEP) % PLANE_COPIES
-            plane_col = col - PLANE_STEP * v
-            nc.tensor.matmul_mx(
-                out=bank[:],
-                lhsT=codes[b][:, col : col + P].bitcast(FP8X4), lhsT_scale=planes[b][:, v, plane_col : plane_col + P],
-                rhs=feat_codes[:].bitcast(FP8X4), rhs_scale=feat_plane[:], start=True, stop=True,
-            )
+        rows_of_agg = agg_img[:].rearrange("p (r w) j -> p r w j", w=SIDE)
 
-        def weight(t, di, dj):
-            if di == 0 and dj == 0:
-                return 1.0
-            g, j = group_and_place(di, dj)
-            return e_mid[:, t, GROUP * g + j : GROUP * g + j + 1]
-
-        def add_on_vector(b, t, di, dj, is_first):
-            bank = psum_turns.tile([P, C], F32, name="bank_v", tag="bank")
-            messages_of_neighbours(bank, b, t, di)
-            if is_first:
-                nc.vector.tensor_scalar_mul(out=acc[t][:], in0=bank[:], scalar1=weight(t, di, dj))
-            else:
-                nc.vector.scalar_tensor_tensor(
-                    out=acc[t][:], in0=bank[:], scalar=weight(t, di, dj), in1=acc[t][:], op0=ALU.mult, op1=ALU.add
+        def collect_bank(key, mates):
+            rows = slice(B_ROWS * key[0], B_ROWS * (key[0] + 1))
+            runs = []
+            for place, bc in enumerate(mates):
+                if runs and runs[-1][1] + runs[-1][2] == bc:
+                    runs[-1][2] += 1
+                else:
+                    runs.append([place, bc, 1])
+            for place, bc, n in runs:
+                nc.scalar.copy(
+                    out=rows_of_agg[:, rows, B_COLS * bc : B_COLS * (bc + n), :],
+                    in_=main_bank[key][:, :, :, B_COLS * place : B_COLS * (place + n)].rearrange("p j r w -> p r w j"),
                 )
-
-        def add_on_gpsimd(b, t, di, dj, is_first):
-            bank = psum_s.tile([P, C], F32, name="bank_s")
-            messages_of_neighbours(bank, b, t, di)
-            if is_first:
-                nc.scalar.activation(out=acc[t][:], in_=bank[:], func=ACT.Copy, scale=weight(t, di, dj))
-            else:
-                product = product_pool.tile([P, C], F32, name="product")
-                nc.scalar.activation(out=product[:], in_=bank[:], func=ACT.Copy, scale=weight(t, di, dj))
-                nc.gpsimd.tensor_tensor(out=acc[t][:], in0=acc[t][:], in1=product[:], op=ALU.add)
 
         agg = {}
         turned = {}
-        grouped_agg = {}
         agg_mx = {}
         refined = {}
 
@@ -464,21 +574,19 @@ def tile_dcblock_kernel(
             for j in range(PACK):
                 nc.tensor.transpose(out=turned[t][:, j, :], in_=agg[t][:, j, :], identity=ident_bf16[:])
 
-        def regroup_agg(t):
-            tile = late_work.tile([P, P, PACK], BF16, name="agg_grouped", align_bytes=64)
-            nc.scalar.copy(out=tile[:], in_=turned[t][:].rearrange("q j m -> q m j"))
-            grouped_agg[TILES + t] = tile[:]
+        def place_core(t):
+            rows = slice(CORE_ROW + TILE_ROWS * t, CORE_ROW + TILE_ROWS * (t + 1))
+            nc.scalar.copy(
+                out=rows_of_agg[:, rows, CORE_COL : CORE_COL + CORE_USED, :],
+                in_=turned[t][:].rearrange("q j (r w) -> q r w j", w=CORE_COLS)[:, :, 0:CORE_USED, :],
+            )
 
         def quantise_agg(t):
             agg_codes = late_work.tile([P, P], U32, name="agg_codes", align_bytes=64)
             agg_plane = late_work.tile([P, P], U8, name="agg_plane", align_bytes=64)
-            if TILES <= t < 2 * TILES:
-                source = grouped_agg[t]
-            else:
-                m = t % TILES
-                source = agg_out[:, t // (2 * TILES), P * m : P * (m + 1), :]
             nc.vector.quantize_mx(
-                out=agg_codes[:].bitcast(FP8X4), scales=agg_plane[:], in_=source.rearrange("q m j -> q (m j)")
+                out=agg_codes[:].bitcast(FP8X4), scales=agg_plane[:],
+                in_=agg_img[:, P * t : P * (t + 1), :].rearrange("q m j -> q (m j)"),
             )
             agg_mx[t] = (agg_codes, agg_plane)
 
@@ -498,103 +606,88 @@ def tile_dcblock_kernel(
             nc.vector.tensor_tensor(out=result[:], in0=refined[t][:], in1=x_res[:, :, pixels], op=ALU.add)
             nc.sync.dma_start(out=out_by_tile[:, :, pixels], in_=result[:])
 
-        later_groups = {0: (4, nc.gpsimd), 2: (5, nc.vector), 4: (6, nc.gpsimd), 6: (7, nc.vector)}
-        spread_step = 11
-        first_block_step = 13
-        blocks_per_step = 2
-        n_block = 0
-        n_aggregated = 0
-        quads_to_collect = []
         stage_queue = {}
 
         def plan(step, stage, t):
             stage_queue.setdefault(step, []).append((stage, t))
 
-        tail = 3 + 5 + TILES
-        with tc.manual_schedule():
-            nc.gpsimd.memset(spread[:], 0.0)
-            for step in range(STEPS + tail):
-                adding = step < STEPS
-                phase, k = divmod(step, KW)
-                dj, di = phase - R, k - R
-                b = phase % 2
+        def plan_finish(step, tiles):
+            for place, t in enumerate(tiles):
+                plan(step + place, quantise_agg, t)
+                plan(step + 1 + place, fuse, t)
+                plan(step + 2 + place, add_x_and_store, t)
 
-                if step == 1:
-                    fuse_codes, fuse_plane = load_weight(w_fuse_words, w_fuse_scales, "fuse")
-                    x_res = late.tile([P, C // P, NPX], BF16, name="x_res")
-                    nc.sync.dma_start(out=x_res[:], in_=x[0].rearrange("(m p) h w -> p m (h w)", p=P))
-                if step in later_groups:
-                    i, engine = later_groups[step]
-                    subtract(engine, i)
-                if step - 2 in later_groups:
-                    i = later_groups[step - 2][0]
-                    square_diff(i)
-                if step - 3 in later_groups:
-                    exps(later_groups[step - 3][0])
-                if step == spread_step - 1:
-                    softmax_out()
-                    nc.vector.tensor_reduce(out=inv_sum[:], in_=e_mid[:], axis=AXIS.X, op=ALU.add)
+        for t in range(CORE_TILES):
+            plan(STEPS + t, normalise, t)
+            plan(STEPS + t + 1, turn, t)
+            plan(STEPS + t + 2, place_core, t)
+        plan_finish(STEPS + 3, (6,))
+        plan_finish(STEPS + 4, (7, 8))
+        plan_finish(STEPS + 6, (9, 10, 11))
+
+        nc.sync.dma_start(out=x_res[:], in_=x[0].rearrange("(m p) h w -> p m (h w)", p=P))
+        n_block = 0
+        n_aggregated = 0
+        n_gathered = 0
+        to_collect = []
+        with tc.manual_schedule():
+            for step in range(PART_ONE, STEPS + 11):
+                if step == PART_ONE:
+                    spread_class()
+                    nc.vector.tensor_reduce(out=inv_sum[:], in_=e_core[:], axis=AXIS.X, op=ALU.add)
                     nc.vector.tensor_scalar_add(out=inv_sum[:], in0=inv_sum[:], scalar1=1.0)
                     nc.vector.reciprocal(out=inv_sum[:], in_=inv_sum[:])
-                if step == spread_step:
-                    for h in range(2):
-                        for half_row in range(HALF_ROWS):
-                            spread_out(h, half_row)
-
-                if adding and phase < KW - 1 and k == 4:
-                    move_codes(dj + 1, 1 - b)
-                if adding and phase < KW - 1 and k == 5:
-                    move_planes(1 - b)
-                for strip in range(STRIPS):
-                    if step == first_block_step - 2 + strip * B_PER_STRIP // blocks_per_step:
-                        gather_strip(strip)
+                if step < STEPS:
+                    next_codes(step)
 
                 for stage, t in stage_queue.get(step, []):
-                    if stage in (add_x_and_store, quantise_agg, regroup_agg, normalise):
+                    if stage in (add_x_and_store, quantise_agg, place_core, normalise):
                         stage(t)
 
-                if adding:
-                    is_first = step == 0
-                    for place in range(V_TILES):
-                        add_on_vector(b, place, di, dj, is_first)
-                        if V_TILES + place < TILES:
-                            add_on_gpsimd(b, V_TILES + place, di, dj, is_first)
+                for key, mates in to_collect:
+                    collect_bank(key, mates)
+                    strip = key[0]
+                    in_core = len(strips[strip]) < PER_STRIP
+                    if not in_core and mates[-1] == PER_STRIP - 1:
+                        base = 3 * (strip // 2)
+                        plan_finish(step + 1, (base,) if strip % 2 == 0 else (base + 1, base + 2))
 
-                for m in quads_to_collect:
-                    collect_quad(m)
-                    strip, half = divmod(m, 2)
-                    if half == 1:
-                        base = 2 * TILES * (strip // 4) + 3 * (strip % 4 // 2)
-                        for place, tile in enumerate((base,) if strip % 2 == 0 else (base + 1, base + 2)):
-                            plan(step + 1 + place, quantise_agg, tile)
-                            plan(step + 2 + place, fuse, tile)
-                            plan(step + 3 + place, add_x_and_store, tile)
-                quads_to_collect = []
-                done = n_block
-                if step >= first_block_step:
-                    for i in range(blocks_per_step):
-                        if n_block < BLOCKS:
-                            make_messages(n_block)
-                            n_block += 1
-                while n_aggregated < done:
-                    aggregate(n_aggregated)
-                    n_aggregated += 1
-                    if n_aggregated % 4 == 0:
-                        quads_to_collect.append(n_aggregated // 4 - 1)
+                parts = []
+                ready = []
+                if step >= FIRST_SUM_STEP:
+                    while n_aggregated < n_block:
+                        for j in range(PACK):
+                            parts.append((n_aggregated, j))
+                        key, place, mates = bank_of(n_aggregated)
+                        if place == len(mates) - 1:
+                            ready.append((key, mates))
+                        n_aggregated += 1
 
-                if step - 2 in later_groups:
-                    sum_channels(later_groups[step - 2][0])
-                if step == spread_step:
-                    for bank_no in range(3):
-                        turn_out(bank_no)
+                to_collect = ready
+
+                def some_parts(parts, count):
+                    for n, j in parts[0:count]:
+                        aggregate_part(n, j)
+                    parts[0:count] = []
+
+                if step < STEPS:
+                    add_products(step, lambda count: some_parts(parts, count))
+
+                if step >= FIRST_BLOCK_STEP:
+                    goal = min(len(blocks), -(-len(blocks) * (step + 1 - FIRST_BLOCK_STEP) // (STEPS - 1 - FIRST_BLOCK_STEP)))
+                    while n_block < goal:
+                        while n_gathered < min(STRIPS, blocks[n_block][0] + 2):
+                            gather_strip(n_gathered)
+                            n_gathered += 1
+                        make_messages(n_block)
+                        some_parts(parts, 2)
+                        n_block += 1
+                some_parts(parts, len(parts))
+
+                if step == PART_ONE:
+                    for q in range(B_PX // 4):
+                        turn_class(q)
+                        collect_class(nc.scalar.copy if q % 2 == 0 else nc.vector.tensor_copy, q)
                 for stage, t in stage_queue.get(step, []):
                     if stage in (fuse, turn):
                         stage(t)
-                if step == STEPS - 1:
-                    for t in range(TILES):
-                        plan(STEPS + t, normalise, t)
-                        plan(STEPS + t + 1, turn, t)
-                        plan(STEPS + t + 2, regroup_agg, t)
-                        plan(STEPS + t + 3, quantise_agg, TILES + t)
-                        plan(STEPS + t + 4, fuse, TILES + t)
-                        plan(STEPS + t + 5, add_x_and_store, TILES + t)

@@ -46,6 +46,12 @@ Q_PX = Q_ROWS * Q_COLS
 STRIPS = SIDE // B_ROWS
 PER_STRIP = SIDE // B_COLS
 LANES = STRIPS * PER_STRIP
+INNER = 6
+INNER_LANES = (STRIPS - 2) * INNER
+SIDES = ("top", "bottom", "left", "right")
+PAIR_ROWS, PAIR_COLS = B_ROWS + R, 2 * B_COLS + 2 * R
+EDGE_COLS = B_COLS + R
+TOP_LANE, BOTTOM_LANE, LEFT_LANE, RIGHT_LANE = 60, 68, 76, 86
 
 SETS = 4
 D = 6
@@ -67,10 +73,12 @@ STORE_ROWS = 32
 BLOCK_ROWS = STORE_ROWS * D
 PARK_PITCH = 3072
 
-PART_ONE = 10
-FIRST_BLOCK_STEP = 10
-FIRST_SUM_STEP = 12
-FIRST_GPSIMD_STEP = 6
+TURNS = [(0, q) for q in range(1, 7)] + [(1, q) for q in range(7)]
+PART_ONE = 8
+FIRST_BLOCK_STEP = 8
+FIRST_SUM_STEP = 10
+FIRST_GPSIMD_STEP = 2
+LAST_BLOCK_STEP = 46
 
 FLOPS = 2 * 2 * C * C * NPX + 2 * KW * KW * C * NPX
 
@@ -123,9 +131,16 @@ def tile_dcblock_kernel(
         dist_class = keep.tile([P, B_PX, 2 * SETS * D], F32, name="dist_class")
         e_class = keep.tile([P, B_PX, 8, 8], F32, name="e_class")
         inv_class = keep.tile([P, B_PX], F32, name="inv_class")
-        spread = keep.tile([P, B_PX, P], F32, name="spread")
+        spread = keep.tile([P, 30 * P], F32, name="spread")
+        mask = keep.tile([P, 9], F32, name="mask")
         nc.vector.memset(e_class[:, :, R, R], 1.0)
-        nc.gpsimd.memset(spread[:], 0.0)
+        nc.gpsimd.memset(spread[:, 0 : B_PX * P], 0.0)
+        kinds = [(0, INNER_LANES, 1)]
+        for lane, n in ((TOP_LANE, PER_STRIP), (BOTTOM_LANE, PER_STRIP), (LEFT_LANE, STRIPS - 2), (RIGHT_LANE, STRIPS - 2)):
+            for member in range(2):
+                kinds.append((lane + member, lane + n, 2))
+        for m, (lane, end, hop) in enumerate(kinds):
+            nc.vector.tensor_reduce(out=mask[:, m : m + 1], in_=ident_f32[:, lane:end:hop], axis=AXIS.X, op=ALU.add)
 
         def load_weight(words, scales, label):
             w_codes = keep.tile([P, C], U32, name=label + "_codes", align_bytes=64)
@@ -197,15 +212,15 @@ def tile_dcblock_kernel(
             nc.scalar.activation(out=product[:], in_=bank[:], func=ACT.Copy, scale=weight(t, di, dj))
             nc.gpsimd.tensor_tensor(out=acc[t][:], in0=acc[t][:], in1=product[:], op=ALU.add)
 
-        def add_products(step, between=None):
+        def product_calls(step):
             phase, k = divmod(step, KW)
+            on_vector, on_scalar = [], []
             for t in range(CORE_TILES):
                 if t == CORE_TILES - 1 and step >= FIRST_GPSIMD_STEP:
-                    add_on_gpsimd(phase % 2, t, k - R, phase - R)
+                    on_scalar.append(lambda t=t: add_on_gpsimd(phase % 2, t, k - R, phase - R))
                 else:
-                    add_on_vector(phase % 2, t, k - R, phase - R, step == 0)
-                if between is not None:
-                    between(1)
+                    on_vector.append(lambda t=t: add_on_vector(phase % 2, t, k - R, phase - R, step == 0))
+            return on_vector, on_scalar
 
         pools = {}
         with ExitStack() as ctx_one:
@@ -249,12 +264,24 @@ def tile_dcblock_kernel(
                     rows = t[:].rearrange("p (b i w) -> p b i w", i=B_ROWS, w=PAD_PITCH)
                     return rows[:, :, i, 0:SIDE].rearrange("p b (c j) -> p j b c", j=B_COLS)
 
+                def inner_blocks(v):
+                    return v[:, :, 1 : STRIPS - 1, 1 : 1 + INNER]
+
+                def outer_rows(v):
+                    return v[:, :, 0 : STRIPS : STRIPS - 1, :]
+
+                def outer_cols(v):
+                    return v[:, :, 1 : STRIPS - 1, 0 : PER_STRIP : PER_STRIP - 1].rearrange("p j b c -> p j c b")
+
                 for i in range(B_ROWS):
                     first_col = CORE_PX + LANES * B_COLS * i
-                    engine.tensor_tensor(
-                        out=d[:, first_col : first_col + LANES * B_COLS].rearrange("p (j b c) -> p j b c", j=B_COLS, c=PER_STRIP),
-                        in0=class_row(a, i), in1=class_row(c, i), op=ALU.subtract,
-                    )
+                    lanes = d[:, first_col : first_col + LANES * B_COLS].rearrange("p (j l) -> p j l", l=LANES)
+                    for view, lane, width in ((inner_blocks, 0, INNER), (outer_rows, TOP_LANE, PER_STRIP), (outer_cols, LEFT_LANE, STRIPS - 2)):
+                        in0, in1 = view(class_row(a, i)), view(class_row(c, i))
+                        n = in0.shape[2] * in0.shape[3]
+                        engine.tensor_tensor(
+                            out=lanes[:, :, lane : lane + n].rearrange("p j (b c) -> p j b c", c=width), in0=in0, in1=in1, op=ALU.subtract
+                        )
 
             def square_core(u):
                 d = sq[u]
@@ -409,51 +436,51 @@ def tile_dcblock_kernel(
             pools["product"] = ctx_one.enter_context(tc.tile_pool(name="product_one", bufs=4))
             more_squares(ctx_one.enter_context(tc.tile_pool(name="dist_two", bufs=1)), SLICES - 1)
             with tc.manual_schedule():
-                for u in range(SLICES):
-                    subtract_core(nc.vector, u)
-                    if u % 2 == 0:
-                        subtract_class(nc.gpsimd, u)
-                    else:
-                        subtract_class(nc.vector, u)
-                    load_shifted(u + SLICES)
+                subtract_core(nc.vector, 0)
                 square_core(0)
+                subtract_class(nc.gpsimd, 0)
+                load_shifted(4)
+                subtract_core(nc.vector, 1)
                 square_core(1)
-                square_class(0)
-                square_core(2)
+                subtract_class(nc.vector, 1)
                 square_class(1)
-                square_core(3)
+                load_shifted(5)
+                for u in (2, 3):
+                    subtract_core(nc.vector, u)
+                    square_core(u)
+                square_class(0)
                 turn_squares(0, 0)
-                sum_channels(0, 0)
-                square_class(2)
-                exp_core(0)
-                square_class(3)
+                for u in (2, 3):
+                    subtract_class(nc.vector, u)
+                    load_shifted(u + SLICES)
+                    square_class(u)
+                    if u == 2:
+                        sum_channels(0, 0)
+                        exp_core(0)
                 for step in range(PART_ONE):
-                    phase, k = divmod(step, KW)
-                    for u, at, engine in ((4, 0, nc.gpsimd), (5, 0, nc.gpsimd), (6, 1, nc.vector), (7, 3, nc.vector)):
+                    for u, at, engine in ((4, 0, nc.gpsimd), (5, 0, nc.vector), (6, 0, nc.gpsimd), (7, 1, nc.vector)):
                         if step == at:
                             subtract_core(engine, u)
                             subtract_class(engine, u)
-                    for q in range(B_PX // 4 + 1):
-                        if q > 0 and step == q:
-                            sum_channels(0, q)
-                        if step == 6 + q // 2:
-                            sum_channels(1, q)
-                    if step == 7:
-                        exp_core(1)
-                        exp_class(0)
-                    if step == 9:
-                        exp_class(1)
-                    for u, at in ((4, 2), (6, 2), (7, 4), (5, 4)):
+                    for u, at in ((4, 0), (5, 0), (7, 1), (6, 1)):
                         if step == at:
                             square_core(u)
                             square_class(u)
+                    if step > 0:
+                        for half, q in TURNS[2 * step - 2 : 2 * step]:
+                            sum_channels(half, q)
+                    if step == 3:
+                        exp_class(0)
+                    if step == 5:
+                        exp_core(1)
+                    if step == 7:
+                        exp_class(1)
                     next_codes(step)
-                    add_products(step)
-                    for q in range(B_PX // 4 + 1):
-                        if q > 0 and step == q - 1:
-                            turn_squares(0, q)
-                        if step == 5 + q // 2:
-                            turn_squares(1, q)
+                    on_vector, on_scalar = product_calls(step)
+                    for call in on_vector + on_scalar:
+                        call()
+                    for half, q in TURNS[2 * step : 2 * step + 2]:
+                        turn_squares(half, q)
             fuse_codes, fuse_plane = load_weight(w_fuse_words, w_fuse_scales, "fuse")
 
         late = ctx.enter_context(tc.tile_pool(name="late", bufs=1))
@@ -462,101 +489,224 @@ def tile_dcblock_kernel(
         message_pool = ctx.enter_context(tc.tile_pool(name="message_pool", bufs=8))
         out_by_tile = out[0].rearrange("(m p) h w -> p m (h w)", p=P)
         weights = late.tile([P, LANES, B_PX], F32, name="weights")
+        edge_codes, edge_plane = [], []
+        for side in range(4):
+            n = 4 if side < 2 else 5
+            edge_codes.append(late.tile([P, n, P], U32, name="edge_codes%d" % side, align_bytes=64))
+            edge_plane.append(late.tile([P, n, P], U8, name="edge_plane%d" % side, align_bytes=64))
+            nc.vector.memset(edge_codes[side][:, :, PAIR_ROWS * PAIR_COLS : P], 0)
+            nc.vector.memset(edge_plane[side][:].bitcast(I32), 0)
         agg_img = late.tile([P, NPX, PACK], BF16, name="agg_img", align_bytes=64)
         x_res = late.tile([P, C // P, NPX], BF16, name="x_res")
 
-        def spread_class():
-            seven = e_class[:, :, 0:KW, 0:KW]
+        seven = e_class[:, :, 0:KW, 0:KW]
+
+        def windows(base, hop, n, pitch, rows, cols):
+            view = spread[:, base : base + n * hop].rearrange("p (n f) -> p n f", f=hop)[:, :, 0 : pitch * rows]
+            return view.rearrange("p n (r c) -> p n r c", c=pitch)[:, :, :, 0:cols]
+
+        def spread_inner():
             nc.vector.tensor_reduce(out=inv_class[:], in_=seven, axis=AXIS.XY, op=ALU.add)
             nc.vector.reciprocal(out=inv_class[:], in_=inv_class[:])
-            for k in range(B_PX):
-                i, j = divmod(k, B_COLS)
-                window = spread[:, k, 0:Q_PX].rearrange("p (r c) -> p r c", c=Q_COLS)
+            nc.vector.tensor_tensor(
+                out=seven, in0=seven, in1=inv_class[:].unsqueeze(2).unsqueeze(3).to_broadcast([P, B_PX, KW, KW]), op=ALU.mult
+            )
+            for i in range(B_ROWS):
                 nc.vector.tensor_scalar_mul(
-                    out=window[:, i : i + KW, j : j + KW], in0=seven[:, k], scalar1=inv_class[:, k : k + 1]
+                    out=windows(B_COLS * P * i + Q_COLS * i, P + 1, B_COLS, Q_COLS, KW, KW),
+                    in0=seven[:, B_COLS * i : B_COLS * (i + 1)], scalar1=mask[:, 0:1],
                 )
+
+        masked_e = {}
+
+        def mask_edge(kind):
+            masked_e[kind] = late_work.tile([P, B_PX, KW, KW], F32, name="masked_e")
+            nc.scalar.activation(out=masked_e[kind][:], in_=seven, func=ACT.Copy, scale=mask[:, kind : kind + 1])
+
+        def spread_edge(kind):
+            side, member = divmod(kind - 1, 2)
+            masked = masked_e[kind]
+            calls = []
+            if side < 2:
+                for i in range(B_ROWS):
+                    rows = slice(R - i, KW) if side == 0 else slice(0, KW - i)
+                    row0 = 0 if side == 0 else i
+                    calls.append((
+                        windows(B_COLS * P * i + PAIR_COLS * row0 + B_COLS * member, P + 1, B_COLS, PAIR_COLS, rows.stop - rows.start, KW),
+                        masked[:, B_COLS * i : B_COLS * (i + 1), rows, :],
+                    ))
+            else:
+                for j in range(B_COLS):
+                    cols = slice(max(0, R - j), KW) if side == 2 else slice(0, min(KW, EDGE_COLS - j))
+                    col0 = max(0, j - R) if side == 2 else j
+                    calls.append((
+                        windows(P * j + EDGE_COLS * B_ROWS * member + col0, B_COLS * P + EDGE_COLS, B_ROWS, EDGE_COLS, KW, cols.stop - cols.start),
+                        masked[:, j : B_PX : B_COLS, :, cols],
+                    ))
+            for place, e in calls:
+                nc.vector.tensor_tensor(out=place, in0=place, in1=e, op=ALU.add)
 
         turned_class = {}
 
         def turn_class(q):
             turned_class[q] = psum_turns.tile([P, 4, P], F32, name="turned_class", tag="bank")
             for m in range(4):
-                nc.tensor.transpose(out=turned_class[q][:, m, :], in_=spread[:, 4 * q + m, :], identity=ident_f32[:])
+                nc.tensor.transpose(out=turned_class[q][:, m, :], in_=spread[:, P * (4 * q + m) : P * (4 * q + m + 1)], identity=ident_f32[:])
 
-        def collect_class(engine_copy, q):
+        def collect_class(engine_copy, q, lanes):
             engine_copy(
-                out=weights[:, :, 4 * q : 4 * q + 4], in_=turned_class[q][:].rearrange("q m b -> q b m")[:, 0:LANES, :]
+                out=weights[:, lanes, 4 * q : 4 * q + 4], in_=turned_class[q][:].rearrange("q m b -> q b m")[:, lanes, :]
             )
 
-        strips = []
-        for strip in range(STRIPS):
-            row = B_ROWS * strip
-            in_core = CORE_ROW <= row < CORE_ROW + CORE_ROWS
-            taken = range(CORE_COL // B_COLS, (CORE_COL + CORE_USED) // B_COLS) if in_core else ()
-            strips.append([bc for bc in range(PER_STRIP) if bc not in taken])
-        blocks = [(strip, bc) for strip in range(STRIPS) for bc in strips[strip]]
+        def turn_and_collect(lanes):
+            for q in range(B_PX // 4):
+                turn_class(q)
+                collect_class(nc.scalar.copy if q % 2 == 0 else nc.vector.tensor_copy, q, lanes)
+
+        gathered = {}
+
+        def gather(dst_codes, dst_plane, dst_view, source_view):
+            for dst, source, dtype in ((dst_codes, codes_img, I32), (dst_plane, plane_img, U8)):
+                rows = source[:, 0 : PITCH * PITCH].bitcast(dtype).rearrange("p (r w) -> p r w", w=PITCH)
+                nc.vector.tensor_copy(out=dst_view(dst[:].bitcast(dtype)), in_=source_view(rows))
 
         def gather_strip(strip):
-            b = strip % 2
-            start = B_ROWS * strip * PITCH
-            rows = slice(start, start + Q_ROWS * PITCH)
+            slot = strip % 2
+            row = B_ROWS * strip
             for half in range(2):
-                cols = slice(B_COLS * half, B_COLS * half + SIDE)
-                for dst, source, dtype in ((q_codes[b], codes_img, I32), (q_plane[b], plane_img, U8)):
-                    nc.vector.tensor_copy(
-                        out=dst[:, :, 0:Q_PX].bitcast(dtype).rearrange("p b (r c) -> p b r c", c=Q_COLS)[
-                            :, :, :, B_COLS * half : B_COLS * (half + 1)
+                col = B_COLS * (1 + half)
+                gather(
+                    q_codes[slot], q_plane[slot],
+                    lambda t: t[:, 0:INNER, 0:Q_PX].rearrange("p b (r c) -> p b r c", c=Q_COLS)[:, :, :, B_COLS * half : B_COLS * (half + 1)],
+                    lambda v: v[:, row : row + Q_ROWS, col : col + B_COLS * INNER].rearrange("p r (b c) -> p b r c", c=B_COLS),
+                )
+            for bc in range(1, 1 + INNER):
+                gathered[strip, bc] = (q_codes[slot][:, bc - 1, :], q_plane[slot][:, bc - 1, :])
+
+        def gather_one(strip, bc):
+            slot = strip % 2
+            row, col = B_ROWS * strip, B_COLS * bc
+            gather(
+                q_codes[slot], q_plane[slot],
+                lambda t: t[:, strip // 2, 0:Q_PX].rearrange("p (r c) -> p r c", c=Q_COLS),
+                lambda v: v[:, row : row + Q_ROWS, col : col + Q_COLS],
+            )
+            gathered[strip, bc] = (q_codes[slot][:, strip // 2, :], q_plane[slot][:, strip // 2, :])
+
+        def gather_side(side):
+            if side < 2:
+                row = R if side == 0 else R + SIDE - PAIR_ROWS
+                for third in range(3):
+                    col = B_COLS * third
+                    start = min(col, B_COLS)
+                    gather(
+                        edge_codes[side], edge_plane[side],
+                        lambda t: t[:, 0:4, 0 : PAIR_ROWS * PAIR_COLS].rearrange("p b (r c) -> p b r c", c=PAIR_COLS)[
+                            :, :, :, col : col + B_COLS
                         ],
-                        in_=source[:, rows].bitcast(dtype).rearrange("p (r w) -> p r w", w=PITCH)[:, :, cols].rearrange(
-                            "p r (b c) -> p b r c", c=B_COLS
-                        ),
+                        lambda v: v[:, row : row + PAIR_ROWS, start : start + SIDE].rearrange("p r (b c) -> p b r c", c=2 * B_COLS)[
+                            :, :, :, col - start : col - start + B_COLS
+                        ],
                     )
+            else:
+                col = R if side == 2 else R + SIDE - EDGE_COLS
+                for first_row, n in ((0, 8), (8, 6)):
+                    row = B_ROWS + first_row
+                    gather(
+                        edge_codes[side], edge_plane[side],
+                        lambda t: t[:, 0:5, EDGE_COLS * first_row : EDGE_COLS * (first_row + n)].rearrange("p b (r c) -> p b r c", c=EDGE_COLS),
+                        lambda v: v[:, row : row + 40, col : col + EDGE_COLS].rearrange("p (b r) c -> p b r c", r=8)[:, :, 0:n, :],
+                    )
+            for m in range(4 if side < 2 else 5):
+                gathered[SIDES[side], m] = (edge_codes[side][:, m, :], edge_plane[side][:, m, :])
+
+        def inner_banks(strip):
+            return [
+                ("wide", B_ROWS * strip, B_COLS * bc, [((strip, b), INNER * (strip - 1) + b - 1, 1) for b in range(bc, bc + 3)])
+                for bc in (1, 4)
+            ]
+
+        def row_banks(side):
+            lane = TOP_LANE if side == 0 else BOTTOM_LANE
+            row = 0 if side == 0 else SIDE - B_ROWS
+            return [
+                ("wide", row, 4 * B_COLS * h, [((SIDES[side], m), lane + 2 * m, 2) for m in (2 * h, 2 * h + 1)]) for h in range(2)
+            ]
+
+        def col_bank(side, pairs):
+            lane = LEFT_LANE if side == 2 else RIGHT_LANE
+            col = 0 if side == 2 else SIDE - B_COLS
+            return ("tall", B_ROWS + 2 * B_ROWS * pairs[0], col, [((SIDES[side], m), lane + 2 * m, 2) for m in pairs])
+
+        core_end = CORE_COL + CORE_USED
+        leftover = ("tall", CORE_ROW, core_end, [((st, core_end // B_COLS), INNER * (st - 1) + core_end // B_COLS - 1, 1) for st in range(4, 8)])
+        bank_list = []
+        for strip in (1, 2, 3):
+            bank_list += inner_banks(strip)
+        bank_list += row_banks(0) + [col_bank(2, (0, 1)), col_bank(3, (0, 1))]
+        after_bank = {len(bank_list) - 1: range(0, 6)}
+        for strip in (8, 9, 10):
+            bank_list += inner_banks(strip)
+        bank_list += row_banks(1) + [col_bank(2, (3, 4)), col_bank(3, (3, 4))]
+        after_bank[len(bank_list) - 1] = range(12, 18)
+        bank_list += [col_bank(2, (2,)), col_bank(3, (2,)), leftover]
+        blocks = [(m, place) for m in range(len(bank_list)) for place in range(len(bank_list[m][3]))]
+
+        def gather_for(n):
+            name = bank_list[blocks[n][0]][3][blocks[n][1]][0]
+            if name not in gathered:
+                if name[0] in SIDES:
+                    gather_side(SIDES.index(name[0]))
+                elif 4 <= name[0] < 8:
+                    gather_one(name[0], name[1])
+                else:
+                    gather_strip(name[0])
 
         messages = {}
         main_bank = {}
 
         def make_messages(n):
-            strip, bc = blocks[n]
+            m, place = blocks[n]
+            q, plane = gathered[bank_list[m][3][place][0]]
             bank = psum_s.tile([P, C], F32, name="bank_s")
             nc.tensor.matmul_mx(
-                out=bank[:],
-                lhsT=q_codes[strip % 2][:, bc, :].bitcast(FP8X4), lhsT_scale=q_plane[strip % 2][:, bc, :],
+                out=bank[:], lhsT=q.bitcast(FP8X4), lhsT_scale=plane,
                 rhs=feat_codes[:].bitcast(FP8X4), rhs_scale=feat_plane[:], start=True, stop=True,
             )
             messages[n] = message_pool.tile([P, PACK, P], F32, name="messages")
             nc.scalar.copy(out=messages[n][:], in_=bank[:].rearrange("p (q j) -> p j q", j=PACK))
 
-        def bank_of(n):
-            strip, bc = blocks[n]
-            i = strips[strip].index(bc)
-            mates = strips[strip][4 * (i // 4) : 4 * (i // 4) + 4]
-            return (strip, i // 4), i % 4, mates
-
         def aggregate_part(n, j):
-            key, place, mates = bank_of(n)
+            m, place = blocks[n]
+            shape, row, col, members = bank_list[m]
+            name, lane, count = members[place]
             if place == 0 and j == 0:
-                main_bank[key] = psum_main.tile([P, PACK, B_ROWS, 4 * B_COLS], F32, name="main_bank")
-            strip, bc = blocks[n]
-            nc.tensor.matmul(
-                out=main_bank[key][:, j, :, B_COLS * place : B_COLS * (place + 1)], lhsT=messages[n][:, j, :],
-                rhs=weights[:, PER_STRIP * strip + bc, :].rearrange("q (i j) -> q i j", j=B_COLS), start=True, stop=True,
-            )
+                main_bank[m] = psum_main.tile([P, PACK, 96], F32, name="main_bank")
+            px = count * B_PX
+            bank = main_bank[m][:, j, 0 : px * len(members)]
+            rhs = weights[:, lane : lane + count, :]
+            if shape == "tall":
+                dst = bank[:, px * place : px * (place + 1)]
+                rhs = rhs.rearrange("q l k -> q (l k)")
+            else:
+                width = B_COLS * count
+                dst = bank.rearrange("p (i w) -> p i w", i=B_ROWS)[:, :, width * place : width * (place + 1)].rearrange(
+                    "p i (l j) -> p l i j", j=B_COLS
+                )
+                rhs = rhs.rearrange("q l (i j) -> q l i j", j=B_COLS)
+            nc.tensor.matmul(out=dst, lhsT=messages[n][:, j, :], rhs=rhs, start=True, stop=True)
 
         rows_of_agg = agg_img[:].rearrange("p (r w) j -> p r w j", w=SIDE)
 
-        def collect_bank(key, mates):
-            rows = slice(B_ROWS * key[0], B_ROWS * (key[0] + 1))
-            runs = []
-            for place, bc in enumerate(mates):
-                if runs and runs[-1][1] + runs[-1][2] == bc:
-                    runs[-1][2] += 1
-                else:
-                    runs.append([place, bc, 1])
-            for place, bc, n in runs:
-                nc.scalar.copy(
-                    out=rows_of_agg[:, rows, B_COLS * bc : B_COLS * (bc + n), :],
-                    in_=main_bank[key][:, :, :, B_COLS * place : B_COLS * (place + n)].rearrange("p j r w -> p r w j"),
-                )
+        def collect_bank(m):
+            shape, row, col, members = bank_list[m]
+            px = sum([count for name, lane, count in members]) * B_PX
+            n_rows = B_ROWS if shape == "wide" else px // B_COLS
+            width = px // n_rows
+            nc.scalar.copy(
+                out=rows_of_agg[:, row : row + n_rows, col : col + width, :],
+                in_=main_bank[m][:, :, 0:px].rearrange("p j (r w) -> p r w j", w=width),
+            )
 
         agg = {}
         turned = {}
@@ -628,15 +778,19 @@ def tile_dcblock_kernel(
         nc.sync.dma_start(out=x_res[:], in_=x[0].rearrange("(m p) h w -> p m (h w)", p=P))
         n_block = 0
         n_aggregated = 0
-        n_gathered = 0
         to_collect = []
         with tc.manual_schedule():
             for step in range(PART_ONE, STEPS + 11):
                 if step == PART_ONE:
-                    spread_class()
+                    spread_inner()
                     nc.vector.tensor_reduce(out=inv_sum[:], in_=e_core[:], axis=AXIS.X, op=ALU.add)
                     nc.vector.tensor_scalar_add(out=inv_sum[:], in0=inv_sum[:], scalar1=1.0)
                     nc.vector.reciprocal(out=inv_sum[:], in_=inv_sum[:])
+                for kind in range(1, 9):
+                    if step == PART_ONE + 1 + kind // 2:
+                        mask_edge(kind)
+                    if step == PART_ONE + 2 + kind // 2:
+                        spread_edge(kind)
                 if step < STEPS:
                     next_codes(step)
 
@@ -644,50 +798,51 @@ def tile_dcblock_kernel(
                     if stage in (add_x_and_store, quantise_agg, place_core, normalise):
                         stage(t)
 
-                for key, mates in to_collect:
-                    collect_bank(key, mates)
-                    strip = key[0]
-                    in_core = len(strips[strip]) < PER_STRIP
-                    if not in_core and mates[-1] == PER_STRIP - 1:
-                        base = 3 * (strip // 2)
-                        plan_finish(step + 1, (base,) if strip % 2 == 0 else (base + 1, base + 2))
+                for m in to_collect:
+                    collect_bank(m)
+                    plan_finish(step + 1, after_bank.get(m, ()))
+                to_collect = []
 
                 parts = []
-                ready = []
                 if step >= FIRST_SUM_STEP:
                     while n_aggregated < n_block:
                         for j in range(PACK):
                             parts.append((n_aggregated, j))
-                        key, place, mates = bank_of(n_aggregated)
-                        if place == len(mates) - 1:
-                            ready.append((key, mates))
+                        m, place = blocks[n_aggregated]
+                        if place == len(bank_list[m][3]) - 1:
+                            to_collect.append(m)
                         n_aggregated += 1
+                first_new = n_block
+                if step >= FIRST_BLOCK_STEP:
+                    span = LAST_BLOCK_STEP - FIRST_BLOCK_STEP
+                    n_block = min(len(blocks), -(-len(blocks) * (step + 1 - FIRST_BLOCK_STEP) // span))
+                for n in range(first_new, min(n_block + 1, len(blocks))):
+                    gather_for(n)
+                n_mx = (CORE_TILES if step < STEPS else 0) + n_block - first_new
+                shares = [len(parts) * (m + 1) // n_mx - len(parts) * m // n_mx for m in range(n_mx)]
 
-                to_collect = ready
-
-                def some_parts(parts, count):
+                def some_parts(parts, shares):
+                    count = shares[0]
                     for n, j in parts[0:count]:
                         aggregate_part(n, j)
                     parts[0:count] = []
+                    shares[0:1] = []
 
-                if step < STEPS:
-                    add_products(step, lambda count: some_parts(parts, count))
-
-                if step >= FIRST_BLOCK_STEP:
-                    goal = min(len(blocks), -(-len(blocks) * (step + 1 - FIRST_BLOCK_STEP) // (STEPS - 1 - FIRST_BLOCK_STEP)))
-                    while n_block < goal:
-                        while n_gathered < min(STRIPS, blocks[n_block][0] + 2):
-                            gather_strip(n_gathered)
-                            n_gathered += 1
-                        make_messages(n_block)
-                        some_parts(parts, 2)
-                        n_block += 1
-                some_parts(parts, len(parts))
+                on_vector, on_scalar = product_calls(step) if step < STEPS else ([], [])
+                for n in range(first_new, n_block):
+                    on_scalar.append(lambda n=n: make_messages(n))
+                for m in range(max(len(on_vector), len(on_scalar))):
+                    for calls in (on_vector, on_scalar):
+                        if m < len(calls):
+                            calls[m]()
+                            some_parts(parts, shares)
+                for n, j in parts:
+                    aggregate_part(n, j)
 
                 if step == PART_ONE:
-                    for q in range(B_PX // 4):
-                        turn_class(q)
-                        collect_class(nc.scalar.copy if q % 2 == 0 else nc.vector.tensor_copy, q)
+                    turn_and_collect(slice(0, INNER_LANES))
+                if step == PART_ONE + 6:
+                    turn_and_collect(slice(INNER_LANES, LANES))
                 for stage, t in stage_queue.get(step, []):
                     if stage in (fuse, turn):
                         stage(t)

@@ -47,11 +47,9 @@ STRIPS = SIDE // B_ROWS
 PER_STRIP = SIDE // B_COLS
 LANES = STRIPS * PER_STRIP
 INNER = 6
-INNER_LANES = (STRIPS - 2) * INNER
 SIDES = ("top", "bottom", "left", "right")
 PAIR_ROWS, PAIR_COLS = B_ROWS + R, 2 * B_COLS + 2 * R
 EDGE_COLS = B_COLS + R
-TOP_LANE, BOTTOM_LANE, LEFT_LANE, RIGHT_LANE = 60, 68, 76, 86
 
 SETS = 4
 D = 6
@@ -77,7 +75,6 @@ TURNS = [(0, q) for q in range(1, 7)] + [(1, q) for q in range(7)]
 PART_ONE = 8
 FIRST_BLOCK_STEP = 8
 FIRST_SUM_STEP = 10
-FIRST_GPSIMD_STEP = 2
 LAST_BLOCK_STEP = 46
 
 FLOPS = 2 * 2 * C * C * NPX + 2 * KW * KW * C * NPX
@@ -107,8 +104,8 @@ def tile_dcblock_kernel(
     nc = tc.nc
     with ExitStack() as ctx:
         keep = ctx.enter_context(tc.tile_pool(name="keep", bufs=1))
-        psum_turns = ctx.enter_context(tc.psum_pool(name="psum_turns", bufs=4))
-        psum_s = ctx.enter_context(tc.psum_pool(name="psum_s", bufs=2))
+        psum_turns = ctx.enter_context(tc.psum_pool(name="psum_turns", bufs=3))
+        psum_s = ctx.enter_context(tc.psum_pool(name="psum_s", bufs=3))
         psum_main = ctx.enter_context(tc.psum_pool(name="psum_main", bufs=2))
 
         ident_f32 = keep.tile([P, P], F32, name="ident_f32")
@@ -124,7 +121,11 @@ def tile_dcblock_kernel(
         planes = [keep.tile([P, 2, MID_COLS], U8, name="planes%d" % b, align_bytes=64) for b in range(2)]
         q_codes = [keep.tile([P, PER_STRIP, P], U32, name="q_codes%d" % b, align_bytes=64) for b in range(2)]
         q_plane = [keep.tile([P, PER_STRIP, P], U8, name="q_plane%d" % b, align_bytes=64) for b in range(2)]
-        acc = [keep.tile([P, C], F32, name="acc%d" % t) for t in range(CORE_TILES)]
+        acc = [keep.tile([P, PACK, P], F32, name="acc%d" % t) for t in range(CORE_TILES)]
+        acc_turned = keep.tile([P, PACK, P], F32, name="acc_turned")
+        inv_spread = keep.tile([P, P], F32, name="inv_spread")
+        ones = keep.tile([P, P], F32, name="ones")
+        nc.gpsimd.memset(ones[:], 1.0)
         dist_core = keep.tile([P, CORE_TILES, 2 * SETS * D], F32, name="dist_core")
         e_core = keep.tile([P, CORE_TILES, 2 * SETS * D], F32, name="e_core")
         inv_sum = keep.tile([P, CORE_TILES], F32, name="inv_sum")
@@ -135,12 +136,16 @@ def tile_dcblock_kernel(
         mask = keep.tile([P, 9], F32, name="mask")
         nc.vector.memset(e_class[:, :, R, R], 1.0)
         nc.gpsimd.memset(spread[:, 0 : B_PX * P], 0.0)
-        kinds = [(0, INNER_LANES, 1)]
-        for lane, n in ((TOP_LANE, PER_STRIP), (BOTTOM_LANE, PER_STRIP), (LEFT_LANE, STRIPS - 2), (RIGHT_LANE, STRIPS - 2)):
+        by_lane = ident_f32[:, 0:LANES].rearrange("p (b c) -> p b c", c=PER_STRIP)
+        kinds = [by_lane[:, 1 : STRIPS - 1, 1 : 1 + INNER]]
+        for strip in (0, STRIPS - 1):
             for member in range(2):
-                kinds.append((lane + member, lane + n, 2))
-        for m, (lane, end, hop) in enumerate(kinds):
-            nc.vector.tensor_reduce(out=mask[:, m : m + 1], in_=ident_f32[:, lane:end:hop], axis=AXIS.X, op=ALU.add)
+                kinds.append(by_lane[:, strip : strip + 1, member:PER_STRIP:2])
+        for bc in (0, PER_STRIP - 1):
+            for member in range(2):
+                kinds.append(by_lane[:, 1 + member : STRIPS - 1 : 2, bc : bc + 1])
+        for m, kind in enumerate(kinds):
+            nc.vector.tensor_reduce(out=mask[:, m : m + 1], in_=kind, axis=AXIS.XY, op=ALU.add)
 
         def load_weight(words, scales, label):
             w_codes = keep.tile([P, C], U32, name=label + "_codes", align_bytes=64)
@@ -174,11 +179,12 @@ def tile_dcblock_kernel(
         def add_on_vector(b, t, di, dj, is_first):
             bank = psum_turns.tile([P, C], F32, name="bank_v", tag="bank")
             messages_of_neighbours(bank, b, t, di)
+            by_place = bank[:].rearrange("p (q j) -> p j q", j=PACK)
             if is_first:
-                nc.vector.tensor_scalar_mul(out=acc[t][:], in0=bank[:], scalar1=weight(t, di, dj))
+                nc.vector.tensor_scalar_mul(out=acc[t][:], in0=by_place, scalar1=weight(t, di, dj))
             else:
                 nc.vector.scalar_tensor_tensor(
-                    out=acc[t][:], in0=bank[:], scalar=weight(t, di, dj), in1=acc[t][:], op0=ALU.mult, op1=ALU.add
+                    out=acc[t][:], in0=by_place, scalar=weight(t, di, dj), in1=acc[t][:], op0=ALU.mult, op1=ALU.add
                 )
 
         def move_codes(dj, b):
@@ -205,24 +211,45 @@ def tile_dcblock_kernel(
             if phase < KW - 1 and k == 5:
                 move_plane((phase + 1) % 2)
 
-        def add_on_gpsimd(b, t, di, dj):
+        products = {}
+        sum_bank = {}
+
+        def multiply_for_tensor(b, phase, di, dj):
+            t = CORE_TILES - 1
             bank = psum_s.tile([P, C], F32, name="bank_s")
             messages_of_neighbours(bank, b, t, di)
-            product = pools["product"].tile([P, C], F32, name="product")
-            nc.scalar.activation(out=product[:], in_=bank[:], func=ACT.Copy, scale=weight(t, di, dj))
-            nc.gpsimd.tensor_tensor(out=acc[t][:], in0=acc[t][:], in1=product[:], op=ALU.add)
+            product = product_pool.tile([P, PACK, P], F32, name="product")
+            nc.scalar.activation(
+                out=product[:], in_=bank[:].rearrange("p (q j) -> p j q", j=PACK), func=ACT.Copy, scale=weight(t, di, dj)
+            )
+            products.setdefault(phase, []).append(product)
+
+        def add_on_tensor(phase):
+            sum_bank[phase] = psum_turns.tile([P, PACK, P], F32, name="sum_bank", tag="bank")
+            n = len(products[phase])
+            for j in range(PACK):
+                for m, product in enumerate(products[phase]):
+                    nc.tensor.matmul(
+                        out=sum_bank[phase][:, j, :], lhsT=product[:, j, :], rhs=ident_f32[:],
+                        is_transpose=True, start=(m == 0), stop=(m == n - 1),
+                    )
+
+        def collect_turned(phase):
+            if phase == 1:
+                nc.vector.tensor_copy(out=acc_turned[:], in_=sum_bank[phase][:])
+            else:
+                nc.vector.tensor_tensor(out=acc_turned[:], in0=sum_bank[phase][:], in1=acc_turned[:], op=ALU.add)
 
         def product_calls(step):
             phase, k = divmod(step, KW)
             on_vector, on_scalar = [], []
             for t in range(CORE_TILES):
-                if t == CORE_TILES - 1 and step >= FIRST_GPSIMD_STEP:
-                    on_scalar.append(lambda t=t: add_on_gpsimd(phase % 2, t, k - R, phase - R))
+                if t == CORE_TILES - 1 and step >= PART_ONE:
+                    on_scalar.append(lambda t=t: multiply_for_tensor(phase % 2, phase, k - R, phase - R))
                 else:
                     on_vector.append(lambda t=t: add_on_vector(phase % 2, t, k - R, phase - R, step == 0))
             return on_vector, on_scalar
 
-        pools = {}
         with ExitStack() as ctx_one:
             dist = ctx_one.enter_context(tc.tile_pool(name="dist", bufs=1))
             centre = [dist.tile([P, ROW_LEN], BF16, name="centre%d" % s) for s in range(SLICES)]
@@ -264,24 +291,12 @@ def tile_dcblock_kernel(
                     rows = t[:].rearrange("p (b i w) -> p b i w", i=B_ROWS, w=PAD_PITCH)
                     return rows[:, :, i, 0:SIDE].rearrange("p b (c j) -> p j b c", j=B_COLS)
 
-                def inner_blocks(v):
-                    return v[:, :, 1 : STRIPS - 1, 1 : 1 + INNER]
-
-                def outer_rows(v):
-                    return v[:, :, 0 : STRIPS : STRIPS - 1, :]
-
-                def outer_cols(v):
-                    return v[:, :, 1 : STRIPS - 1, 0 : PER_STRIP : PER_STRIP - 1].rearrange("p j b c -> p j c b")
-
                 for i in range(B_ROWS):
                     first_col = CORE_PX + LANES * B_COLS * i
-                    lanes = d[:, first_col : first_col + LANES * B_COLS].rearrange("p (j l) -> p j l", l=LANES)
-                    for view, lane, width in ((inner_blocks, 0, INNER), (outer_rows, TOP_LANE, PER_STRIP), (outer_cols, LEFT_LANE, STRIPS - 2)):
-                        in0, in1 = view(class_row(a, i)), view(class_row(c, i))
-                        n = in0.shape[2] * in0.shape[3]
-                        engine.tensor_tensor(
-                            out=lanes[:, :, lane : lane + n].rearrange("p j (b c) -> p j b c", c=width), in0=in0, in1=in1, op=ALU.subtract
-                        )
+                    engine.tensor_tensor(
+                        out=d[:, first_col : first_col + LANES * B_COLS].rearrange("p (j b c) -> p j b c", j=B_COLS, c=PER_STRIP),
+                        in0=class_row(a, i), in1=class_row(c, i), op=ALU.subtract,
+                    )
 
             def square_core(u):
                 d = sq[u]
@@ -294,7 +309,7 @@ def tile_dcblock_kernel(
             banks = {}
 
             def turn_squares(half, q):
-                banks[half, q] = psum_turns.tile([P, 4, P], F32, name="turned_squares", tag="bank")
+                banks[half, q] = psum_main.tile([P, 4, P], F32, name="turned_squares", tag="main")
                 for m in range(4):
                     first_col = P * m if q == 0 else CORE_PX + LANES * (4 * (q - 1) + m)
                     for s in range(SLICES):
@@ -412,10 +427,16 @@ def tile_dcblock_kernel(
                 for third in range(3):
                     px = slice(THIRD_PX * third, THIRD_PX * (third + 1))
                     for j in range(PACK):
-                        nc.vector.tensor_scalar(
-                            out=xn[:, j, px], in0=xn[:, j, px],
-                            scalar1=bn_scale[:, j : j + 1], scalar2=bn_shift[:, j : j + 1], op0=ALU.mult, op1=ALU.add,
-                        )
+                        if j == 0:
+                            nc.scalar.activation(
+                                out=xn[:, j, px], in_=xn[:, j, px], func=ACT.Identity,
+                                scale=bn_scale[:, j : j + 1], bias=bn_shift[:, j : j + 1],
+                            )
+                        else:
+                            nc.vector.tensor_scalar(
+                                out=xn[:, j, px], in0=xn[:, j, px],
+                                scalar1=bn_scale[:, j : j + 1], scalar2=bn_shift[:, j : j + 1], op0=ALU.mult, op1=ALU.add,
+                            )
                 image = grouped[:, top : top + SIDE * PITCH, :].rearrange("p (r w) j -> p r w j", w=PITCH)
                 for chunk in range(SIDE // CHUNK_ROWS):
                     rows = slice(CHUNK_ROWS * chunk, CHUNK_ROWS * (chunk + 1))
@@ -433,22 +454,21 @@ def tile_dcblock_kernel(
                 move_codes(-R, 0)
                 move_plane(0)
 
-            pools["product"] = ctx_one.enter_context(tc.tile_pool(name="product_one", bufs=4))
             more_squares(ctx_one.enter_context(tc.tile_pool(name="dist_two", bufs=1)), SLICES - 1)
             with tc.manual_schedule():
-                subtract_core(nc.vector, 0)
-                square_core(0)
-                subtract_class(nc.gpsimd, 0)
+                for u in (0, 1):
+                    subtract_core(nc.vector, u)
+                    square_core(u)
+                subtract_class(nc.vector, 0)
+                square_class(0)
                 load_shifted(4)
-                subtract_core(nc.vector, 1)
-                square_core(1)
+                subtract_core(nc.vector, 2)
+                square_core(2)
                 subtract_class(nc.vector, 1)
                 square_class(1)
                 load_shifted(5)
-                for u in (2, 3):
-                    subtract_core(nc.vector, u)
-                    square_core(u)
-                square_class(0)
+                subtract_core(nc.vector, 3)
+                square_core(3)
                 turn_squares(0, 0)
                 for u in (2, 3):
                     subtract_class(nc.vector, u)
@@ -458,11 +478,11 @@ def tile_dcblock_kernel(
                         sum_channels(0, 0)
                         exp_core(0)
                 for step in range(PART_ONE):
-                    for u, at, engine in ((4, 0, nc.gpsimd), (5, 0, nc.vector), (6, 0, nc.gpsimd), (7, 1, nc.vector)):
+                    for u, at, engine in ((4, 0, nc.gpsimd), (6, 0, nc.gpsimd), (5, 0, nc.gpsimd), (7, 1, nc.vector)):
                         if step == at:
                             subtract_core(engine, u)
                             subtract_class(engine, u)
-                    for u, at in ((4, 0), (5, 0), (7, 1), (6, 1)):
+                    for u, at in ((4, 0), (7, 1), (6, 1), (5, 2)):
                         if step == at:
                             square_core(u)
                             square_class(u)
@@ -485,7 +505,7 @@ def tile_dcblock_kernel(
 
         late = ctx.enter_context(tc.tile_pool(name="late", bufs=1))
         late_work = ctx.enter_context(tc.tile_pool(name="late_work", bufs=3))
-        pools["product"] = ctx.enter_context(tc.tile_pool(name="product_two", bufs=6))
+        product_pool = ctx.enter_context(tc.tile_pool(name="product_pool", bufs=10))
         message_pool = ctx.enter_context(tc.tile_pool(name="message_pool", bufs=8))
         out_by_tile = out[0].rearrange("(m p) h w -> p m (h w)", p=P)
         weights = late.tile([P, LANES, B_PX], F32, name="weights")
@@ -544,7 +564,7 @@ def tile_dcblock_kernel(
                         masked[:, j : B_PX : B_COLS, :, cols],
                     ))
             for place, e in calls:
-                nc.vector.tensor_tensor(out=place, in0=place, in1=e, op=ALU.add)
+                nc.gpsimd.tensor_tensor(out=place, in0=place, in1=e, op=ALU.add)
 
         turned_class = {}
 
@@ -553,15 +573,26 @@ def tile_dcblock_kernel(
             for m in range(4):
                 nc.tensor.transpose(out=turned_class[q][:, m, :], in_=spread[:, P * (4 * q + m) : P * (4 * q + m + 1)], identity=ident_f32[:])
 
-        def collect_class(engine_copy, q, lanes):
-            engine_copy(
-                out=weights[:, lanes, 4 * q : 4 * q + 4], in_=turned_class[q][:].rearrange("q m b -> q b m")[:, lanes, :]
+        def collect_class(q, lanes_of):
+            nc.scalar.copy(
+                out=lanes_of(weights[:, :, 4 * q : 4 * q + 4].rearrange("q (b c) m -> q b c m", c=PER_STRIP)),
+                in_=lanes_of(turned_class[q][:, :, 0:LANES].rearrange("q m (b c) -> q b c m", c=PER_STRIP)),
             )
 
-        def turn_and_collect(lanes):
+        def inner_lanes(v):
+            return v[:, 1 : STRIPS - 1, 1 : 1 + INNER, :]
+
+        def row_lanes(v):
+            return v[:, 0 : STRIPS : STRIPS - 1, :, :]
+
+        def col_lanes(v):
+            return v[:, 1 : STRIPS - 1, 0 : PER_STRIP : PER_STRIP - 1, :]
+
+        def turn_and_collect(lane_sets):
             for q in range(B_PX // 4):
                 turn_class(q)
-                collect_class(nc.scalar.copy if q % 2 == 0 else nc.vector.tensor_copy, q, lanes)
+                for lanes_of in lane_sets:
+                    collect_class(q, lanes_of)
 
         gathered = {}
 
@@ -622,30 +653,30 @@ def tile_dcblock_kernel(
 
         def inner_banks(strip):
             return [
-                ("wide", B_ROWS * strip, B_COLS * bc, [((strip, b), INNER * (strip - 1) + b - 1, 1) for b in range(bc, bc + 3)])
+                ("wide", B_ROWS * strip, B_COLS * bc, [((strip, b), PER_STRIP * strip + b, 1) for b in range(bc, bc + 3)])
                 for bc in (1, 4)
             ]
 
         def row_banks(side):
-            lane = TOP_LANE if side == 0 else BOTTOM_LANE
+            lane = 0 if side == 0 else LANES - PER_STRIP
             row = 0 if side == 0 else SIDE - B_ROWS
             return [
                 ("wide", row, 4 * B_COLS * h, [((SIDES[side], m), lane + 2 * m, 2) for m in (2 * h, 2 * h + 1)]) for h in range(2)
             ]
 
         def col_bank(side, pairs):
-            lane = LEFT_LANE if side == 2 else RIGHT_LANE
+            lane = PER_STRIP if side == 2 else 2 * PER_STRIP - 1
             col = 0 if side == 2 else SIDE - B_COLS
-            return ("tall", B_ROWS + 2 * B_ROWS * pairs[0], col, [((SIDES[side], m), lane + 2 * m, 2) for m in pairs])
+            return ("tall", B_ROWS + 2 * B_ROWS * pairs[0], col, [((SIDES[side], m), lane + 2 * PER_STRIP * m, 2) for m in pairs])
 
         core_end = CORE_COL + CORE_USED
-        leftover = ("tall", CORE_ROW, core_end, [((st, core_end // B_COLS), INNER * (st - 1) + core_end // B_COLS - 1, 1) for st in range(4, 8)])
+        leftover = ("tall", CORE_ROW, core_end, [((st, core_end // B_COLS), PER_STRIP * st + core_end // B_COLS, 1) for st in range(4, 8)])
         bank_list = []
-        for strip in (1, 2, 3):
+        for strip in (1, 2, 3, 8):
             bank_list += inner_banks(strip)
         bank_list += row_banks(0) + [col_bank(2, (0, 1)), col_bank(3, (0, 1))]
         after_bank = {len(bank_list) - 1: range(0, 6)}
-        for strip in (8, 9, 10):
+        for strip in (9, 10):
             bank_list += inner_banks(strip)
         bank_list += row_banks(1) + [col_bank(2, (3, 4)), col_bank(3, (3, 4))]
         after_bank[len(bank_list) - 1] = range(12, 18)
@@ -681,14 +712,14 @@ def tile_dcblock_kernel(
             shape, row, col, members = bank_list[m]
             name, lane, count = members[place]
             if place == 0 and j == 0:
-                main_bank[m] = psum_main.tile([P, PACK, 96], F32, name="main_bank")
+                main_bank[m] = psum_main.tile([P, PACK, 96], F32, name="main_bank", tag="main")
             px = count * B_PX
             bank = main_bank[m][:, j, 0 : px * len(members)]
-            rhs = weights[:, lane : lane + count, :]
             if shape == "tall":
-                dst = bank[:, px * place : px * (place + 1)]
-                rhs = rhs.rearrange("q l k -> q (l k)")
+                dst = bank[:, px * place : px * (place + 1)].rearrange("p (l k) -> p l k", k=B_PX)
+                rhs = weights[:, lane : lane + PER_STRIP * (count - 1) + 1 : PER_STRIP, :]
             else:
+                rhs = weights[:, lane : lane + count, :]
                 width = B_COLS * count
                 dst = bank.rearrange("p (i w) -> p i w", i=B_ROWS)[:, :, width * place : width * (place + 1)].rearrange(
                     "p i (l j) -> p l i j", j=B_COLS
@@ -716,7 +747,7 @@ def tile_dcblock_kernel(
         def normalise(t):
             agg[t] = late_work.tile([P, PACK, P], BF16, name="agg")
             nc.scalar.activation(
-                out=agg[t][:], in_=acc[t][:].rearrange("p (q j) -> p j q", j=PACK), func=ACT.Copy, scale=inv_sum[:, t : t + 1]
+                out=agg[t][:], in_=acc[t][:], func=ACT.Copy, scale=inv_sum[:, t : t + 1]
             )
 
         def turn(t):
@@ -729,6 +760,26 @@ def tile_dcblock_kernel(
             nc.scalar.copy(
                 out=rows_of_agg[:, rows, CORE_COL : CORE_COL + CORE_USED, :],
                 in_=turned[t][:].rearrange("q j (r w) -> q r w j", w=CORE_COLS)[:, :, 0:CORE_USED, :],
+            )
+
+        def spread_inv_sum():
+            t = CORE_TILES - 1
+            repeated = late_work.tile([P, P], F32, name="repeated")
+            nc.scalar.activation(out=repeated[:], in_=ones[:], func=ACT.Copy, scale=inv_sum[:, t : t + 1])
+            bank = psum_turns.tile([P, P], F32, name="inv_bank", tag="bank")
+            nc.tensor.transpose(out=bank[:], in_=repeated[:], identity=ident_f32[:])
+            nc.scalar.copy(out=inv_spread[:], in_=bank[:])
+
+        def place_turned():
+            row = CORE_ROW + TILE_ROWS * (CORE_TILES - 1)
+            by_row = "q (r w) -> q r w"
+            nc.vector.tensor_tensor(
+                out=rows_of_agg[:, row : row + TILE_ROWS, CORE_COL : CORE_COL + CORE_USED, :],
+                in0=acc_turned[:].rearrange("q j (r w) -> q r w j", w=CORE_COLS)[:, :, 0:CORE_USED, :],
+                in1=inv_spread[:].rearrange(by_row, w=CORE_COLS)[:, :, 0:CORE_USED].unsqueeze(3).to_broadcast(
+                    [P, TILE_ROWS, CORE_USED, PACK]
+                ),
+                op=ALU.mult,
             )
 
         def quantise_agg(t):
@@ -767,7 +818,7 @@ def tile_dcblock_kernel(
                 plan(step + 1 + place, fuse, t)
                 plan(step + 2 + place, add_x_and_store, t)
 
-        for t in range(CORE_TILES):
+        for t in range(CORE_TILES - 1):
             plan(STEPS + t, normalise, t)
             plan(STEPS + t + 1, turn, t)
             plan(STEPS + t + 2, place_core, t)
@@ -778,6 +829,8 @@ def tile_dcblock_kernel(
         nc.sync.dma_start(out=x_res[:], in_=x[0].rearrange("(m p) h w -> p m (h w)", p=P))
         n_block = 0
         n_aggregated = 0
+        made = {}
+        products[1] = [acc[CORE_TILES - 1]]
         to_collect = []
         with tc.manual_schedule():
             for step in range(PART_ONE, STEPS + 11):
@@ -787,10 +840,17 @@ def tile_dcblock_kernel(
                     nc.vector.tensor_scalar_add(out=inv_sum[:], in0=inv_sum[:], scalar1=1.0)
                     nc.vector.reciprocal(out=inv_sum[:], in_=inv_sum[:])
                 for kind in range(1, 9):
-                    if step == PART_ONE + 1 + kind // 2:
+                    if step == PART_ONE + kind:
                         mask_edge(kind)
-                    if step == PART_ONE + 2 + kind // 2:
+                    if step == PART_ONE + kind + 1:
                         spread_edge(kind)
+                phase, k = divmod(step, KW)
+                if k == 2 and 2 <= phase < KW:
+                    collect_turned(phase - 1)
+                if step == STEPS + 1:
+                    collect_turned(KW - 1)
+                if step == STEPS + 2:
+                    place_turned()
                 if step < STEPS:
                     next_codes(step)
 
@@ -805,7 +865,7 @@ def tile_dcblock_kernel(
 
                 parts = []
                 if step >= FIRST_SUM_STEP:
-                    while n_aggregated < n_block:
+                    while n_aggregated < made[step - 2]:
                         for j in range(PACK):
                             parts.append((n_aggregated, j))
                         m, place = blocks[n_aggregated]
@@ -816,6 +876,7 @@ def tile_dcblock_kernel(
                 if step >= FIRST_BLOCK_STEP:
                     span = LAST_BLOCK_STEP - FIRST_BLOCK_STEP
                     n_block = min(len(blocks), -(-len(blocks) * (step + 1 - FIRST_BLOCK_STEP) // span))
+                made[step] = n_block
                 for n in range(first_new, min(n_block + 1, len(blocks))):
                     gather_for(n)
                 n_mx = (CORE_TILES if step < STEPS else 0) + n_block - first_new
@@ -840,9 +901,15 @@ def tile_dcblock_kernel(
                     aggregate_part(n, j)
 
                 if step == PART_ONE:
-                    turn_and_collect(slice(0, INNER_LANES))
-                if step == PART_ONE + 6:
-                    turn_and_collect(slice(INNER_LANES, LANES))
+                    turn_and_collect((inner_lanes,))
+                if step == PART_ONE + 11:
+                    turn_and_collect((row_lanes, col_lanes))
+                if k == 1 and 2 <= phase < KW:
+                    add_on_tensor(phase - 1)
+                if step == STEPS:
+                    add_on_tensor(KW - 1)
+                if step == PART_ONE + 12:
+                    spread_inv_sum()
                 for stage, t in stage_queue.get(step, []):
                     if stage in (fuse, turn):
                         stage(t)

@@ -76,6 +76,7 @@ PART_ONE = 8
 FIRST_BLOCK_STEP = 8
 FIRST_SUM_STEP = 10
 LAST_BLOCK_STEP = 46
+GATHER_AHEAD = 4
 
 FLOPS = 2 * 2 * C * C * NPX + 2 * KW * KW * C * NPX
 
@@ -122,10 +123,6 @@ def tile_dcblock_kernel(
         q_codes = [keep.tile([P, PER_STRIP, P], U32, name="q_codes%d" % b, align_bytes=64) for b in range(2)]
         q_plane = [keep.tile([P, PER_STRIP, P], U8, name="q_plane%d" % b, align_bytes=64) for b in range(2)]
         acc = [keep.tile([P, PACK, P], F32, name="acc%d" % t) for t in range(CORE_TILES)]
-        acc_turned = keep.tile([P, PACK, P], F32, name="acc_turned")
-        inv_spread = keep.tile([P, P], F32, name="inv_spread")
-        ones = keep.tile([P, P], F32, name="ones")
-        nc.gpsimd.memset(ones[:], 1.0)
         dist_core = keep.tile([P, CORE_TILES, 2 * SETS * D], F32, name="dist_core")
         e_core = keep.tile([P, CORE_TILES, 2 * SETS * D], F32, name="e_core")
         inv_sum = keep.tile([P, CORE_TILES], F32, name="inv_sum")
@@ -190,7 +187,7 @@ def tile_dcblock_kernel(
         def move_codes(dj, b):
             rows = slice(CORE_ROW * PITCH, (CORE_ROW + MID_ROWS) * PITCH)
             cols = slice(CORE_COL + R + dj, CORE_COL + R + dj + CORE_COLS)
-            nc.vector.tensor_copy(
+            nc.sync.dma_start(
                 out=codes[b][:].bitcast(I32).rearrange("p (r w) -> p r w", w=CORE_COLS),
                 in_=codes_img[:, rows].bitcast(I32).rearrange("p (r w) -> p r w", w=PITCH)[:, :, cols],
             )
@@ -211,41 +208,21 @@ def tile_dcblock_kernel(
             if phase < KW - 1 and k == 5:
                 move_plane((phase + 1) % 2)
 
-        products = {}
-        sum_bank = {}
-
-        def multiply_for_tensor(b, phase, di, dj):
-            t = CORE_TILES - 1
-            bank = psum_s.tile([P, C], F32, name="bank_s")
+        def add_on_gpsimd(b, t, di, dj):
+            bank = psum_s.tile([P, C], F32, name="bank_s", tag="s")
             messages_of_neighbours(bank, b, t, di)
             product = product_pool.tile([P, PACK, P], F32, name="product")
             nc.scalar.activation(
                 out=product[:], in_=bank[:].rearrange("p (q j) -> p j q", j=PACK), func=ACT.Copy, scale=weight(t, di, dj)
             )
-            products.setdefault(phase, []).append(product)
-
-        def add_on_tensor(phase):
-            sum_bank[phase] = psum_turns.tile([P, PACK, P], F32, name="sum_bank", tag="bank")
-            n = len(products[phase])
-            for j in range(PACK):
-                for m, product in enumerate(products[phase]):
-                    nc.tensor.matmul(
-                        out=sum_bank[phase][:, j, :], lhsT=product[:, j, :], rhs=ident_f32[:],
-                        is_transpose=True, start=(m == 0), stop=(m == n - 1),
-                    )
-
-        def collect_turned(phase):
-            if phase == 1:
-                nc.vector.tensor_copy(out=acc_turned[:], in_=sum_bank[phase][:])
-            else:
-                nc.vector.tensor_tensor(out=acc_turned[:], in0=sum_bank[phase][:], in1=acc_turned[:], op=ALU.add)
+            nc.gpsimd.tensor_tensor(out=acc[t][:], in0=acc[t][:], in1=product[:], op=ALU.add)
 
         def product_calls(step):
             phase, k = divmod(step, KW)
             on_vector, on_scalar = [], []
             for t in range(CORE_TILES):
                 if t == CORE_TILES - 1 and step >= PART_ONE:
-                    on_scalar.append(lambda t=t: multiply_for_tensor(phase % 2, phase, k - R, phase - R))
+                    on_scalar.append(lambda t=t: add_on_gpsimd(phase % 2, t, k - R, phase - R))
                 else:
                     on_vector.append(lambda t=t: add_on_vector(phase % 2, t, k - R, phase - R, step == 0))
             return on_vector, on_scalar
@@ -309,7 +286,10 @@ def tile_dcblock_kernel(
             banks = {}
 
             def turn_squares(half, q):
-                banks[half, q] = psum_main.tile([P, 4, P], F32, name="turned_squares", tag="main")
+                if (half + q) % 2 == 0:
+                    banks[half, q] = psum_main.tile([P, 4, P], F32, name="turned_squares", tag="main")
+                else:
+                    banks[half, q] = psum_s.tile([P, 4, P], F32, name="turned_squares", tag="s")
                 for m in range(4):
                     first_col = P * m if q == 0 else CORE_PX + LANES * (4 * (q - 1) + m)
                     for s in range(SLICES):
@@ -336,17 +316,20 @@ def tile_dcblock_kernel(
             def exp_class(half):
                 cols = slice(SETS * D * half, SETS * D * (half + 1))
                 nc.scalar.activation(out=dist_class[:, :, cols], in_=dist_class[:, :, cols], func=ACT.Exp, scale=neg_inv_denom[:, 0:1])
-                for pos in range(SETS):
-                    g = SET_ORDER[SETS * half + pos]
-                    first_col = D * (SETS * half + pos)
-                    if g < KW:
-                        places = e_class[:, :, :, g]
-                    else:
-                        places = e_class[:, :, R, :]
+                first_set = SETS * half
+                if half == 0:
                     nc.scalar.activation(
-                        out=places.rearrange("p k (s r) -> p k s r", s=2)[:, :, :, 0:R],
-                        in_=dist_class[:, :, first_col : first_col + D].rearrange("p k (s r) -> p k s r", s=2),
-                        func=ACT.Exp, bias=minus_one[:, 0:1],
+                        out=e_class[:, :, R, :].rearrange("p k (s r) -> p k s r", s=2)[:, :, :, 0:R],
+                        in_=dist_class[:, :, 0:D].rearrange("p k (s r) -> p k s r", s=2), func=ACT.Exp, bias=minus_one[:, 0:1],
+                    )
+                    first_set = 1
+                last_set = SETS * (half + 1)
+                sets = dist_class[:, :, D * first_set : D * last_set].rearrange("p k (g s r) -> p k s r g", s=2, r=R)
+                for side in range(2):
+                    row = (R + 1) * side
+                    nc.scalar.activation(
+                        out=e_class[:, :, row : row + R, first_set - 1 : last_set - 1], in_=sets[:, :, side], func=ACT.Exp,
+                        bias=minus_one[:, 0:1],
                     )
 
             with tc.tile_pool(name="early", bufs=1) as first:
@@ -419,10 +402,10 @@ def tile_dcblock_kernel(
                 nc.vector.memset(grouped[:, (R + SIDE) * PITCH - R : WORDS, :], 0.0)
                 between = grouped[:, top + SIDE : top + SIDE + (SIDE - 1) * PITCH, :].rearrange("p (r w) j -> p r w j", w=PITCH)
                 nc.vector.memset(between[:, :, 0 : 2 * R, :], 0.0)
-                nc.vector.memset(plane_img[:].bitcast(I32), 0)
+                nc.gpsimd.memset(plane_img[:].bitcast(I32), 0)
                 for b in range(2):
-                    nc.vector.memset(q_codes[b][:, :, Q_PX:P], 0)
-                    nc.vector.memset(q_plane[b][:].bitcast(I32), 0)
+                    nc.gpsimd.memset(q_codes[b][:, :, Q_PX:P], 0)
+                    nc.gpsimd.memset(q_plane[b][:].bitcast(I32), 0)
 
                 for third in range(3):
                     px = slice(THIRD_PX * third, THIRD_PX * (third + 1))
@@ -486,26 +469,27 @@ def tile_dcblock_kernel(
                         if step == at:
                             square_core(u)
                             square_class(u)
-                    if step > 0:
-                        for half, q in TURNS[2 * step - 2 : 2 * step]:
-                            sum_channels(half, q)
-                    if step == 3:
-                        exp_class(0)
-                    if step == 5:
-                        exp_core(1)
-                    if step == 7:
-                        exp_class(1)
                     next_codes(step)
                     on_vector, on_scalar = product_calls(step)
-                    for call in on_vector + on_scalar:
+                    last_turns = TURNS[2 * step - 2 : 2 * step] if step > 0 else []
+                    for m, call in enumerate(on_vector):
                         call()
+                        if m % 2 == 1 and m // 2 < len(last_turns):
+                            half, q = last_turns[m // 2]
+                            sum_channels(half, q)
+                            if (half, q) == (0, 6):
+                                exp_class(0)
+                            elif (half, q) == (1, 0):
+                                exp_core(1)
+                            elif (half, q) == (1, 6):
+                                exp_class(1)
                     for half, q in TURNS[2 * step : 2 * step + 2]:
                         turn_squares(half, q)
             fuse_codes, fuse_plane = load_weight(w_fuse_words, w_fuse_scales, "fuse")
 
         late = ctx.enter_context(tc.tile_pool(name="late", bufs=1))
         late_work = ctx.enter_context(tc.tile_pool(name="late_work", bufs=3))
-        product_pool = ctx.enter_context(tc.tile_pool(name="product_pool", bufs=10))
+        product_pool = ctx.enter_context(tc.tile_pool(name="product_pool", bufs=8))
         message_pool = ctx.enter_context(tc.tile_pool(name="message_pool", bufs=8))
         out_by_tile = out[0].rearrange("(m p) h w -> p m (h w)", p=P)
         weights = late.tile([P, LANES, B_PX], F32, name="weights")
@@ -514,8 +498,8 @@ def tile_dcblock_kernel(
             n = 4 if side < 2 else 5
             edge_codes.append(late.tile([P, n, P], U32, name="edge_codes%d" % side, align_bytes=64))
             edge_plane.append(late.tile([P, n, P], U8, name="edge_plane%d" % side, align_bytes=64))
-            nc.vector.memset(edge_codes[side][:, :, PAIR_ROWS * PAIR_COLS : P], 0)
-            nc.vector.memset(edge_plane[side][:].bitcast(I32), 0)
+            nc.gpsimd.memset(edge_codes[side][:, :, PAIR_ROWS * PAIR_COLS : P], 0)
+            nc.gpsimd.memset(edge_plane[side][:].bitcast(I32), 0)
         agg_img = late.tile([P, NPX, PACK], BF16, name="agg_img", align_bytes=64)
         x_res = late.tile([P, C // P, NPX], BF16, name="x_res")
 
@@ -596,59 +580,72 @@ def tile_dcblock_kernel(
 
         gathered = {}
 
-        def gather(dst_codes, dst_plane, dst_view, source_view):
-            for dst, source, dtype in ((dst_codes, codes_img, I32), (dst_plane, plane_img, U8)):
-                rows = source[:, 0 : PITCH * PITCH].bitcast(dtype).rearrange("p (r w) -> p r w", w=PITCH)
-                nc.vector.tensor_copy(out=dst_view(dst[:].bitcast(dtype)), in_=source_view(rows))
+        def rows_of(source, dtype):
+            return source[:, 0 : PITCH * PITCH].bitcast(dtype).rearrange("p (r w) -> p r w", w=PITCH)
+
+        def window_codes(dst, row, col, rows, cols):
+            nc.sync.dma_start(
+                out=dst[:, 0 : rows * cols].bitcast(I32).rearrange("p (r c) -> p r c", c=cols),
+                in_=rows_of(codes_img, I32)[:, row : row + rows, col : col + cols],
+            )
 
         def gather_strip(strip):
             slot = strip % 2
             row = B_ROWS * strip
             for half in range(2):
                 col = B_COLS * (1 + half)
-                gather(
-                    q_codes[slot], q_plane[slot],
-                    lambda t: t[:, 0:INNER, 0:Q_PX].rearrange("p b (r c) -> p b r c", c=Q_COLS)[:, :, :, B_COLS * half : B_COLS * (half + 1)],
-                    lambda v: v[:, row : row + Q_ROWS, col : col + B_COLS * INNER].rearrange("p r (b c) -> p b r c", c=B_COLS),
+                nc.vector.tensor_copy(
+                    out=q_plane[slot][:, 0:INNER, 0:Q_PX].rearrange("p b (r c) -> p b r c", c=Q_COLS)[
+                        :, :, :, B_COLS * half : B_COLS * (half + 1)
+                    ],
+                    in_=rows_of(plane_img, U8)[:, row : row + Q_ROWS, col : col + B_COLS * INNER].rearrange(
+                        "p r (b c) -> p b r c", c=B_COLS
+                    ),
                 )
             for bc in range(1, 1 + INNER):
+                window_codes(q_codes[slot][:, bc - 1, :], row, B_COLS * bc, Q_ROWS, Q_COLS)
                 gathered[strip, bc] = (q_codes[slot][:, bc - 1, :], q_plane[slot][:, bc - 1, :])
 
         def gather_one(strip, bc):
             slot = strip % 2
             row, col = B_ROWS * strip, B_COLS * bc
-            gather(
-                q_codes[slot], q_plane[slot],
-                lambda t: t[:, strip // 2, 0:Q_PX].rearrange("p (r c) -> p r c", c=Q_COLS),
-                lambda v: v[:, row : row + Q_ROWS, col : col + Q_COLS],
+            q, plane = q_codes[slot][:, strip // 2, :], q_plane[slot][:, strip // 2, :]
+            window_codes(q, row, col, Q_ROWS, Q_COLS)
+            nc.vector.tensor_copy(
+                out=plane[:, 0:Q_PX].rearrange("p (r c) -> p r c", c=Q_COLS),
+                in_=rows_of(plane_img, U8)[:, row : row + Q_ROWS, col : col + Q_COLS],
             )
-            gathered[strip, bc] = (q_codes[slot][:, strip // 2, :], q_plane[slot][:, strip // 2, :])
+            gathered[strip, bc] = (q, plane)
 
         def gather_side(side):
+            planes_here = rows_of(plane_img, U8)
             if side < 2:
                 row = R if side == 0 else R + SIDE - PAIR_ROWS
+                windows_here = [(row, 2 * B_COLS * m, PAIR_ROWS, PAIR_COLS) for m in range(4)]
                 for third in range(3):
                     col = B_COLS * third
                     start = min(col, B_COLS)
-                    gather(
-                        edge_codes[side], edge_plane[side],
-                        lambda t: t[:, 0:4, 0 : PAIR_ROWS * PAIR_COLS].rearrange("p b (r c) -> p b r c", c=PAIR_COLS)[
+                    nc.vector.tensor_copy(
+                        out=edge_plane[side][:, :, 0 : PAIR_ROWS * PAIR_COLS].rearrange("p b (r c) -> p b r c", c=PAIR_COLS)[
                             :, :, :, col : col + B_COLS
                         ],
-                        lambda v: v[:, row : row + PAIR_ROWS, start : start + SIDE].rearrange("p r (b c) -> p b r c", c=2 * B_COLS)[
-                            :, :, :, col - start : col - start + B_COLS
-                        ],
+                        in_=planes_here[:, row : row + PAIR_ROWS, start : start + SIDE].rearrange(
+                            "p r (b c) -> p b r c", c=2 * B_COLS
+                        )[:, :, :, col - start : col - start + B_COLS],
                     )
             else:
                 col = R if side == 2 else R + SIDE - EDGE_COLS
+                windows_here = [(B_ROWS + 2 * B_ROWS * m, col, 14, EDGE_COLS) for m in range(5)]
                 for first_row, n in ((0, 8), (8, 6)):
                     row = B_ROWS + first_row
-                    gather(
-                        edge_codes[side], edge_plane[side],
-                        lambda t: t[:, 0:5, EDGE_COLS * first_row : EDGE_COLS * (first_row + n)].rearrange("p b (r c) -> p b r c", c=EDGE_COLS),
-                        lambda v: v[:, row : row + 40, col : col + EDGE_COLS].rearrange("p (b r) c -> p b r c", r=8)[:, :, 0:n, :],
+                    nc.vector.tensor_copy(
+                        out=edge_plane[side][:, :, EDGE_COLS * first_row : EDGE_COLS * (first_row + n)].rearrange(
+                            "p b (r c) -> p b r c", c=EDGE_COLS
+                        ),
+                        in_=planes_here[:, row : row + 40, col : col + EDGE_COLS].rearrange("p (b r) c -> p b r c", r=8)[:, :, 0:n, :],
                     )
-            for m in range(4 if side < 2 else 5):
+            for m, window in enumerate(windows_here):
+                window_codes(edge_codes[side][:, m, :], window[0], window[1], window[2], window[3])
                 gathered[SIDES[side], m] = (edge_codes[side][:, m, :], edge_plane[side][:, m, :])
 
         def inner_banks(strip):
@@ -699,7 +696,7 @@ def tile_dcblock_kernel(
         def make_messages(n):
             m, place = blocks[n]
             q, plane = gathered[bank_list[m][3][place][0]]
-            bank = psum_s.tile([P, C], F32, name="bank_s")
+            bank = psum_s.tile([P, C], F32, name="bank_s", tag="s")
             nc.tensor.matmul_mx(
                 out=bank[:], lhsT=q.bitcast(FP8X4), lhsT_scale=plane,
                 rhs=feat_codes[:].bitcast(FP8X4), rhs_scale=feat_plane[:], start=True, stop=True,
@@ -762,26 +759,6 @@ def tile_dcblock_kernel(
                 in_=turned[t][:].rearrange("q j (r w) -> q r w j", w=CORE_COLS)[:, :, 0:CORE_USED, :],
             )
 
-        def spread_inv_sum():
-            t = CORE_TILES - 1
-            repeated = late_work.tile([P, P], F32, name="repeated")
-            nc.scalar.activation(out=repeated[:], in_=ones[:], func=ACT.Copy, scale=inv_sum[:, t : t + 1])
-            bank = psum_turns.tile([P, P], F32, name="inv_bank", tag="bank")
-            nc.tensor.transpose(out=bank[:], in_=repeated[:], identity=ident_f32[:])
-            nc.scalar.copy(out=inv_spread[:], in_=bank[:])
-
-        def place_turned():
-            row = CORE_ROW + TILE_ROWS * (CORE_TILES - 1)
-            by_row = "q (r w) -> q r w"
-            nc.vector.tensor_tensor(
-                out=rows_of_agg[:, row : row + TILE_ROWS, CORE_COL : CORE_COL + CORE_USED, :],
-                in0=acc_turned[:].rearrange("q j (r w) -> q r w j", w=CORE_COLS)[:, :, 0:CORE_USED, :],
-                in1=inv_spread[:].rearrange(by_row, w=CORE_COLS)[:, :, 0:CORE_USED].unsqueeze(3).to_broadcast(
-                    [P, TILE_ROWS, CORE_USED, PACK]
-                ),
-                op=ALU.mult,
-            )
-
         def quantise_agg(t):
             agg_codes = late_work.tile([P, P], U32, name="agg_codes", align_bytes=64)
             agg_plane = late_work.tile([P, P], U8, name="agg_plane", align_bytes=64)
@@ -818,7 +795,7 @@ def tile_dcblock_kernel(
                 plan(step + 1 + place, fuse, t)
                 plan(step + 2 + place, add_x_and_store, t)
 
-        for t in range(CORE_TILES - 1):
+        for t in range(CORE_TILES):
             plan(STEPS + t, normalise, t)
             plan(STEPS + t + 1, turn, t)
             plan(STEPS + t + 2, place_core, t)
@@ -830,27 +807,14 @@ def tile_dcblock_kernel(
         n_block = 0
         n_aggregated = 0
         made = {}
-        products[1] = [acc[CORE_TILES - 1]]
         to_collect = []
         with tc.manual_schedule():
             for step in range(PART_ONE, STEPS + 11):
-                if step == PART_ONE:
-                    spread_inner()
-                    nc.vector.tensor_reduce(out=inv_sum[:], in_=e_core[:], axis=AXIS.X, op=ALU.add)
-                    nc.vector.tensor_scalar_add(out=inv_sum[:], in0=inv_sum[:], scalar1=1.0)
-                    nc.vector.reciprocal(out=inv_sum[:], in_=inv_sum[:])
                 for kind in range(1, 9):
                     if step == PART_ONE + kind:
                         mask_edge(kind)
                     if step == PART_ONE + kind + 1:
                         spread_edge(kind)
-                phase, k = divmod(step, KW)
-                if k == 2 and 2 <= phase < KW:
-                    collect_turned(phase - 1)
-                if step == STEPS + 1:
-                    collect_turned(KW - 1)
-                if step == STEPS + 2:
-                    place_turned()
                 if step < STEPS:
                     next_codes(step)
 
@@ -877,7 +841,7 @@ def tile_dcblock_kernel(
                     span = LAST_BLOCK_STEP - FIRST_BLOCK_STEP
                     n_block = min(len(blocks), -(-len(blocks) * (step + 1 - FIRST_BLOCK_STEP) // span))
                 made[step] = n_block
-                for n in range(first_new, min(n_block + 1, len(blocks))):
+                for n in range(first_new, min(n_block + GATHER_AHEAD, len(blocks))):
                     gather_for(n)
                 n_mx = (CORE_TILES if step < STEPS else 0) + n_block - first_new
                 shares = [len(parts) * (m + 1) // n_mx - len(parts) * m // n_mx for m in range(n_mx)]
@@ -901,15 +865,14 @@ def tile_dcblock_kernel(
                     aggregate_part(n, j)
 
                 if step == PART_ONE:
+                    spread_inner()
                     turn_and_collect((inner_lanes,))
-                if step == PART_ONE + 11:
+                if step == PART_ONE + 1:
+                    nc.vector.tensor_reduce(out=inv_sum[:], in_=e_core[:], axis=AXIS.X, op=ALU.add)
+                    nc.vector.tensor_scalar_add(out=inv_sum[:], in0=inv_sum[:], scalar1=1.0)
+                    nc.vector.reciprocal(out=inv_sum[:], in_=inv_sum[:])
+                if step == PART_ONE + 14:
                     turn_and_collect((row_lanes, col_lanes))
-                if k == 1 and 2 <= phase < KW:
-                    add_on_tensor(phase - 1)
-                if step == STEPS:
-                    add_on_tensor(KW - 1)
-                if step == PART_ONE + 12:
-                    spread_inv_sum()
                 for stage, t in stage_queue.get(step, []):
                     if stage in (fuse, turn):
                         stage(t)

@@ -51,11 +51,15 @@ SIDES = ("top", "bottom", "left", "right")
 PAIR_ROWS, PAIR_COLS = B_ROWS + R, 2 * B_COLS + 2 * R
 EDGE_COLS = B_COLS + R
 
-SETS = 4
+SETS = 2
 D = 6
-CH = 5
-SLICES = 4
-SET_ROWS = 32
+CH = 10
+SLICES = 2
+SET_ROWS = 64
+ROUNDS = 4
+UNITS = ROUNDS * SLICES
+BANK_ORDER = [(r, q) for r in range(ROUNDS) for q in range(7)]
+CLASS_BANKS = 6
 PAD_LEFT = 4
 PAD_PITCH = PAD_LEFT + SIDE + 4
 PAD_ROWS = SIDE + 2 * R
@@ -65,18 +69,20 @@ ONE_SIDE = (-3, -2, -1, 1, 2, 3)
 SET_ORDER = [KW] + list(range(KW))
 CLASS_PX = LANES * B_PX
 SQ_COLS = CORE_PX + CLASS_PX + P - LANES
-SHIFTED_BUFS = 4
+SHIFTED_BUFS = 6
 
 STORE_ROWS = 32
 BLOCK_ROWS = STORE_ROWS * D
 PARK_PITCH = 3072
 
-TURNS = [(0, q) for q in range(1, 7)] + [(1, q) for q in range(7)]
-PART_ONE = 8
-FIRST_BLOCK_STEP = 8
-FIRST_SUM_STEP = 10
-LAST_BLOCK_STEP = 46
-GATHER_AHEAD = 4
+PART_ONE = 5
+FIRST_BLOCK_STEP = 5
+FIRST_SUM_STEP = 7
+LAST_BLOCK_STEP = 45
+PARTS_PER_STEP = 7
+GATHER_AHEAD = 2
+CODES_AHEAD = 12
+WINDOWS = 58
 
 FLOPS = 2 * 2 * C * C * NPX + 2 * KW * KW * C * NPX
 
@@ -120,13 +126,12 @@ def tile_dcblock_kernel(
         plane_img = keep.tile([P, WORDS], U8, name="plane_img", align_bytes=64)
         codes = [keep.tile([P, MID_COLS], U32, name="codes%d" % b, align_bytes=64) for b in range(2)]
         planes = [keep.tile([P, 2, MID_COLS], U8, name="planes%d" % b, align_bytes=64) for b in range(2)]
-        q_codes = [keep.tile([P, PER_STRIP, P], U32, name="q_codes%d" % b, align_bytes=64) for b in range(2)]
         q_plane = [keep.tile([P, PER_STRIP, P], U8, name="q_plane%d" % b, align_bytes=64) for b in range(2)]
         acc = [keep.tile([P, PACK, P], F32, name="acc%d" % t) for t in range(CORE_TILES)]
-        dist_core = keep.tile([P, CORE_TILES, 2 * SETS * D], F32, name="dist_core")
-        e_core = keep.tile([P, CORE_TILES, 2 * SETS * D], F32, name="e_core")
+        dist_core = keep.tile([P, CORE_TILES, ROUNDS * SETS * D], F32, name="dist_core")
+        e_core = keep.tile([P, CORE_TILES, ROUNDS * SETS * D], F32, name="e_core")
         inv_sum = keep.tile([P, CORE_TILES], F32, name="inv_sum")
-        dist_class = keep.tile([P, B_PX, 2 * SETS * D], F32, name="dist_class")
+        dist_class = keep.tile([P, B_PX, ROUNDS * SETS * D], F32, name="dist_class")
         e_class = keep.tile([P, B_PX, 8, 8], F32, name="e_class")
         inv_class = keep.tile([P, B_PX], F32, name="inv_class")
         spread = keep.tile([P, 30 * P], F32, name="spread")
@@ -187,7 +192,8 @@ def tile_dcblock_kernel(
         def move_codes(dj, b):
             rows = slice(CORE_ROW * PITCH, (CORE_ROW + MID_ROWS) * PITCH)
             cols = slice(CORE_COL + R + dj, CORE_COL + R + dj + CORE_COLS)
-            nc.sync.dma_start(
+            move = nc.vector.tensor_copy if dj == -R else nc.sync.dma_start
+            move(
                 out=codes[b][:].bitcast(I32).rearrange("p (r w) -> p r w", w=CORE_COLS),
                 in_=codes_img[:, rows].bitcast(I32).rearrange("p (r w) -> p r w", w=PITCH)[:, :, cols],
             )
@@ -220,6 +226,14 @@ def tile_dcblock_kernel(
         def product_calls(step):
             phase, k = divmod(step, KW)
             on_vector, on_scalar = [], []
+            if phase == KW - 1:
+                order = [(t, di) for di in range(-R, R + 1) for t in (0, 1)] + [(2, di) for di in range(-R, R + 1)]
+                for t, di in order[3 * k : 3 * k + 3]:
+                    on_vector.append(lambda t=t, di=di: add_on_vector(phase % 2, t, di, phase - R, False))
+                for m in (2 * k, 2 * k + 1):
+                    if m < KW:
+                        on_scalar.append(lambda m=m: add_on_gpsimd(phase % 2, CORE_TILES - 1, m - R, phase - R))
+                return on_vector, on_scalar
             for t in range(CORE_TILES):
                 if t == CORE_TILES - 1 and step >= PART_ONE:
                     on_scalar.append(lambda t=t: add_on_gpsimd(phase % 2, t, k - R, phase - R))
@@ -239,7 +253,7 @@ def tile_dcblock_kernel(
                     nc.vector.memset(tile[:, CORE_PX + CLASS_PX : SQ_COLS], 0.0)
                     sq.append(tile)
 
-            more_squares(dist, SLICES + 1)
+            more_squares(dist, UNITS - 3)
 
             def load_shifted(u):
                 half, s = divmod(u, SLICES)
@@ -286,7 +300,7 @@ def tile_dcblock_kernel(
             banks = {}
 
             def turn_squares(half, q):
-                if (half + q) % 2 == 0:
+                if BANK_ORDER.index((half, q)) % 5 in (1, 3):
                     banks[half, q] = psum_main.tile([P, 4, P], F32, name="turned_squares", tag="main")
                 else:
                     banks[half, q] = psum_s.tile([P, 4, P], F32, name="turned_squares", tag="s")
@@ -376,9 +390,10 @@ def tile_dcblock_kernel(
                             in_=parked_of(1, s)[:, PAD_LEFT : PAD_LEFT + RUN],
                         )
 
-                for s in range(SLICES):
-                    load_centre(s)
-                    load_shifted(s)
+                for u in range(SHIFTED_BUFS):
+                    if u < SLICES:
+                        load_centre(u)
+                    load_shifted(u)
                 feat_codes, feat_plane = load_weight(w_feat_words, w_feat_scales, "feat")
 
                 neg_inv_denom = keep.tile([P, 1], F32, name="neg_inv_denom")
@@ -404,7 +419,6 @@ def tile_dcblock_kernel(
                 nc.vector.memset(between[:, :, 0 : 2 * R, :], 0.0)
                 nc.gpsimd.memset(plane_img[:].bitcast(I32), 0)
                 for b in range(2):
-                    nc.gpsimd.memset(q_codes[b][:, :, Q_PX:P], 0)
                     nc.gpsimd.memset(q_plane[b][:].bitcast(I32), 0)
 
                 for third in range(3):
@@ -437,68 +451,62 @@ def tile_dcblock_kernel(
                 move_codes(-R, 0)
                 move_plane(0)
 
-            more_squares(ctx_one.enter_context(tc.tile_pool(name="dist_two", bufs=1)), SLICES - 1)
+            dist_two = ctx_one.enter_context(tc.tile_pool(name="dist_two", bufs=1))
+            more_squares(dist_two, 3)
             with tc.manual_schedule():
                 for u in (0, 1):
                     subtract_core(nc.vector, u)
                     square_core(u)
                 subtract_class(nc.vector, 0)
                 square_class(0)
-                load_shifted(4)
-                subtract_core(nc.vector, 2)
-                square_core(2)
-                subtract_class(nc.vector, 1)
-                square_class(1)
-                load_shifted(5)
-                subtract_core(nc.vector, 3)
-                square_core(3)
                 turn_squares(0, 0)
-                for u in (2, 3):
-                    subtract_class(nc.vector, u)
-                    load_shifted(u + SLICES)
-                    square_class(u)
-                    if u == 2:
-                        sum_channels(0, 0)
-                        exp_core(0)
+                subtract_class(nc.vector, 1)
+                sum_channels(0, 0)
+                exp_core(0)
+                square_class(1)
+                turned = 1
+                summed = 1
                 for step in range(PART_ONE):
-                    for u, at, engine in ((4, 0, nc.gpsimd), (6, 0, nc.gpsimd), (5, 0, nc.gpsimd), (7, 1, nc.vector)):
+                    for u, at, engine in ((2, 0, nc.gpsimd), (3, 0, nc.vector), (4, 1, nc.gpsimd), (5, 1, nc.vector), (6, 2, nc.gpsimd), (7, 2, nc.vector)):
                         if step == at:
+                            if u >= SHIFTED_BUFS:
+                                load_shifted(u)
                             subtract_core(engine, u)
                             subtract_class(engine, u)
-                    for u, at in ((4, 0), (7, 1), (6, 1), (5, 2)):
-                        if step == at:
                             square_core(u)
                             square_class(u)
                     next_codes(step)
                     on_vector, on_scalar = product_calls(step)
-                    last_turns = TURNS[2 * step - 2 : 2 * step] if step > 0 else []
                     for m, call in enumerate(on_vector):
                         call()
-                        if m % 2 == 1 and m // 2 < len(last_turns):
-                            half, q = last_turns[m // 2]
-                            sum_channels(half, q)
-                            if (half, q) == (0, 6):
-                                exp_class(0)
-                            elif (half, q) == (1, 0):
-                                exp_core(1)
-                            elif (half, q) == (1, 6):
-                                exp_class(1)
-                    for half, q in TURNS[2 * step : 2 * step + 2]:
-                        turn_squares(half, q)
+                        if step > 0:
+                            goal = min(7 * step, 7 * (step - 1) + 2 * (m + 1))
+                            while turned < goal:
+                                turn_squares(BANK_ORDER[turned][0], BANK_ORDER[turned][1])
+                                turned += 1
+                            while summed < turned - 2 or (m == 3 and summed < turned):
+                                half, q = BANK_ORDER[summed]
+                                sum_channels(half, q)
+                                if q == 0:
+                                    exp_core(half)
+                                if q == CLASS_BANKS:
+                                    exp_class(half)
+                                summed += 1
             fuse_codes, fuse_plane = load_weight(w_fuse_words, w_fuse_scales, "fuse")
 
         late = ctx.enter_context(tc.tile_pool(name="late", bufs=1))
-        late_work = ctx.enter_context(tc.tile_pool(name="late_work", bufs=3))
+        late_work = ctx.enter_context(tc.tile_pool(name="late_work", bufs=5))
+        mask_pool = ctx.enter_context(tc.tile_pool(name="mask_pool", bufs=3))
         product_pool = ctx.enter_context(tc.tile_pool(name="product_pool", bufs=8))
         message_pool = ctx.enter_context(tc.tile_pool(name="message_pool", bufs=8))
         out_by_tile = out[0].rearrange("(m p) h w -> p m (h w)", p=P)
         weights = late.tile([P, LANES, B_PX], F32, name="weights")
-        edge_codes, edge_plane = [], []
+        window_tile = late.tile([P, WINDOWS, P], U32, name="window_tile", align_bytes=64)
+        nc.gpsimd.memset(window_tile[:, :, Q_PX:P], 0)
+        edge_plane = []
         for side in range(4):
             n = 4 if side < 2 else 5
-            edge_codes.append(late.tile([P, n, P], U32, name="edge_codes%d" % side, align_bytes=64))
             edge_plane.append(late.tile([P, n, P], U8, name="edge_plane%d" % side, align_bytes=64))
-            nc.gpsimd.memset(edge_codes[side][:, :, PAIR_ROWS * PAIR_COLS : P], 0)
             nc.gpsimd.memset(edge_plane[side][:].bitcast(I32), 0)
         agg_img = late.tile([P, NPX, PACK], BF16, name="agg_img", align_bytes=64)
         x_res = late.tile([P, C // P, NPX], BF16, name="x_res")
@@ -524,7 +532,7 @@ def tile_dcblock_kernel(
         masked_e = {}
 
         def mask_edge(kind):
-            masked_e[kind] = late_work.tile([P, B_PX, KW, KW], F32, name="masked_e")
+            masked_e[kind] = mask_pool.tile([P, B_PX, KW, KW], F32, name="masked_e")
             nc.scalar.activation(out=masked_e[kind][:], in_=seven, func=ACT.Copy, scale=mask[:, kind : kind + 1])
 
         def spread_edge(kind):
@@ -583,11 +591,24 @@ def tile_dcblock_kernel(
         def rows_of(source, dtype):
             return source[:, 0 : PITCH * PITCH].bitcast(dtype).rearrange("p (r w) -> p r w", w=PITCH)
 
-        def window_codes(dst, row, col, rows, cols):
+        def gather_codes(n):
+            name = bank_list[blocks[n][0]][3][blocks[n][1]][0]
+            row, col, rows, cols = window_of(name)
             nc.sync.dma_start(
-                out=dst[:, 0 : rows * cols].bitcast(I32).rearrange("p (r c) -> p r c", c=cols),
+                out=window_tile[:, n, 0 : rows * cols].bitcast(I32).rearrange("p (r c) -> p r c", c=cols),
                 in_=rows_of(codes_img, I32)[:, row : row + rows, col : col + cols],
             )
+
+        def window_of(name):
+            if name[0] == "top":
+                return R, 2 * B_COLS * name[1], PAIR_ROWS, PAIR_COLS
+            if name[0] == "bottom":
+                return R + SIDE - PAIR_ROWS, 2 * B_COLS * name[1], PAIR_ROWS, PAIR_COLS
+            if name[0] == "left":
+                return B_ROWS + 2 * B_ROWS * name[1], R, 14, EDGE_COLS
+            if name[0] == "right":
+                return B_ROWS + 2 * B_ROWS * name[1], R + SIDE - EDGE_COLS, 14, EDGE_COLS
+            return B_ROWS * name[0], B_COLS * name[1], Q_ROWS, Q_COLS
 
         def gather_strip(strip):
             slot = strip % 2
@@ -603,25 +624,22 @@ def tile_dcblock_kernel(
                     ),
                 )
             for bc in range(1, 1 + INNER):
-                window_codes(q_codes[slot][:, bc - 1, :], row, B_COLS * bc, Q_ROWS, Q_COLS)
-                gathered[strip, bc] = (q_codes[slot][:, bc - 1, :], q_plane[slot][:, bc - 1, :])
+                gathered[strip, bc] = q_plane[slot][:, bc - 1, :]
 
         def gather_one(strip, bc):
             slot = strip % 2
             row, col = B_ROWS * strip, B_COLS * bc
-            q, plane = q_codes[slot][:, strip // 2, :], q_plane[slot][:, strip // 2, :]
-            window_codes(q, row, col, Q_ROWS, Q_COLS)
+            plane = q_plane[slot][:, strip // 2, :]
             nc.vector.tensor_copy(
                 out=plane[:, 0:Q_PX].rearrange("p (r c) -> p r c", c=Q_COLS),
                 in_=rows_of(plane_img, U8)[:, row : row + Q_ROWS, col : col + Q_COLS],
             )
-            gathered[strip, bc] = (q, plane)
+            gathered[strip, bc] = plane
 
         def gather_side(side):
             planes_here = rows_of(plane_img, U8)
             if side < 2:
                 row = R if side == 0 else R + SIDE - PAIR_ROWS
-                windows_here = [(row, 2 * B_COLS * m, PAIR_ROWS, PAIR_COLS) for m in range(4)]
                 for third in range(3):
                     col = B_COLS * third
                     start = min(col, B_COLS)
@@ -635,7 +653,6 @@ def tile_dcblock_kernel(
                     )
             else:
                 col = R if side == 2 else R + SIDE - EDGE_COLS
-                windows_here = [(B_ROWS + 2 * B_ROWS * m, col, 14, EDGE_COLS) for m in range(5)]
                 for first_row, n in ((0, 8), (8, 6)):
                     row = B_ROWS + first_row
                     nc.vector.tensor_copy(
@@ -644,9 +661,8 @@ def tile_dcblock_kernel(
                         ),
                         in_=planes_here[:, row : row + 40, col : col + EDGE_COLS].rearrange("p (b r) c -> p b r c", r=8)[:, :, 0:n, :],
                     )
-            for m, window in enumerate(windows_here):
-                window_codes(edge_codes[side][:, m, :], window[0], window[1], window[2], window[3])
-                gathered[SIDES[side], m] = (edge_codes[side][:, m, :], edge_plane[side][:, m, :])
+            for m in range(4 if side < 2 else 5):
+                gathered[SIDES[side], m] = edge_plane[side][:, m, :]
 
         def inner_banks(strip):
             return [
@@ -695,10 +711,10 @@ def tile_dcblock_kernel(
 
         def make_messages(n):
             m, place = blocks[n]
-            q, plane = gathered[bank_list[m][3][place][0]]
+            plane = gathered[bank_list[m][3][place][0]]
             bank = psum_s.tile([P, C], F32, name="bank_s", tag="s")
             nc.tensor.matmul_mx(
-                out=bank[:], lhsT=q.bitcast(FP8X4), lhsT_scale=plane,
+                out=bank[:], lhsT=window_tile[:, n, :].bitcast(FP8X4), lhsT_scale=plane,
                 rhs=feat_codes[:].bitcast(FP8X4), rhs_scale=feat_plane[:], start=True, stop=True,
             )
             messages[n] = message_pool.tile([P, PACK, P], F32, name="messages")
@@ -795,19 +811,19 @@ def tile_dcblock_kernel(
                 plan(step + 1 + place, fuse, t)
                 plan(step + 2 + place, add_x_and_store, t)
 
-        for t in range(CORE_TILES):
-            plan(STEPS + t, normalise, t)
-            plan(STEPS + t + 1, turn, t)
-            plan(STEPS + t + 2, place_core, t)
-        plan_finish(STEPS + 3, (6,))
-        plan_finish(STEPS + 4, (7, 8))
-        plan_finish(STEPS + 6, (9, 10, 11))
+        for t, at in ((3, STEPS - 2), (0, STEPS - 2), (1, STEPS - 1), (2, STEPS)):
+            plan(at, normalise, t)
+            plan(at, turn, t)
+            plan(at + 1, place_core, t)
+        for tile, at in ((11, STEPS), (6, STEPS), (7, STEPS + 1), (8, STEPS + 1), (9, STEPS + 2), (10, STEPS + 2)):
+            plan_finish(at, (tile,))
 
-        nc.sync.dma_start(out=x_res[:], in_=x[0].rearrange("(m p) h w -> p m (h w)", p=P))
         n_block = 0
+        n_gathered = 0
         n_aggregated = 0
         made = {}
         to_collect = []
+        parts = []
         with tc.manual_schedule():
             for step in range(PART_ONE, STEPS + 11):
                 for kind in range(1, 9):
@@ -817,24 +833,28 @@ def tile_dcblock_kernel(
                         spread_edge(kind)
                 if step < STEPS:
                     next_codes(step)
+                if step == PART_ONE + 6:
+                    nc.sync.dma_start(out=x_res[:], in_=x[0].rearrange("(m p) h w -> p m (h w)", p=P))
+                while n_gathered < min(WINDOWS, n_block + CODES_AHEAD):
+                    gather_codes(n_gathered)
+                    n_gathered += 1
 
                 for stage, t in stage_queue.get(step, []):
                     if stage in (add_x_and_store, quantise_agg, place_core, normalise):
                         stage(t)
 
-                for m in to_collect:
+                def collect_now(m):
                     collect_bank(m)
                     plan_finish(step + 1, after_bank.get(m, ()))
+
+                for m in to_collect:
+                    collect_now(m)
                 to_collect = []
 
-                parts = []
                 if step >= FIRST_SUM_STEP:
                     while n_aggregated < made[step - 2]:
                         for j in range(PACK):
                             parts.append((n_aggregated, j))
-                        m, place = blocks[n_aggregated]
-                        if place == len(bank_list[m][3]) - 1:
-                            to_collect.append(m)
                         n_aggregated += 1
                 first_new = n_block
                 if step >= FIRST_BLOCK_STEP:
@@ -843,26 +863,32 @@ def tile_dcblock_kernel(
                 made[step] = n_block
                 for n in range(first_new, min(n_block + GATHER_AHEAD, len(blocks))):
                     gather_for(n)
-                n_mx = (CORE_TILES if step < STEPS else 0) + n_block - first_new
-                shares = [len(parts) * (m + 1) // n_mx - len(parts) * m // n_mx for m in range(n_mx)]
-
-                def some_parts(parts, shares):
-                    count = shares[0]
-                    for n, j in parts[0:count]:
-                        aggregate_part(n, j)
-                    parts[0:count] = []
-                    shares[0:1] = []
-
                 on_vector, on_scalar = product_calls(step) if step < STEPS else ([], [])
+                n_mx = len(on_vector) + len(on_scalar) + n_block - first_new
+                quota = min(len(parts), PARTS_PER_STEP) if step < STEPS else len(parts)
+                shares = [quota * (m + 1) // n_mx - quota * m // n_mx for m in range(n_mx)]
+
+                def emit_parts(count):
+                    for n, j in parts[0:count]:
+                        m, place = blocks[n]
+                        if place == 0 and j == 0 and len(to_collect) > 1:
+                            collect_now(to_collect[0])
+                            to_collect[0:1] = []
+                        aggregate_part(n, j)
+                        if place == len(bank_list[m][3]) - 1 and j == PACK - 1:
+                            to_collect.append(m)
+                    parts[0:count] = []
+
                 for n in range(first_new, n_block):
                     on_scalar.append(lambda n=n: make_messages(n))
                 for m in range(max(len(on_vector), len(on_scalar))):
                     for calls in (on_vector, on_scalar):
                         if m < len(calls):
                             calls[m]()
-                            some_parts(parts, shares)
-                for n, j in parts:
-                    aggregate_part(n, j)
+                            emit_parts(shares[0])
+                            shares[0:1] = []
+                if step >= STEPS:
+                    emit_parts(len(parts))
 
                 if step == PART_ONE:
                     spread_inner()

@@ -22,7 +22,6 @@ PROBS = 19
 R = 3
 KW = 2 * R + 1
 BN_EPS = 1e-5
-STEPS = KW * KW
 
 PITCH = SIDE + 2 * R
 WORDS = 2944
@@ -36,8 +35,8 @@ CORE_USED = 30
 CORE_PX = CORE_ROWS * CORE_COLS
 CORE_TILES = CORE_PX // P
 TILE_ROWS = P // CORE_COLS
-MID_ROWS = CORE_ROWS + 2 * R
-MID_COLS = MID_ROWS * CORE_COLS
+WINDOWS_DJ = CORE_ROWS // TILE_ROWS + 2 * R
+STEPS = KW * WINDOWS_DJ
 
 B_ROWS, B_COLS = 4, 6
 B_PX = B_ROWS * B_COLS
@@ -75,11 +74,12 @@ STORE_ROWS = 32
 BLOCK_ROWS = STORE_ROWS * D
 PARK_PITCH = 3072
 
-PART_ONE = 5
-FIRST_BLOCK_STEP = 5
-FIRST_SUM_STEP = 7
-LAST_BLOCK_STEP = 45
-PARTS_PER_STEP = 7
+FIRST_TURN_STEP = 3
+PART_ONE = 7
+FIRST_BLOCK_STEP = 7
+FIRST_SUM_STEP = 9
+LAST_BLOCK_STEP = 65
+PARTS_PER_STEP = 5
 GATHER_AHEAD = 2
 CODES_AHEAD = 12
 WINDOWS = 58
@@ -111,8 +111,8 @@ def tile_dcblock_kernel(
     nc = tc.nc
     with ExitStack() as ctx:
         keep = ctx.enter_context(tc.tile_pool(name="keep", bufs=1))
-        psum_turns = ctx.enter_context(tc.psum_pool(name="psum_turns", bufs=3))
-        psum_s = ctx.enter_context(tc.psum_pool(name="psum_s", bufs=3))
+        psum_turns = ctx.enter_context(tc.psum_pool(name="psum_turns", bufs=4))
+        psum_s = ctx.enter_context(tc.psum_pool(name="psum_s", bufs=2))
         psum_main = ctx.enter_context(tc.psum_pool(name="psum_main", bufs=2))
 
         ident_f32 = keep.tile([P, P], F32, name="ident_f32")
@@ -124,8 +124,8 @@ def tile_dcblock_kernel(
 
         codes_img = keep.tile([P, WORDS], U32, name="codes_img", align_bytes=64)
         plane_img = keep.tile([P, WORDS], U8, name="plane_img", align_bytes=64)
-        codes = [keep.tile([P, MID_COLS], U32, name="codes%d" % b, align_bytes=64) for b in range(2)]
-        planes = [keep.tile([P, 2, MID_COLS], U8, name="planes%d" % b, align_bytes=64) for b in range(2)]
+        codes = [keep.tile([P, WINDOWS_DJ, P], U32, name="codes%d" % b, align_bytes=64) for b in range(2)]
+        planes = [keep.tile([P, WINDOWS_DJ, P], U8, name="planes%d" % b, align_bytes=64) for b in range(2)]
         q_plane = [keep.tile([P, PER_STRIP, P], U8, name="q_plane%d" % b, align_bytes=64) for b in range(2)]
         acc = [keep.tile([P, PACK, P], F32, name="acc%d" % t) for t in range(CORE_TILES)]
         dist_core = keep.tile([P, CORE_TILES, ROUNDS * SETS * D], F32, name="dist_core")
@@ -162,13 +162,14 @@ def tile_dcblock_kernel(
                 )
             return w_codes, w_plane
 
-        def messages_of_neighbours(bank, b, t, di):
-            col = P * t + CORE_COLS * (di + R)
-            v = (di + R) % 2
-            plane_col = col - CORE_COLS * v
+        core_bank = {}
+
+        def core_messages(step):
+            phase, n = divmod(step, WINDOWS_DJ)
+            core_bank[step] = psum_turns.tile([P, C], F32, name="core_bank", tag="bank")
             nc.tensor.matmul_mx(
-                out=bank[:],
-                lhsT=codes[b][:, col : col + P].bitcast(FP8X4), lhsT_scale=planes[b][:, v, plane_col : plane_col + P],
+                out=core_bank[step][:],
+                lhsT=codes[phase % 2][:, n, :].bitcast(FP8X4), lhsT_scale=planes[phase % 2][:, n, :],
                 rhs=feat_codes[:].bitcast(FP8X4), rhs_scale=feat_plane[:], start=True, stop=True,
             )
 
@@ -178,68 +179,61 @@ def tile_dcblock_kernel(
             j = place_of(di, dj)
             return e_core[:, t, j : j + 1]
 
-        def add_on_vector(b, t, di, dj, is_first):
-            bank = psum_turns.tile([P, C], F32, name="bank_v", tag="bank")
-            messages_of_neighbours(bank, b, t, di)
-            by_place = bank[:].rearrange("p (q j) -> p j q", j=PACK)
-            if is_first:
+        def core_sums(step):
+            phase, n = divmod(step, WINDOWS_DJ)
+            on_vector, on_scalar = [], []
+            for t in range(CORE_TILES):
+                di = n - R - t
+                if -R <= di <= R:
+                    if t == CORE_TILES - 1 and step >= PART_ONE:
+                        on_scalar.append(lambda t=t, di=di: add_on_gpsimd(step, t, di, phase - R))
+                    else:
+                        on_vector.append(lambda t=t, di=di: add_on_vector(step, t, di, phase - R))
+            return on_vector, on_scalar
+
+        def add_on_vector(step, t, di, dj):
+            by_place = core_bank[step][:].rearrange("p (q j) -> p j q", j=PACK)
+            if di == -R and dj == -R:
                 nc.vector.tensor_scalar_mul(out=acc[t][:], in0=by_place, scalar1=weight(t, di, dj))
             else:
                 nc.vector.scalar_tensor_tensor(
                     out=acc[t][:], in0=by_place, scalar=weight(t, di, dj), in1=acc[t][:], op0=ALU.mult, op1=ALU.add
                 )
 
-        def move_codes(dj, b):
-            rows = slice(CORE_ROW * PITCH, (CORE_ROW + MID_ROWS) * PITCH)
-            cols = slice(CORE_COL + R + dj, CORE_COL + R + dj + CORE_COLS)
-            move = nc.vector.tensor_copy if dj == -R else nc.sync.dma_start
-            move(
-                out=codes[b][:].bitcast(I32).rearrange("p (r w) -> p r w", w=CORE_COLS),
-                in_=codes_img[:, rows].bitcast(I32).rearrange("p (r w) -> p r w", w=PITCH)[:, :, cols],
-            )
-            nc.vector.tensor_copy(
-                out=planes[b][:, 0, :].rearrange("p (r w) -> p r w", w=CORE_COLS),
-                in_=plane_img[:, rows].rearrange("p (r w) -> p r w", w=PITCH)[:, :, cols],
-            )
-
-        def move_plane(b):
-            nc.vector.tensor_copy(
-                out=planes[b][:, 1, 0 : MID_COLS - CORE_COLS].bitcast(I32), in_=planes[b][:, 0, CORE_COLS:MID_COLS].bitcast(I32)
-            )
-
-        def next_codes(step):
-            phase, k = divmod(step, KW)
-            if phase < KW - 1 and k == 4:
-                move_codes(phase + 1 - R, (phase + 1) % 2)
-            if phase < KW - 1 and k == 5:
-                move_plane((phase + 1) % 2)
-
-        def add_on_gpsimd(b, t, di, dj):
-            bank = psum_s.tile([P, C], F32, name="bank_s", tag="s")
-            messages_of_neighbours(bank, b, t, di)
+        def add_on_gpsimd(step, t, di, dj):
             product = product_pool.tile([P, PACK, P], F32, name="product")
             nc.scalar.activation(
-                out=product[:], in_=bank[:].rearrange("p (q j) -> p j q", j=PACK), func=ACT.Copy, scale=weight(t, di, dj)
+                out=product[:], in_=core_bank[step][:].rearrange("p (q j) -> p j q", j=PACK), func=ACT.Copy,
+                scale=weight(t, di, dj),
             )
             nc.gpsimd.tensor_tensor(out=acc[t][:], in0=acc[t][:], in1=product[:], op=ALU.add)
 
-        def product_calls(step):
-            phase, k = divmod(step, KW)
-            on_vector, on_scalar = [], []
-            if phase == KW - 1:
-                order = [(t, di) for di in range(-R, R + 1) for t in (0, 1)] + [(2, di) for di in range(-R, R + 1)]
-                for t, di in order[3 * k : 3 * k + 3]:
-                    on_vector.append(lambda t=t, di=di: add_on_vector(phase % 2, t, di, phase - R, False))
-                for m in (2 * k, 2 * k + 1):
-                    if m < KW:
-                        on_scalar.append(lambda m=m: add_on_gpsimd(phase % 2, CORE_TILES - 1, m - R, phase - R))
-                return on_vector, on_scalar
-            for t in range(CORE_TILES):
-                if t == CORE_TILES - 1 and step >= PART_ONE:
-                    on_scalar.append(lambda t=t: add_on_gpsimd(phase % 2, t, k - R, phase - R))
+        def move_codes(dj, b):
+            cols = slice(CORE_COL + R + dj, CORE_COL + R + dj + CORE_COLS)
+            for dst, source, dtype in ((codes[b], codes_img, I32), (planes[b], plane_img, U8)):
+                rows = source[:, 0 : PITCH * PITCH].bitcast(dtype).rearrange("p (r w) -> p r w", w=PITCH)
+                if dst is codes[b] and dj > -R:
+                    for n in range(WINDOWS_DJ):
+                        first_row = CORE_ROW + n
+                        nc.sync.dma_start(
+                            out=dst[:, n, :].bitcast(dtype).rearrange("p (g c) -> p g c", c=CORE_COLS),
+                            in_=rows[:, first_row : first_row + CORE_ROWS - TILE_ROWS + 1 : TILE_ROWS, cols],
+                        )
                 else:
-                    on_vector.append(lambda t=t: add_on_vector(phase % 2, t, k - R, phase - R, step == 0))
-            return on_vector, on_scalar
+                    for n in range(0, WINDOWS_DJ, TILE_ROWS):
+                        count = min(TILE_ROWS, WINDOWS_DJ - n)
+                        first_row = CORE_ROW + n
+                        nc.vector.tensor_copy(
+                            out=dst[:, n : n + count, :].bitcast(dtype).rearrange("p n (g c) -> p g n c", c=CORE_COLS),
+                            in_=rows[:, first_row : first_row + CORE_ROWS, cols].rearrange("p (g n) c -> p g n c", n=TILE_ROWS)[
+                                :, :, 0:count, :
+                            ],
+                        )
+
+        def next_codes(step):
+            phase, n = divmod(step, WINDOWS_DJ)
+            if phase < KW - 1 and n == 4:
+                move_codes(phase + 1 - R, (phase + 1) % 2)
 
         with ExitStack() as ctx_one:
             dist = ctx_one.enter_context(tc.tile_pool(name="dist", bufs=1))
@@ -268,10 +262,12 @@ def tile_dcblock_kernel(
             def subtract_core(engine, u):
                 def core(t):
                     rows = t[:].rearrange("p (h w) -> p h w", w=PAD_PITCH)
-                    return rows[:, CORE_ROW : CORE_ROW + CORE_ROWS, CORE_COL : CORE_COL + CORE_COLS]
+                    return rows[:, CORE_ROW : CORE_ROW + CORE_ROWS, CORE_COL : CORE_COL + CORE_COLS].rearrange(
+                        "p (g r) c -> p r g c", r=TILE_ROWS
+                    )
 
                 engine.tensor_tensor(
-                    out=sq[u][:, 0:CORE_PX].rearrange("p (h w) -> p h w", w=CORE_COLS),
+                    out=sq[u][:, 0:CORE_PX].rearrange("p (r g c) -> p r g c", r=CORE_TILES, c=CORE_COLS),
                     in0=core(shifted[u % SHIFTED_BUFS]), in1=core(centre[u % SLICES]), op=ALU.subtract,
                 )
 
@@ -300,7 +296,7 @@ def tile_dcblock_kernel(
             banks = {}
 
             def turn_squares(half, q):
-                if BANK_ORDER.index((half, q)) % 5 in (1, 3):
+                if BANK_ORDER.index((half, q)) % 2 == 1:
                     banks[half, q] = psum_main.tile([P, 4, P], F32, name="turned_squares", tag="main")
                 else:
                     banks[half, q] = psum_s.tile([P, 4, P], F32, name="turned_squares", tag="s")
@@ -449,7 +445,6 @@ def tile_dcblock_kernel(
                         in_=grouped[:, words, :].rearrange("p w j -> p (w j)"),
                     )
                 move_codes(-R, 0)
-                move_plane(0)
 
             dist_two = ctx_one.enter_context(tc.tile_pool(name="dist_two", bufs=1))
             more_squares(dist_two, 3)
@@ -467,7 +462,7 @@ def tile_dcblock_kernel(
                 turned = 1
                 summed = 1
                 for step in range(PART_ONE):
-                    for u, at, engine in ((2, 0, nc.gpsimd), (3, 0, nc.vector), (4, 1, nc.gpsimd), (5, 1, nc.vector), (6, 2, nc.gpsimd), (7, 2, nc.vector)):
+                    for u, at, engine in ((2, 0, nc.gpsimd), (3, 0, nc.vector), (4, 2, nc.gpsimd), (5, 2, nc.vector), (6, 3, nc.gpsimd), (7, 3, nc.vector)):
                         if step == at:
                             if u >= SHIFTED_BUFS:
                                 load_shifted(u)
@@ -476,11 +471,12 @@ def tile_dcblock_kernel(
                             square_core(u)
                             square_class(u)
                     next_codes(step)
-                    on_vector, on_scalar = product_calls(step)
-                    for m, call in enumerate(on_vector):
+                    core_messages(step)
+                    for m, call in enumerate(core_sums(step)[0]):
                         call()
-                        if step > 0:
-                            goal = min(7 * step, 7 * (step - 1) + 2 * (m + 1))
+                        if step >= FIRST_TURN_STEP:
+                            rounds = step - FIRST_TURN_STEP
+                            goal = min(7 * (rounds + 1), 7 * rounds + 2 * (m + 1))
                             while turned < goal:
                                 turn_squares(BANK_ORDER[turned][0], BANK_ORDER[turned][1])
                                 turned += 1
@@ -769,7 +765,7 @@ def tile_dcblock_kernel(
                 nc.tensor.transpose(out=turned[t][:, j, :], in_=agg[t][:, j, :], identity=ident_bf16[:])
 
         def place_core(t):
-            rows = slice(CORE_ROW + TILE_ROWS * t, CORE_ROW + TILE_ROWS * (t + 1))
+            rows = slice(CORE_ROW + t, CORE_ROW + CORE_ROWS - TILE_ROWS + 1 + t, TILE_ROWS)
             nc.scalar.copy(
                 out=rows_of_agg[:, rows, CORE_COL : CORE_COL + CORE_USED, :],
                 in_=turned[t][:].rearrange("q j (r w) -> q r w j", w=CORE_COLS)[:, :, 0:CORE_USED, :],
@@ -811,12 +807,13 @@ def tile_dcblock_kernel(
                 plan(step + 1 + place, fuse, t)
                 plan(step + 2 + place, add_x_and_store, t)
 
-        for t, at in ((3, STEPS - 2), (0, STEPS - 2), (1, STEPS - 1), (2, STEPS)):
+        for t in range(CORE_TILES):
+            at = STEPS - CORE_TILES + 1 + t
             plan(at, normalise, t)
             plan(at, turn, t)
             plan(at + 1, place_core, t)
-        for tile, at in ((11, STEPS), (6, STEPS), (7, STEPS + 1), (8, STEPS + 1), (9, STEPS + 2), (10, STEPS + 2)):
-            plan_finish(at, (tile,))
+        for place, tile in enumerate(range(6, 12)):
+            plan_finish(STEPS + 3 + place // 2, (tile,))
 
         n_block = 0
         n_gathered = 0
@@ -827,13 +824,13 @@ def tile_dcblock_kernel(
         with tc.manual_schedule():
             for step in range(PART_ONE, STEPS + 11):
                 for kind in range(1, 9):
-                    if step == PART_ONE + kind:
+                    if step == PART_ONE + 2 * kind:
                         mask_edge(kind)
-                    if step == PART_ONE + kind + 1:
+                    if step == PART_ONE + 2 * kind + 1:
                         spread_edge(kind)
                 if step < STEPS:
                     next_codes(step)
-                if step == PART_ONE + 6:
+                if step == PART_ONE + 9:
                     nc.sync.dma_start(out=x_res[:], in_=x[0].rearrange("(m p) h w -> p m (h w)", p=P))
                 while n_gathered < min(WINDOWS, n_block + CODES_AHEAD):
                     gather_codes(n_gathered)
@@ -863,8 +860,10 @@ def tile_dcblock_kernel(
                 made[step] = n_block
                 for n in range(first_new, min(n_block + GATHER_AHEAD, len(blocks))):
                     gather_for(n)
-                on_vector, on_scalar = product_calls(step) if step < STEPS else ([], [])
-                n_mx = len(on_vector) + len(on_scalar) + n_block - first_new
+                mx_calls = [lambda: core_messages(step)] if step < STEPS else []
+                for n in range(first_new, n_block):
+                    mx_calls.append(lambda n=n: make_messages(n))
+                n_mx = len(mx_calls)
                 quota = min(len(parts), PARTS_PER_STEP) if step < STEPS else len(parts)
                 shares = [quota * (m + 1) // n_mx - quota * m // n_mx for m in range(n_mx)]
 
@@ -879,14 +878,13 @@ def tile_dcblock_kernel(
                             to_collect.append(m)
                     parts[0:count] = []
 
-                for n in range(first_new, n_block):
-                    on_scalar.append(lambda n=n: make_messages(n))
-                for m in range(max(len(on_vector), len(on_scalar))):
-                    for calls in (on_vector, on_scalar):
-                        if m < len(calls):
-                            calls[m]()
-                            emit_parts(shares[0])
-                            shares[0:1] = []
+                for call, share in zip(mx_calls, shares):
+                    call()
+                    emit_parts(share)
+                if step < STEPS:
+                    on_vector, on_scalar = core_sums(step)
+                    for call in on_vector + on_scalar:
+                        call()
                 if step >= STEPS:
                     emit_parts(len(parts))
 
@@ -897,7 +895,7 @@ def tile_dcblock_kernel(
                     nc.vector.tensor_reduce(out=inv_sum[:], in_=e_core[:], axis=AXIS.X, op=ALU.add)
                     nc.vector.tensor_scalar_add(out=inv_sum[:], in0=inv_sum[:], scalar1=1.0)
                     nc.vector.reciprocal(out=inv_sum[:], in_=inv_sum[:])
-                if step == PART_ONE + 14:
+                if step == PART_ONE + 24:
                     turn_and_collect((row_lanes, col_lanes))
                 for stage, t in stage_queue.get(step, []):
                     if stage in (fuse, turn):

@@ -74,11 +74,8 @@ STORE_ROWS = 32
 BLOCK_ROWS = STORE_ROWS * D
 PARK_PITCH = 3072
 
-FIRST_TURN_STEP = 3
-PART_ONE = 7
-FIRST_BLOCK_STEP = 7
-FIRST_SUM_STEP = 9
-LAST_BLOCK_STEP = 65
+FIRST_SUM_STEP = 2
+LAST_BLOCK_STEP = 66
 PARTS_PER_STEP = 5
 GATHER_AHEAD = 2
 CODES_AHEAD = 12
@@ -185,7 +182,7 @@ def tile_dcblock_kernel(
             for t in range(CORE_TILES):
                 di = n - R - t
                 if -R <= di <= R:
-                    if t == CORE_TILES - 1 and step >= PART_ONE:
+                    if t == CORE_TILES - 1:
                         on_scalar.append(lambda t=t, di=di: add_on_gpsimd(step, t, di, phase - R))
                     else:
                         on_vector.append(lambda t=t, di=di: add_on_vector(step, t, di, phase - R))
@@ -201,12 +198,14 @@ def tile_dcblock_kernel(
                 )
 
         def add_on_gpsimd(step, t, di, dj):
-            product = product_pool.tile([P, PACK, P], F32, name="product")
+            is_first = di == -R and dj == -R
+            product = acc[t] if is_first else product_pool.tile([P, PACK, P], F32, name="product")
             nc.scalar.activation(
                 out=product[:], in_=core_bank[step][:].rearrange("p (q j) -> p j q", j=PACK), func=ACT.Copy,
                 scale=weight(t, di, dj),
             )
-            nc.gpsimd.tensor_tensor(out=acc[t][:], in0=acc[t][:], in1=product[:], op=ALU.add)
+            if not is_first:
+                nc.gpsimd.tensor_tensor(out=acc[t][:], in0=acc[t][:], in1=product[:], op=ALU.add)
 
         def move_codes(dj, b):
             cols = slice(CORE_COL + R + dj, CORE_COL + R + dj + CORE_COLS)
@@ -459,35 +458,33 @@ def tile_dcblock_kernel(
                 sum_channels(0, 0)
                 exp_core(0)
                 square_class(1)
-                turned = 1
+                for u, engine in ((2, nc.gpsimd), (3, nc.vector), (4, nc.gpsimd), (6, nc.gpsimd)):
+                    if u >= SHIFTED_BUFS:
+                        load_shifted(u)
+                    subtract_core(engine, u)
+                    subtract_class(engine, u)
                 summed = 1
-                for step in range(PART_ONE):
-                    for u, at, engine in ((2, 0, nc.gpsimd), (3, 0, nc.vector), (4, 2, nc.gpsimd), (5, 2, nc.vector), (6, 3, nc.gpsimd), (7, 3, nc.vector)):
-                        if step == at:
-                            if u >= SHIFTED_BUFS:
-                                load_shifted(u)
-                            subtract_core(engine, u)
-                            subtract_class(engine, u)
-                            square_core(u)
-                            square_class(u)
-                    next_codes(step)
-                    core_messages(step)
-                    for m, call in enumerate(core_sums(step)[0]):
-                        call()
-                        if step >= FIRST_TURN_STEP:
-                            rounds = step - FIRST_TURN_STEP
-                            goal = min(7 * (rounds + 1), 7 * rounds + 2 * (m + 1))
-                            while turned < goal:
-                                turn_squares(BANK_ORDER[turned][0], BANK_ORDER[turned][1])
-                                turned += 1
-                            while summed < turned - 2 or (m == 3 and summed < turned):
-                                half, q = BANK_ORDER[summed]
-                                sum_channels(half, q)
-                                if q == 0:
-                                    exp_core(half)
-                                if q == CLASS_BANKS:
-                                    exp_class(half)
-                                summed += 1
+                for half in range(ROUNDS):
+                    for u in range(SLICES * (half + 1), min(SLICES * (half + 2), UNITS)):
+                        square_core(u)
+                        square_class(u)
+                    last = 7 * (half + 1)
+                    for turned in range(max(1, last - 7), last):
+                        turn_squares(BANK_ORDER[turned][0], BANK_ORDER[turned][1])
+                        while summed <= turned - 2 or (turned == last - 1 and summed <= turned):
+                            r, q = BANK_ORDER[summed]
+                            sum_channels(r, q)
+                            if q == 0:
+                                exp_core(r)
+                            if q == CLASS_BANKS:
+                                exp_class(r)
+                            summed += 1
+                    if half < 2:
+                        u = 2 * half + 5
+                        if u >= SHIFTED_BUFS:
+                            load_shifted(u)
+                        subtract_core(nc.vector, u)
+                        subtract_class(nc.vector, u)
             fuse_codes, fuse_plane = load_weight(w_fuse_words, w_fuse_scales, "fuse")
 
         late = ctx.enter_context(tc.tile_pool(name="late", bufs=1))
@@ -780,15 +777,15 @@ def tile_dcblock_kernel(
             )
             agg_mx[t] = (agg_codes, agg_plane)
 
-        def fuse(t):
+        def fuse(t, m):
             agg_codes, agg_plane = agg_mx[t]
-            refined[t] = psum_turns.tile([P, C // P, P], F32, name="refined", tag="bank")
-            for m in range(C // P):
-                nc.tensor.matmul_mx(
-                    out=refined[t][:, m, :],
-                    lhsT=fuse_codes[:, P * m : P * (m + 1)].bitcast(FP8X4), lhsT_scale=fuse_plane[:, P * m : P * (m + 1)],
-                    rhs=agg_codes[:].bitcast(FP8X4), rhs_scale=agg_plane[:], start=True, stop=True,
-                )
+            if m == 0:
+                refined[t] = psum_turns.tile([P, C // P, P], F32, name="refined", tag="bank")
+            nc.tensor.matmul_mx(
+                out=refined[t][:, m, :],
+                lhsT=fuse_codes[:, P * m : P * (m + 1)].bitcast(FP8X4), lhsT_scale=fuse_plane[:, P * m : P * (m + 1)],
+                rhs=agg_codes[:].bitcast(FP8X4), rhs_scale=agg_plane[:], start=True, stop=True,
+            )
 
         def add_x_and_store(t):
             result = late_work.tile([P, C // P, P], F32, name="result")
@@ -822,15 +819,15 @@ def tile_dcblock_kernel(
         to_collect = []
         parts = []
         with tc.manual_schedule():
-            for step in range(PART_ONE, STEPS + 11):
+            for step in range(STEPS + 11):
                 for kind in range(1, 9):
-                    if step == PART_ONE + 2 * kind:
+                    if step == 2 * kind:
                         mask_edge(kind)
-                    if step == PART_ONE + 2 * kind + 1:
+                    if step == 2 * kind + 1:
                         spread_edge(kind)
                 if step < STEPS:
                     next_codes(step)
-                if step == PART_ONE + 9:
+                if step == 9:
                     nc.sync.dma_start(out=x_res[:], in_=x[0].rearrange("(m p) h w -> p m (h w)", p=P))
                 while n_gathered < min(WINDOWS, n_block + CODES_AHEAD):
                     gather_codes(n_gathered)
@@ -854,15 +851,16 @@ def tile_dcblock_kernel(
                             parts.append((n_aggregated, j))
                         n_aggregated += 1
                 first_new = n_block
-                if step >= FIRST_BLOCK_STEP:
-                    span = LAST_BLOCK_STEP - FIRST_BLOCK_STEP
-                    n_block = min(len(blocks), -(-len(blocks) * (step + 1 - FIRST_BLOCK_STEP) // span))
+                n_block = min(len(blocks), -(-len(blocks) * (step + 1) // LAST_BLOCK_STEP))
                 made[step] = n_block
                 for n in range(first_new, min(n_block + GATHER_AHEAD, len(blocks))):
                     gather_for(n)
                 mx_calls = [lambda: core_messages(step)] if step < STEPS else []
                 for n in range(first_new, n_block):
                     mx_calls.append(lambda n=n: make_messages(n))
+                for stage, t in stage_queue.get(step, []):
+                    if stage == fuse:
+                        mx_calls += [lambda t=t, m=m: fuse(t, m) for m in range(C // P)]
                 n_mx = len(mx_calls)
                 quota = min(len(parts), PARTS_PER_STEP) if step < STEPS else len(parts)
                 shares = [quota * (m + 1) // n_mx - quota * m // n_mx for m in range(n_mx)]
@@ -888,15 +886,15 @@ def tile_dcblock_kernel(
                 if step >= STEPS:
                     emit_parts(len(parts))
 
-                if step == PART_ONE:
+                if step == 0:
                     spread_inner()
                     turn_and_collect((inner_lanes,))
-                if step == PART_ONE + 1:
+                if step == 1:
                     nc.vector.tensor_reduce(out=inv_sum[:], in_=e_core[:], axis=AXIS.X, op=ALU.add)
                     nc.vector.tensor_scalar_add(out=inv_sum[:], in0=inv_sum[:], scalar1=1.0)
                     nc.vector.reciprocal(out=inv_sum[:], in_=inv_sum[:])
-                if step == PART_ONE + 24:
+                if step == 24:
                     turn_and_collect((row_lanes, col_lanes))
                 for stage, t in stage_queue.get(step, []):
-                    if stage in (fuse, turn):
+                    if stage == turn:
                         stage(t)

@@ -876,13 +876,15 @@ def tile_dcblock_kernel(
                             to_collect.append(m)
                     parts[0:count] = []
 
-                for call, share in zip(mx_calls, shares):
+                on_vector, on_scalar = core_sums(step) if step < STEPS else ([], [])
+                for m, (call, share) in enumerate(zip(mx_calls, shares)):
                     call()
+                    if m == 0:
+                        for scalar_call in on_scalar:
+                            scalar_call()
                     emit_parts(share)
-                if step < STEPS:
-                    on_vector, on_scalar = core_sums(step)
-                    for call in on_vector + on_scalar:
-                        call()
+                for call in on_vector:
+                    call()
                 if step >= STEPS:
                     emit_parts(len(parts))
 

from contextlib import ExitStack

import concourse.mybir as mybir
from concourse.masks import make_identity

F32 = mybir.dt.float32
BF16 = mybir.dt.bfloat16
I32 = mybir.dt.int32
U32 = mybir.dt.uint32
U8 = mybir.dt.uint8
FP8X4 = mybir.dt.float8_e4m3fn_x4
ALU = mybir.AluOpType
ACT = mybir.ActivationFunctionType
AXIS = mybir.AxisListType

P = 128
PACK = 4
C = 512
SIDE = 48
NPX = SIDE * SIDE
PROBS = 19
R = 3
KW = 2 * R + 1
BN_EPS = 1e-5

PITCH = SIDE + 2 * R
WORDS = 2944
QUANT_CALLS = ((0, 1024), (1024, 1024), (2048, 512), (2560, 256), (2816, 128))
CHUNK_ROWS = 8
THIRD_PX = NPX // 3

CORE_ROW, CORE_COL = 16, 6
CORE_ROWS, CORE_COLS = 16, 32
CORE_USED = 30
CORE_PX = CORE_ROWS * CORE_COLS
CORE_TILES = CORE_PX // P
TILE_ROWS = P // CORE_COLS
WINDOWS_DJ = CORE_ROWS // TILE_ROWS + 2 * R
STEPS = KW * WINDOWS_DJ

B_ROWS, B_COLS = 4, 6
B_PX = B_ROWS * B_COLS
Q_ROWS, Q_COLS = B_ROWS + 2 * R, B_COLS + 2 * R
Q_PX = Q_ROWS * Q_COLS
STRIPS = SIDE // B_ROWS
PER_STRIP = SIDE // B_COLS
LANES = STRIPS * PER_STRIP
INNER = 6
SIDES = ("top", "bottom", "left", "right")
PAIR_ROWS, PAIR_COLS = B_ROWS + R, 2 * B_COLS + 2 * R
EDGE_COLS = B_COLS + R

SETS = 2
D = 6
CH = 10
SLICES = 2
SET_ROWS = 64
ROUNDS = 4
UNITS = ROUNDS * SLICES
BANK_ORDER = [(r, q) for r in range(ROUNDS) for q in range(7)]
CLASS_BANKS = 6
PAD_LEFT = 4
PAD_PITCH = PAD_LEFT + SIDE + 4
PAD_ROWS = SIDE + 2 * R
ROW_LEN = SIDE * PAD_PITCH
RUN = (SIDE - 1) * PAD_PITCH + SIDE
ONE_SIDE = (-3, -2, -1, 1, 2, 3)
SET_ORDER = [KW] + list(range(KW))
CLASS_PX = LANES * B_PX
SQ_COLS = CORE_PX + CLASS_PX + P - LANES
SHIFTED_BUFS = 6

STORE_ROWS = 32
BLOCK_ROWS = STORE_ROWS * D
PARK_PITCH = 3072

FIRST_SUM_STEP = 2
LAST_BLOCK_STEP = 66
PARTS_PER_STEP = 5
GATHER_AHEAD = 2
CODES_AHEAD = 12
WINDOWS = 58

FLOPS = 2 * 2 * C * C * NPX + 2 * KW * KW * C * NPX


def place_of(di, dj):
    if di != 0:
        return D * SET_ORDER.index(dj + R) + ONE_SIDE.index(di)
    return D * SET_ORDER.index(KW) + ONE_SIDE.index(dj)


def tile_dcblock_kernel(
    tc,
    x,
    coarse_probs,
    sigma,
    w_feat_words,
    w_feat_scales,
    w_fuse_words,
    w_fuse_scales,
    bn_gamma,
    bn_beta,
    bn_mean,
    bn_var,
    out,
):
    nc = tc.nc
    with ExitStack() as ctx:
        keep = ctx.enter_context(tc.tile_pool(name="keep", bufs=1))
        psum_turns = ctx.enter_context(tc.psum_pool(name="psum_turns", bufs=4))
        psum_s = ctx.enter_context(tc.psum_pool(name="psum_s", bufs=2))
        psum_main = ctx.enter_context(tc.psum_pool(name="psum_main", bufs=2))

        ident_f32 = keep.tile([P, P], F32, name="ident_f32")
        make_identity(nc, ident_f32[:])
        ident_bf16 = keep.tile([P, P], BF16, name="ident_bf16")
        make_identity(nc, ident_bf16[:])
        minus_one = keep.tile([P, 1], F32, name="minus_one")
        nc.vector.memset(minus_one[:], -1.0)

        codes_img = keep.tile([P, WORDS], U32, name="codes_img", align_bytes=64)
        plane_img = keep.tile([P, WORDS], U8, name="plane_img", align_bytes=64)
        codes = [keep.tile([P, WINDOWS_DJ, P], U32, name="codes%d" % b, align_bytes=64) for b in range(2)]
        planes = [keep.tile([P, WINDOWS_DJ, P], U8, name="planes%d" % b, align_bytes=64) for b in range(2)]
        q_plane = [keep.tile([P, PER_STRIP, P], U8, name="q_plane%d" % b, align_bytes=64) for b in range(2)]
        acc = [keep.tile([P, PACK, P], F32, name="acc%d" % t) for t in range(CORE_TILES)]
        dist_core = keep.tile([P, CORE_TILES, ROUNDS * SETS * D], F32, name="dist_core")
        e_core = keep.tile([P, CORE_TILES, ROUNDS * SETS * D], F32, name="e_core")
        inv_sum = keep.tile([P, CORE_TILES], F32, name="inv_sum")
        dist_class = keep.tile([P, B_PX, ROUNDS * SETS * D], F32, name="dist_class")
        e_class = keep.tile([P, B_PX, 8, 8], F32, name="e_class")
        inv_class = keep.tile([P, B_PX], F32, name="inv_class")
        spread = keep.tile([P, 30 * P], F32, name="spread")
        mask = keep.tile([P, 9], F32, name="mask")
        nc.vector.memset(e_class[:, :, R, R], 1.0)
        nc.gpsimd.memset(spread[:, 0 : B_PX * P], 0.0)
        by_lane = ident_f32[:, 0:LANES].rearrange("p (b c) -> p b c", c=PER_STRIP)
        kinds = [by_lane[:, 1 : STRIPS - 1, 1 : 1 + INNER]]
        for strip in (0, STRIPS - 1):
            for member in range(2):
                kinds.append(by_lane[:, strip : strip + 1, member:PER_STRIP:2])
        for bc in (0, PER_STRIP - 1):
            for member in range(2):
                kinds.append(by_lane[:, 1 + member : STRIPS - 1 : 2, bc : bc + 1])
        for m, kind in enumerate(kinds):
            nc.vector.tensor_reduce(out=mask[:, m : m + 1], in_=kind, axis=AXIS.XY, op=ALU.add)

        def load_weight(words, scales, label):
            w_codes = keep.tile([P, C], U32, name=label + "_codes", align_bytes=64)
            nc.sync.dma_start(out=w_codes[:].bitcast(I32), in_=words[0].rearrange("p n t -> p (n t)").bitcast(I32))
            w_plane = keep.tile([P, C], U8, name=label + "_plane", align_bytes=64)
            nc.vector.memset(w_plane[:].bitcast(I32), 0)
            scale_rows = scales[0].bitcast(I32)
            for quadrant in range(4):
                nc.sync.dma_start(
                    out=w_plane[32 * quadrant : 32 * quadrant + 4, :].bitcast(I32),
                    in_=scale_rows[4 * quadrant : 4 * quadrant + 4, :],
                )
            return w_codes, w_plane

        core_bank = {}

        def core_messages(step):
            phase, n = divmod(step, WINDOWS_DJ)
            core_bank[step] = psum_turns.tile([P, C], F32, name="core_bank", tag="bank")
            nc.tensor.matmul_mx(
                out=core_bank[step][:],
                lhsT=codes[phase % 2][:, n, :].bitcast(FP8X4), lhsT_scale=planes[phase % 2][:, n, :],
                rhs=feat_codes[:].bitcast(FP8X4), rhs_scale=feat_plane[:], start=True, stop=True,
            )

        def weight(t, di, dj):
            if di == 0 and dj == 0:
                return 1.0
            j = place_of(di, dj)
            return e_core[:, t, j : j + 1]

        def core_sums(step):
            phase, n = divmod(step, WINDOWS_DJ)
            on_vector, on_scalar = [], []
            for t in range(CORE_TILES):
                di = n - R - t
                if -R <= di <= R:
                    if t == CORE_TILES - 1:
                        on_scalar.append(lambda t=t, di=di: add_on_gpsimd(step, t, di, phase - R))
                    else:
                        on_vector.append(lambda t=t, di=di: add_on_vector(step, t, di, phase - R))
            return on_vector, on_scalar

        def add_on_vector(step, t, di, dj):
            by_place = core_bank[step][:].rearrange("p (q j) -> p j q", j=PACK)
            if di == -R and dj == -R:
                nc.vector.tensor_scalar_mul(out=acc[t][:], in0=by_place, scalar1=weight(t, di, dj))
            else:
                nc.vector.scalar_tensor_tensor(
                    out=acc[t][:], in0=by_place, scalar=weight(t, di, dj), in1=acc[t][:], op0=ALU.mult, op1=ALU.add
                )

        def add_on_gpsimd(step, t, di, dj):
            is_first = di == -R and dj == -R
            product = acc[t] if is_first else product_pool.tile([P, PACK, P], F32, name="product")
            nc.scalar.activation(
                out=product[:], in_=core_bank[step][:].rearrange("p (q j) -> p j q", j=PACK), func=ACT.Copy,
                scale=weight(t, di, dj),
            )
            if not is_first:
                nc.gpsimd.tensor_tensor(out=acc[t][:], in0=acc[t][:], in1=product[:], op=ALU.add)

        def move_codes(dj, b):
            cols = slice(CORE_COL + R + dj, CORE_COL + R + dj + CORE_COLS)
            for dst, source, dtype in ((codes[b], codes_img, I32), (planes[b], plane_img, U8)):
                rows = source[:, 0 : PITCH * PITCH].bitcast(dtype).rearrange("p (r w) -> p r w", w=PITCH)
                if dst is codes[b] and dj > -R:
                    for n in range(WINDOWS_DJ):
                        first_row = CORE_ROW + n
                        nc.sync.dma_start(
                            out=dst[:, n, :].bitcast(dtype).rearrange("p (g c) -> p g c", c=CORE_COLS),
                            in_=rows[:, first_row : first_row + CORE_ROWS - TILE_ROWS + 1 : TILE_ROWS, cols],
                        )
                else:
                    for n in range(0, WINDOWS_DJ, TILE_ROWS):
                        count = min(TILE_ROWS, WINDOWS_DJ - n)
                        first_row = CORE_ROW + n
                        nc.vector.tensor_copy(
                            out=dst[:, n : n + count, :].bitcast(dtype).rearrange("p n (g c) -> p g n c", c=CORE_COLS),
                            in_=rows[:, first_row : first_row + CORE_ROWS, cols].rearrange("p (g n) c -> p g n c", n=TILE_ROWS)[
                                :, :, 0:count, :
                            ],
                        )

        def next_codes(step):
            phase, n = divmod(step, WINDOWS_DJ)
            if phase < KW - 1 and n == 4:
                move_codes(phase + 1 - R, (phase + 1) % 2)

        with ExitStack() as ctx_one:
            dist = ctx_one.enter_context(tc.tile_pool(name="dist", bufs=1))
            centre = [dist.tile([P, ROW_LEN], BF16, name="centre%d" % s) for s in range(SLICES)]
            shifted = [dist.tile([P, ROW_LEN], BF16, name="shifted%d" % b) for b in range(SHIFTED_BUFS)]
            sq = []

            def more_squares(pool, n):
                for b in range(len(sq), len(sq) + n):
                    tile = pool.tile([P, SQ_COLS], F32, name="sq%d" % b)
                    nc.vector.memset(tile[:, CORE_PX + CLASS_PX : SQ_COLS], 0.0)
                    sq.append(tile)

            more_squares(dist, UNITS - 3)

            def load_shifted(u):
                half, s = divmod(u, SLICES)
                for pos in range(SETS):
                    g = SET_ORDER[SETS * half + pos]
                    start = PAD_LEFT + g - R if g < KW else 2 * R + 1
                    rows = parked_of(2 if g < KW else 0, s)
                    nc.sync.dma_start(
                        out=shifted[u % SHIFTED_BUFS][SET_ROWS * pos : SET_ROWS * (pos + 1), 0:RUN], in_=rows[:, start : start + RUN]
                    )

            def subtract_core(engine, u):
                def core(t):
                    rows = t[:].rearrange("p (h w) -> p h w", w=PAD_PITCH)
                    return rows[:, CORE_ROW : CORE_ROW + CORE_ROWS, CORE_COL : CORE_COL + CORE_COLS].rearrange(
                        "p (g r) c -> p r g c", r=TILE_ROWS
                    )

                engine.tensor_tensor(
                    out=sq[u][:, 0:CORE_PX].rearrange("p (r g c) -> p r g c", r=CORE_TILES, c=CORE_COLS),
                    in0=core(shifted[u % SHIFTED_BUFS]), in1=core(centre[u % SLICES]), op=ALU.subtract,
                )

            def subtract_class(engine, u):
                a, c, d = shifted[u % SHIFTED_BUFS], centre[u % SLICES], sq[u]

                def class_row(t, i):
                    rows = t[:].rearrange("p (b i w) -> p b i w", i=B_ROWS, w=PAD_PITCH)
                    return rows[:, :, i, 0:SIDE].rearrange("p b (c j) -> p j b c", j=B_COLS)

                for i in range(B_ROWS):
                    first_col = CORE_PX + LANES * B_COLS * i
                    engine.tensor_tensor(
                        out=d[:, first_col : first_col + LANES * B_COLS].rearrange("p (j b c) -> p j b c", j=B_COLS, c=PER_STRIP),
                        in0=class_row(a, i), in1=class_row(c, i), op=ALU.subtract,
                    )

            def square_core(u):
                d = sq[u]
                nc.scalar.activation(out=d[:, 0:CORE_PX], in_=d[:, 0:CORE_PX], func=ACT.Square)

            def square_class(u):
                d = sq[u]
                nc.scalar.activation(out=d[:, CORE_PX:SQ_COLS], in_=d[:, CORE_PX:SQ_COLS], func=ACT.Square)

            banks = {}

            def turn_squares(half, q):
                if BANK_ORDER.index((half, q)) % 2 == 1:
                    banks[half, q] = psum_main.tile([P, 4, P], F32, name="turned_squares", tag="main")
                else:
                    banks[half, q] = psum_s.tile([P, 4, P], F32, name="turned_squares", tag="s")
                for m in range(4):
                    first_col = P * m if q == 0 else CORE_PX + LANES * (4 * (q - 1) + m)
                    for s in range(SLICES):
                        nc.tensor.matmul(
                            out=banks[half, q][:, m, :], lhsT=sq[SLICES * half + s][:, first_col : first_col + P],
                            rhs=ident_f32[:], is_transpose=True, start=(s == 0), stop=(s == SLICES - 1),
                        )

            def sum_channels(half, q):
                dst = dist_core[:] if q == 0 else dist_class[:, 4 * (q - 1) : 4 * q, :]
                nc.vector.tensor_reduce(
                    out=dst[:, :, SETS * D * half : SETS * D * (half + 1)].rearrange("p m (g d) -> p m g d", d=D),
                    in_=banks[half, q][:].rearrange("p m (g r) -> p m g r", r=SET_ROWS)[:, :, :, 0 : CH * D].rearrange(
                        "p m g (c d) -> p m g d c", d=D
                    ),
                    axis=AXIS.X, op=ALU.add,
                )

            def exp_core(half):
                cols = slice(SETS * D * half, SETS * D * (half + 1))
                nc.scalar.activation(out=dist_core[:, :, cols], in_=dist_core[:, :, cols], func=ACT.Exp, scale=neg_inv_denom[:, 0:1])
                nc.scalar.activation(out=e_core[:, :, cols], in_=dist_core[:, :, cols], func=ACT.Exp, bias=minus_one[:, 0:1])

            def exp_class(half):
                cols = slice(SETS * D * half, SETS * D * (half + 1))
                nc.scalar.activation(out=dist_class[:, :, cols], in_=dist_class[:, :, cols], func=ACT.Exp, scale=neg_inv_denom[:, 0:1])
                first_set = SETS * half
                if half == 0:
                    nc.scalar.activation(
                        out=e_class[:, :, R, :].rearrange("p k (s r) -> p k s r", s=2)[:, :, :, 0:R],
                        in_=dist_class[:, :, 0:D].rearrange("p k (s r) -> p k s r", s=2), func=ACT.Exp, bias=minus_one[:, 0:1],
                    )
                    first_set = 1
                last_set = SETS * (half + 1)
                sets = dist_class[:, :, D * first_set : D * last_set].rearrange("p k (g s r) -> p k s r g", s=2, r=R)
                for side in range(2):
                    row = (R + 1) * side
                    nc.scalar.activation(
                        out=e_class[:, :, row : row + R, first_set - 1 : last_set - 1], in_=sets[:, :, side], func=ACT.Exp,
                        bias=minus_one[:, 0:1],
                    )

            with tc.tile_pool(name="early", bufs=1) as first:
                padded = first.tile([P, PAD_ROWS, PAD_PITCH], BF16, name="padded")
                nc.vector.memset(padded[:].rearrange("c h w -> c (h w)").bitcast(I32), 0)
                for channels in (slice(0, 16), slice(16, PROBS)):
                    nc.sync.dma_start(
                        out=padded[4 * channels.start : 4 * channels.stop : 4, R : R + SIDE, PAD_LEFT : PAD_LEFT + SIDE],
                        in_=coarse_probs[0, channels],
                    )
                sigma_bf = first.tile([P, 1], BF16, name="sigma_bf")
                nc.scalar.dma_start(out=sigma_bf[:], in_=sigma.partition_broadcast(P))
                bn_in = {}
                for label, vec in (("var", bn_var), ("gamma", bn_gamma), ("mean", bn_mean), ("beta", bn_beta)):
                    bn_in[label] = first.tile([P, PACK], BF16, name="bn_" + label)
                    nc.scalar.dma_start(out=bn_in[label][:], in_=vec.rearrange("(p j) -> p j", j=PACK))
                xn = first.tile([P, PACK, NPX], BF16, name="xn")
                grouped = first.tile([P, WORDS, PACK], BF16, name="grouped", align_bytes=64)
                x_by_word = x[0].rearrange("(p j) h w -> p j (h w)", j=PACK)
                for third in range(3):
                    px = slice(THIRD_PX * third, THIRD_PX * (third + 1))
                    nc.sync.dma_start(out=xn[:, :, px], in_=x_by_word[:, :, px])

                parked = out[0].rearrange("c h w -> (c h w)").bitcast(BF16).rearrange("(r n) -> r n", n=PARK_PITCH)

                def parked_of(block, s):
                    first_row = BLOCK_ROWS * block + CH * D * s
                    return parked[first_row : first_row + SET_ROWS, :]

                flat = padded[0:P:4].rearrange("c h w -> c (h w)")
                for block in (0, 1, 2):
                    rows = parked[BLOCK_ROWS * block : BLOCK_ROWS * (block + 1), :].rearrange("(c d) n -> c d n", d=D)
                    for d in range(D):
                        row0 = R + ONE_SIDE[d] if block == 2 else R
                        at = R - ONE_SIDE[d] if block == 0 else 0
                        nc.sync.dma_start(
                            out=rows[:, d, at : at + ROW_LEN], in_=flat[:, PAD_PITCH * row0 : PAD_PITCH * row0 + ROW_LEN]
                        )

                def load_centre(s):
                    for pos in range(SETS):
                        nc.sync.dma_start(
                            out=centre[s][SET_ROWS * pos : SET_ROWS * (pos + 1), 0:RUN],
                            in_=parked_of(1, s)[:, PAD_LEFT : PAD_LEFT + RUN],
                        )

                for u in range(SHIFTED_BUFS):
                    if u < SLICES:
                        load_centre(u)
                    load_shifted(u)
                feat_codes, feat_plane = load_weight(w_feat_words, w_feat_scales, "feat")

                neg_inv_denom = keep.tile([P, 1], F32, name="neg_inv_denom")
                nc.vector.tensor_scalar_max(out=neg_inv_denom[:], in0=sigma_bf[:], scalar1=0.0)
                nc.vector.tensor_mul(out=neg_inv_denom[:], in0=neg_inv_denom[:], in1=neg_inv_denom[:])
                nc.vector.tensor_scalar(
                    out=neg_inv_denom[:], in0=neg_inv_denom[:], scalar1=-2.0, scalar2=-1e-8, op0=ALU.mult, op1=ALU.add
                )
                nc.vector.reciprocal(out=neg_inv_denom[:], in_=neg_inv_denom[:])
                bn_scale = keep.tile([P, PACK], F32, name="bn_scale")
                bn_shift = keep.tile([P, PACK], F32, name="bn_shift")
                nc.vector.tensor_scalar_add(out=bn_scale[:], in0=bn_in["var"][:], scalar1=BN_EPS)
                nc.scalar.sqrt(out=bn_scale[:], in_=bn_scale[:])
                nc.vector.reciprocal(out=bn_scale[:], in_=bn_scale[:])
                nc.vector.tensor_mul(out=bn_scale[:], in0=bn_scale[:], in1=bn_in["gamma"][:])
                nc.vector.tensor_mul(out=bn_shift[:], in0=bn_scale[:], in1=bn_in["mean"][:])
                nc.vector.tensor_sub(out=bn_shift[:], in0=bn_in["beta"][:], in1=bn_shift[:])

                top = R * PITCH + R
                nc.vector.memset(grouped[:, 0:top, :], 0.0)
                nc.vector.memset(grouped[:, (R + SIDE) * PITCH - R : WORDS, :], 0.0)
                between = grouped[:, top + SIDE : top + SIDE + (SIDE - 1) * PITCH, :].rearrange("p (r w) j -> p r w j", w=PITCH)
                nc.vector.memset(between[:, :, 0 : 2 * R, :], 0.0)
                nc.gpsimd.memset(plane_img[:].bitcast(I32), 0)
                for b in range(2):
                    nc.gpsimd.memset(q_plane[b][:].bitcast(I32), 0)

                for third in range(3):
                    px = slice(THIRD_PX * third, THIRD_PX * (third + 1))
                    for j in range(PACK):
                        if j == 0:
                            nc.scalar.activation(
                                out=xn[:, j, px], in_=xn[:, j, px], func=ACT.Identity,
                                scale=bn_scale[:, j : j + 1], bias=bn_shift[:, j : j + 1],
                            )
                        else:
                            nc.vector.tensor_scalar(
                                out=xn[:, j, px], in0=xn[:, j, px],
                                scalar1=bn_scale[:, j : j + 1], scalar2=bn_shift[:, j : j + 1], op0=ALU.mult, op1=ALU.add,
                            )
                image = grouped[:, top : top + SIDE * PITCH, :].rearrange("p (r w) j -> p r w j", w=PITCH)
                for chunk in range(SIDE // CHUNK_ROWS):
                    rows = slice(CHUNK_ROWS * chunk, CHUNK_ROWS * (chunk + 1))
                    engine_copy = nc.scalar.copy if chunk in (0, 5) else nc.vector.tensor_copy
                    engine_copy(
                        out=image[:, rows, 0:SIDE, :],
                        in_=xn[:, :, SIDE * rows.start : SIDE * rows.stop].rearrange("p j (r w) -> p r w j", w=SIDE),
                    )
                for first_word, n in QUANT_CALLS:
                    words = slice(first_word, first_word + n)
                    nc.vector.quantize_mx(
                        out=codes_img[:, words].bitcast(FP8X4), scales=plane_img[:, words],
                        in_=grouped[:, words, :].rearrange("p w j -> p (w j)"),
                    )
                move_codes(-R, 0)

            dist_two = ctx_one.enter_context(tc.tile_pool(name="dist_two", bufs=1))
            more_squares(dist_two, 3)
            with tc.manual_schedule():
                for u in (0, 1):
                    subtract_core(nc.vector, u)
                    square_core(u)
                subtract_class(nc.vector, 0)
                square_class(0)
                turn_squares(0, 0)
                subtract_class(nc.vector, 1)
                sum_channels(0, 0)
                exp_core(0)
                square_class(1)
                for u, engine in ((2, nc.gpsimd), (3, nc.vector), (4, nc.gpsimd), (6, nc.gpsimd)):
                    if u >= SHIFTED_BUFS:
                        load_shifted(u)
                    subtract_core(engine, u)
                    subtract_class(engine, u)
                summed = 1
                for half in range(ROUNDS):
                    for u in range(SLICES * (half + 1), min(SLICES * (half + 2), UNITS)):
                        square_core(u)
                        square_class(u)
                    last = 7 * (half + 1)
                    for turned in range(max(1, last - 7), last):
                        turn_squares(BANK_ORDER[turned][0], BANK_ORDER[turned][1])
                        while summed <= turned - 2 or (turned == last - 1 and summed <= turned):
                            r, q = BANK_ORDER[summed]
                            sum_channels(r, q)
                            if q == 0:
                                exp_core(r)
                            if q == CLASS_BANKS:
                                exp_class(r)
                            summed += 1
                    if half < 2:
                        u = 2 * half + 5
                        if u >= SHIFTED_BUFS:
                            load_shifted(u)
                        subtract_core(nc.vector, u)
                        subtract_class(nc.vector, u)
            fuse_codes, fuse_plane = load_weight(w_fuse_words, w_fuse_scales, "fuse")

        late = ctx.enter_context(tc.tile_pool(name="late", bufs=1))
        late_work = ctx.enter_context(tc.tile_pool(name="late_work", bufs=5))
        mask_pool = ctx.enter_context(tc.tile_pool(name="mask_pool", bufs=3))
        product_pool = ctx.enter_context(tc.tile_pool(name="product_pool", bufs=8))
        message_pool = ctx.enter_context(tc.tile_pool(name="message_pool", bufs=8))
        out_by_tile = out[0].rearrange("(m p) h w -> p m (h w)", p=P)
        weights = late.tile([P, LANES, B_PX], F32, name="weights")
        window_tile = late.tile([P, WINDOWS, P], U32, name="window_tile", align_bytes=64)
        nc.gpsimd.memset(window_tile[:, :, Q_PX:P], 0)
        edge_plane = []
        for side in range(4):
            n = 4 if side < 2 else 5
            edge_plane.append(late.tile([P, n, P], U8, name="edge_plane%d" % side, align_bytes=64))
            nc.gpsimd.memset(edge_plane[side][:].bitcast(I32), 0)
        agg_img = late.tile([P, NPX, PACK], BF16, name="agg_img", align_bytes=64)
        x_res = late.tile([P, C // P, NPX], BF16, name="x_res")

        seven = e_class[:, :, 0:KW, 0:KW]

        def windows(base, hop, n, pitch, rows, cols):
            view = spread[:, base : base + n * hop].rearrange("p (n f) -> p n f", f=hop)[:, :, 0 : pitch * rows]
            return view.rearrange("p n (r c) -> p n r c", c=pitch)[:, :, :, 0:cols]

        def spread_inner():
            nc.vector.tensor_reduce(out=inv_class[:], in_=seven, axis=AXIS.XY, op=ALU.add)
            nc.vector.reciprocal(out=inv_class[:], in_=inv_class[:])
            nc.vector.tensor_tensor(
                out=seven, in0=seven, in1=inv_class[:].unsqueeze(2).unsqueeze(3).to_broadcast([P, B_PX, KW, KW]), op=ALU.mult
            )
            for i in range(B_ROWS):
                nc.vector.tensor_scalar_mul(
                    out=windows(B_COLS * P * i + Q_COLS * i, P + 1, B_COLS, Q_COLS, KW, KW),
                    in0=seven[:, B_COLS * i : B_COLS * (i + 1)], scalar1=mask[:, 0:1],
                )

        masked_e = {}

        def mask_edge(kind):
            masked_e[kind] = mask_pool.tile([P, B_PX, KW, KW], F32, name="masked_e")
            nc.scalar.activation(out=masked_e[kind][:], in_=seven, func=ACT.Copy, scale=mask[:, kind : kind + 1])

        def spread_edge(kind):
            side, member = divmod(kind - 1, 2)
            masked = masked_e[kind]
            calls = []
            if side < 2:
                for i in range(B_ROWS):
                    rows = slice(R - i, KW) if side == 0 else slice(0, KW - i)
                    row0 = 0 if side == 0 else i
                    calls.append((
                        windows(B_COLS * P * i + PAIR_COLS * row0 + B_COLS * member, P + 1, B_COLS, PAIR_COLS, rows.stop - rows.start, KW),
                        masked[:, B_COLS * i : B_COLS * (i + 1), rows, :],
                    ))
            else:
                for j in range(B_COLS):
                    cols = slice(max(0, R - j), KW) if side == 2 else slice(0, min(KW, EDGE_COLS - j))
                    col0 = max(0, j - R) if side == 2 else j
                    calls.append((
                        windows(P * j + EDGE_COLS * B_ROWS * member + col0, B_COLS * P + EDGE_COLS, B_ROWS, EDGE_COLS, KW, cols.stop - cols.start),
                        masked[:, j : B_PX : B_COLS, :, cols],
                    ))
            for place, e in calls:
                nc.gpsimd.tensor_tensor(out=place, in0=place, in1=e, op=ALU.add)

        turned_class = {}

        def turn_class(q):
            turned_class[q] = psum_turns.tile([P, 4, P], F32, name="turned_class", tag="bank")
            for m in range(4):
                nc.tensor.transpose(out=turned_class[q][:, m, :], in_=spread[:, P * (4 * q + m) : P * (4 * q + m + 1)], identity=ident_f32[:])

        def collect_class(q, lanes_of):
            nc.scalar.copy(
                out=lanes_of(weights[:, :, 4 * q : 4 * q + 4].rearrange("q (b c) m -> q b c m", c=PER_STRIP)),
                in_=lanes_of(turned_class[q][:, :, 0:LANES].rearrange("q m (b c) -> q b c m", c=PER_STRIP)),
            )

        def inner_lanes(v):
            return v[:, 1 : STRIPS - 1, 1 : 1 + INNER, :]

        def row_lanes(v):
            return v[:, 0 : STRIPS : STRIPS - 1, :, :]

        def col_lanes(v):
            return v[:, 1 : STRIPS - 1, 0 : PER_STRIP : PER_STRIP - 1, :]

        def turn_and_collect(lane_sets):
            for q in range(B_PX // 4):
                turn_class(q)
                for lanes_of in lane_sets:
                    collect_class(q, lanes_of)

        gathered = {}

        def rows_of(source, dtype):
            return source[:, 0 : PITCH * PITCH].bitcast(dtype).rearrange("p (r w) -> p r w", w=PITCH)

        def gather_codes(n):
            name = bank_list[blocks[n][0]][3][blocks[n][1]][0]
            row, col, rows, cols = window_of(name)
            nc.sync.dma_start(
                out=window_tile[:, n, 0 : rows * cols].bitcast(I32).rearrange("p (r c) -> p r c", c=cols),
                in_=rows_of(codes_img, I32)[:, row : row + rows, col : col + cols],
            )

        def window_of(name):
            if name[0] == "top":
                return R, 2 * B_COLS * name[1], PAIR_ROWS, PAIR_COLS
            if name[0] == "bottom":
                return R + SIDE - PAIR_ROWS, 2 * B_COLS * name[1], PAIR_ROWS, PAIR_COLS
            if name[0] == "left":
                return B_ROWS + 2 * B_ROWS * name[1], R, 14, EDGE_COLS
            if name[0] == "right":
                return B_ROWS + 2 * B_ROWS * name[1], R + SIDE - EDGE_COLS, 14, EDGE_COLS
            return B_ROWS * name[0], B_COLS * name[1], Q_ROWS, Q_COLS

        def gather_strip(strip):
            slot = strip % 2
            row = B_ROWS * strip
            for half in range(2):
                col = B_COLS * (1 + half)
                nc.vector.tensor_copy(
                    out=q_plane[slot][:, 0:INNER, 0:Q_PX].rearrange("p b (r c) -> p b r c", c=Q_COLS)[
                        :, :, :, B_COLS * half : B_COLS * (half + 1)
                    ],
                    in_=rows_of(plane_img, U8)[:, row : row + Q_ROWS, col : col + B_COLS * INNER].rearrange(
                        "p r (b c) -> p b r c", c=B_COLS
                    ),
                )
            for bc in range(1, 1 + INNER):
                gathered[strip, bc] = q_plane[slot][:, bc - 1, :]

        def gather_one(strip, bc):
            slot = strip % 2
            row, col = B_ROWS * strip, B_COLS * bc
            plane = q_plane[slot][:, strip // 2, :]
            nc.vector.tensor_copy(
                out=plane[:, 0:Q_PX].rearrange("p (r c) -> p r c", c=Q_COLS),
                in_=rows_of(plane_img, U8)[:, row : row + Q_ROWS, col : col + Q_COLS],
            )
            gathered[strip, bc] = plane

        def gather_side(side):
            planes_here = rows_of(plane_img, U8)
            if side < 2:
                row = R if side == 0 else R + SIDE - PAIR_ROWS
                for third in range(3):
                    col = B_COLS * third
                    start = min(col, B_COLS)
                    nc.vector.tensor_copy(
                        out=edge_plane[side][:, :, 0 : PAIR_ROWS * PAIR_COLS].rearrange("p b (r c) -> p b r c", c=PAIR_COLS)[
                            :, :, :, col : col + B_COLS
                        ],
                        in_=planes_here[:, row : row + PAIR_ROWS, start : start + SIDE].rearrange(
                            "p r (b c) -> p b r c", c=2 * B_COLS
                        )[:, :, :, col - start : col - start + B_COLS],
                    )
            else:
                col = R if side == 2 else R + SIDE - EDGE_COLS
                for first_row, n in ((0, 8), (8, 6)):
                    row = B_ROWS + first_row
                    nc.vector.tensor_copy(
                        out=edge_plane[side][:, :, EDGE_COLS * first_row : EDGE_COLS * (first_row + n)].rearrange(
                            "p b (r c) -> p b r c", c=EDGE_COLS
                        ),
                        in_=planes_here[:, row : row + 40, col : col + EDGE_COLS].rearrange("p (b r) c -> p b r c", r=8)[:, :, 0:n, :],
                    )
            for m in range(4 if side < 2 else 5):
                gathered[SIDES[side], m] = edge_plane[side][:, m, :]

        def inner_banks(strip):
            return [
                ("wide", B_ROWS * strip, B_COLS * bc, [((strip, b), PER_STRIP * strip + b, 1) for b in range(bc, bc + 3)])
                for bc in (1, 4)
            ]

        def row_banks(side):
            lane = 0 if side == 0 else LANES - PER_STRIP
            row = 0 if side == 0 else SIDE - B_ROWS
            return [
                ("wide", row, 4 * B_COLS * h, [((SIDES[side], m), lane + 2 * m, 2) for m in (2 * h, 2 * h + 1)]) for h in range(2)
            ]

        def col_bank(side, pairs):
            lane = PER_STRIP if side == 2 else 2 * PER_STRIP - 1
            col = 0 if side == 2 else SIDE - B_COLS
            return ("tall", B_ROWS + 2 * B_ROWS * pairs[0], col, [((SIDES[side], m), lane + 2 * PER_STRIP * m, 2) for m in pairs])

        core_end = CORE_COL + CORE_USED
        leftover = ("tall", CORE_ROW, core_end, [((st, core_end // B_COLS), PER_STRIP * st + core_end // B_COLS, 1) for st in range(4, 8)])
        bank_list = []
        for strip in (1, 2, 3, 8):
            bank_list += inner_banks(strip)
        bank_list += row_banks(0) + [col_bank(2, (0, 1)), col_bank(3, (0, 1))]
        after_bank = {len(bank_list) - 1: range(0, 6)}
        for strip in (9, 10):
            bank_list += inner_banks(strip)
        bank_list += row_banks(1) + [col_bank(2, (3, 4)), col_bank(3, (3, 4))]
        after_bank[len(bank_list) - 1] = range(12, 18)
        bank_list += [col_bank(2, (2,)), col_bank(3, (2,)), leftover]
        blocks = [(m, place) for m in range(len(bank_list)) for place in range(len(bank_list[m][3]))]

        def gather_for(n):
            name = bank_list[blocks[n][0]][3][blocks[n][1]][0]
            if name not in gathered:
                if name[0] in SIDES:
                    gather_side(SIDES.index(name[0]))
                elif 4 <= name[0] < 8:
                    gather_one(name[0], name[1])
                else:
                    gather_strip(name[0])

        messages = {}
        main_bank = {}

        def make_messages(n):
            m, place = blocks[n]
            plane = gathered[bank_list[m][3][place][0]]
            bank = psum_s.tile([P, C], F32, name="bank_s", tag="s")
            nc.tensor.matmul_mx(
                out=bank[:], lhsT=window_tile[:, n, :].bitcast(FP8X4), lhsT_scale=plane,
                rhs=feat_codes[:].bitcast(FP8X4), rhs_scale=feat_plane[:], start=True, stop=True,
            )
            messages[n] = message_pool.tile([P, PACK, P], F32, name="messages")
            nc.scalar.copy(out=messages[n][:], in_=bank[:].rearrange("p (q j) -> p j q", j=PACK))

        def aggregate_part(n, j):
            m, place = blocks[n]
            shape, row, col, members = bank_list[m]
            name, lane, count = members[place]
            if place == 0 and j == 0:
                main_bank[m] = psum_main.tile([P, PACK, 96], F32, name="main_bank", tag="main")
            px = count * B_PX
            bank = main_bank[m][:, j, 0 : px * len(members)]
            if shape == "tall":
                dst = bank[:, px * place : px * (place + 1)].rearrange("p (l k) -> p l k", k=B_PX)
                rhs = weights[:, lane : lane + PER_STRIP * (count - 1) + 1 : PER_STRIP, :]
            else:
                rhs = weights[:, lane : lane + count, :]
                width = B_COLS * count
                dst = bank.rearrange("p (i w) -> p i w", i=B_ROWS)[:, :, width * place : width * (place + 1)].rearrange(
                    "p i (l j) -> p l i j", j=B_COLS
                )
                rhs = rhs.rearrange("q l (i j) -> q l i j", j=B_COLS)
            nc.tensor.matmul(out=dst, lhsT=messages[n][:, j, :], rhs=rhs, start=True, stop=True)

        rows_of_agg = agg_img[:].rearrange("p (r w) j -> p r w j", w=SIDE)

        def collect_bank(m):
            shape, row, col, members = bank_list[m]
            px = sum([count for name, lane, count in members]) * B_PX
            n_rows = B_ROWS if shape == "wide" else px // B_COLS
            width = px // n_rows
            nc.scalar.copy(
                out=rows_of_agg[:, row : row + n_rows, col : col + width, :],
                in_=main_bank[m][:, :, 0:px].rearrange("p j (r w) -> p r w j", w=width),
            )

        agg = {}
        turned = {}
        agg_mx = {}
        refined = {}

        def normalise(t):
            agg[t] = late_work.tile([P, PACK, P], BF16, name="agg")
            nc.scalar.activation(
                out=agg[t][:], in_=acc[t][:], func=ACT.Copy, scale=inv_sum[:, t : t + 1]
            )

        def turn(t):
            turned[t] = psum_turns.tile([P, PACK, P], BF16, name="turned", tag="bank")
            for j in range(PACK):
                nc.tensor.transpose(out=turned[t][:, j, :], in_=agg[t][:, j, :], identity=ident_bf16[:])

        def place_core(t):
            rows = slice(CORE_ROW + t, CORE_ROW + CORE_ROWS - TILE_ROWS + 1 + t, TILE_ROWS)
            nc.scalar.copy(
                out=rows_of_agg[:, rows, CORE_COL : CORE_COL + CORE_USED, :],
                in_=turned[t][:].rearrange("q j (r w) -> q r w j", w=CORE_COLS)[:, :, 0:CORE_USED, :],
            )

        def quantise_agg(t):
            agg_codes = late_work.tile([P, P], U32, name="agg_codes", align_bytes=64)
            agg_plane = late_work.tile([P, P], U8, name="agg_plane", align_bytes=64)
            nc.vector.quantize_mx(
                out=agg_codes[:].bitcast(FP8X4), scales=agg_plane[:],
                in_=agg_img[:, P * t : P * (t + 1), :].rearrange("q m j -> q (m j)"),
            )
            agg_mx[t] = (agg_codes, agg_plane)

        def fuse(t, m):
            agg_codes, agg_plane = agg_mx[t]
            if m == 0:
                refined[t] = psum_turns.tile([P, C // P, P], F32, name="refined", tag="bank")
            nc.tensor.matmul_mx(
                out=refined[t][:, m, :],
                lhsT=fuse_codes[:, P * m : P * (m + 1)].bitcast(FP8X4), lhsT_scale=fuse_plane[:, P * m : P * (m + 1)],
                rhs=agg_codes[:].bitcast(FP8X4), rhs_scale=agg_plane[:], start=True, stop=True,
            )

        def add_x_and_store(t):
            result = late_work.tile([P, C // P, P], F32, name="result")
            pixels = slice(P * t, P * (t + 1))
            nc.vector.tensor_tensor(out=result[:], in0=refined[t][:], in1=x_res[:, :, pixels], op=ALU.add)
            nc.sync.dma_start(out=out_by_tile[:, :, pixels], in_=result[:])

        stage_queue = {}

        def plan(step, stage, t):
            stage_queue.setdefault(step, []).append((stage, t))

        def plan_finish(step, tiles):
            for place, t in enumerate(tiles):
                plan(step + place, quantise_agg, t)
                plan(step + 1 + place, fuse, t)
                plan(step + 2 + place, add_x_and_store, t)

        for t in range(CORE_TILES):
            at = STEPS - CORE_TILES + 1 + t
            plan(at, normalise, t)
            plan(at, turn, t)
            plan(at + 1, place_core, t)
        for place, tile in enumerate(range(6, 12)):
            plan_finish(STEPS + 3 + place // 2, (tile,))

        n_block = 0
        n_gathered = 0
        n_aggregated = 0
        made = {}
        to_collect = []
        parts = []
        with tc.manual_schedule():
            for step in range(STEPS + 11):
                for kind in range(1, 9):
                    if step == 2 * kind:
                        mask_edge(kind)
                    if step == 2 * kind + 1:
                        spread_edge(kind)
                if step < STEPS:
                    next_codes(step)
                if step == 9:
                    nc.sync.dma_start(out=x_res[:], in_=x[0].rearrange("(m p) h w -> p m (h w)", p=P))
                while n_gathered < min(WINDOWS, n_block + CODES_AHEAD):
                    gather_codes(n_gathered)
                    n_gathered += 1

                for stage, t in stage_queue.get(step, []):
                    if stage in (add_x_and_store, quantise_agg, place_core, normalise):
                        stage(t)

                def collect_now(m):
                    collect_bank(m)
                    plan_finish(step + 1, after_bank.get(m, ()))

                for m in to_collect:
                    collect_now(m)
                to_collect = []

                if step >= FIRST_SUM_STEP:
                    while n_aggregated < made[step - 2]:
                        for j in range(PACK):
                            parts.append((n_aggregated, j))
                        n_aggregated += 1
                first_new = n_block
                n_block = min(len(blocks), -(-len(blocks) * (step + 1) // LAST_BLOCK_STEP))
                made[step] = n_block
                for n in range(first_new, min(n_block + GATHER_AHEAD, len(blocks))):
                    gather_for(n)
                mx_calls = [lambda: core_messages(step)] if step < STEPS else []
                for n in range(first_new, n_block):
                    mx_calls.append(lambda n=n: make_messages(n))
                for stage, t in stage_queue.get(step, []):
                    if stage == fuse:
                        mx_calls += [lambda t=t, m=m: fuse(t, m) for m in range(C // P)]
                n_mx = len(mx_calls)
                quota = min(len(parts), PARTS_PER_STEP) if step < STEPS else len(parts)
                shares = [quota * (m + 1) // n_mx - quota * m // n_mx for m in range(n_mx)]

                def emit_parts(count):
                    for n, j in parts[0:count]:
                        m, place = blocks[n]
                        if place == 0 and j == 0 and len(to_collect) > 1:
                            collect_now(to_collect[0])
                            to_collect[0:1] = []
                        aggregate_part(n, j)
                        if place == len(bank_list[m][3]) - 1 and j == PACK - 1:
                            to_collect.append(m)
                    parts[0:count] = []

                on_vector, on_scalar = core_sums(step) if step < STEPS else ([], [])
                for m, (call, share) in enumerate(zip(mx_calls, shares)):
                    call()
                    if m == 0:
                        for scalar_call in on_scalar:
                            scalar_call()
                    emit_parts(share)
                for call in on_vector:
                    call()
                if step >= STEPS:
                    emit_parts(len(parts))

                if step == 0:
                    spread_inner()
                    turn_and_collect((inner_lanes,))
                if step == 1:
                    nc.vector.tensor_reduce(out=inv_sum[:], in_=e_core[:], axis=AXIS.X, op=ALU.add)
                    nc.vector.tensor_scalar_add(out=inv_sum[:], in0=inv_sum[:], scalar1=1.0)
                    nc.vector.reciprocal(out=inv_sum[:], in_=inv_sum[:])
                if step == 24:
                    turn_and_collect((row_lanes, col_lanes))
                for stage, t in stage_queue.get(step, []):
                    if stage == turn:
                        stage(t)
